import numpy as np
import ml_dtypes


def mxq(x, axis, fmt="e4m3"):
    dtype, down = {"e4m3": (ml_dtypes.float8_e4m3fn, 7), "e5m2": (ml_dtypes.float8_e5m2, 14)}[fmt]
    v = np.moveaxis(np.asarray(x, np.float32).astype(ml_dtypes.bfloat16).astype(np.float64), axis, -1)
    blocks = v.reshape(v.shape[:-1] + (-1, 32))
    amax = np.abs(blocks).max(-1, keepdims=True)
    byte = np.maximum(np.where(amax > 0, np.frexp(amax)[1] - 1 + 127, 0) - down, 1)
    scale = np.exp2(byte - 127.0)
    codes = (blocks / scale).astype(np.float32).astype(dtype).astype(np.float64)
    return np.moveaxis((codes * scale).reshape(v.shape), -1, axis)


WIDE = False


def mx_kscale(k):
    if not WIDE:
        return np.ones(k)
    levels = np.array([20, -20, 10, -10, 0])
    a = np.random.permutation(np.resize(levels, k // 512 * 4)).reshape(k // 512, 4)
    idx = np.arange(k)
    return np.exp2(a[idx // 512, idx % 128 // 32])


BF16 = ml_dtypes.bfloat16


def bf(x):
    return np.asarray(x, np.float32).astype(BF16)


def f64(x):
    return np.asarray(x).astype(np.float64)


B, IN, H = 512, 896, 1024
D = IN + H
LN_EPS = 1e-5
DIV_EPS = 1e-6


def sigmoid(v):
    return 1.0 / (1.0 + np.exp(-v))


def setup_inputs():
    s = mx_kscale(4 * H)[H:2 * H]
    x = bf(np.random.standard_normal((B, IN)))
    h_prev = bf(np.random.standard_normal((B, H)))
    c0 = bf(np.random.standard_normal((B, H)))
    n0 = bf(np.random.uniform(0.0, 1.0, (B, H)))
    m_prev = bf(np.random.uniform(0.0, 1.0, (B, H)))
    W = {}
    b = {}
    for g in "ifoz":
        W[g] = bf(np.random.standard_normal((H, D)) * 0.6 / np.sqrt(D))
        b[g] = bf(np.random.standard_normal(H) * 0.3)
    ln_gamma = bf(1.0 + 0.1 * np.random.standard_normal(H))
    ln_beta = bf(0.1 * np.random.standard_normal(H))
    grad_out = bf(np.random.standard_normal((B, H)) * np.exp2(np.random.randint(-12, 1, (B, 1))) * 16.0)
    combined = np.concatenate([f64(x), f64(h_prev)], axis=1)
    gates = np.stack([combined @ f64(W[g]).T + f64(b[g]) for g in "ifoz"], axis=0)
    i_t = np.exp(gates[0])
    f_t = sigmoid(gates[1])
    z_t = np.tanh(gates[3])
    c_t = f_t * f64(c0) + i_t * z_t
    n_t = f_t * f64(n0) + i_t
    return {"x": x, "h_prev": h_prev,
            "c_prev": bf(f64(c0) * s), "n_prev": bf(f64(n0) * s), "m_prev": m_prev,
            "Wi": W["i"], "bi": b["i"],
            "Wf": bf(f64(W["f"]) / s[:, None]), "bf": b["f"],
            "Wo": W["o"], "bo": b["o"],
            "Wz": W["z"], "bz": b["z"],
            "ln_gamma": ln_gamma, "ln_beta": ln_beta,
            "gates": np.asarray(gates, np.float32),
            "c_t": np.asarray(c_t, np.float32),
            "n_t": np.asarray(n_t, np.float32),
            "grad_out": grad_out}


def reference(x, h_prev, c_prev, n_prev, m_prev, Wi, bi, Wf, bf, Wo, bo, Wz, bz, ln_gamma, ln_beta,
              gates, c_t, n_t, grad_out):
    ga = f64(gates)
    i_t = np.exp(ga[0])
    f_t = sigmoid(ga[1])
    o_t = sigmoid(ga[2])
    z_t = np.tanh(ga[3])
    q = 1.0 / (f64(n_t) + DIV_EPS)
    r = f64(c_t) * q
    h = o_t * r
    mu = np.mean(h, axis=-1, keepdims=True)
    var = np.mean(np.square(h - mu), axis=-1, keepdims=True)
    rstd = 1.0 / np.sqrt(var + LN_EPS)
    xhat = (h - mu) * rstd
    dy = f64(grad_out) * f64(ln_gamma)
    dh = rstd * (dy - np.mean(dy, axis=-1, keepdims=True) - xhat * np.mean(dy * xhat, axis=-1, keepdims=True))
    dc = dh * o_t * q
    dgi = dc * (z_t - r) * i_t
    dgf = dc * (f64(c_prev) - r * f64(n_prev)) * f_t * (1.0 - f_t)
    dgo = dh * r * o_t * (1.0 - o_t)
    dgz = dc * i_t * (1.0 - z_t * z_t)
    dG = np.concatenate([dgi, dgf, dgo, dgz], axis=1)
    Wx = np.concatenate([f64(Wi)[:, :IN], f64(Wf)[:, :IN], f64(Wo)[:, :IN], f64(Wz)[:, :IN]], axis=0)
    return mxq(dG, 1, "e5m2") @ mxq(Wx, 0, "e4m3")

@@ -1,0 +1,283 @@
+from contextlib import ExitStack
+
+import concourse.mybir as mybir
+from concourse.masks import make_identity
+
+F32 = mybir.dt.float32
+BF16 = mybir.dt.bfloat16
+U32 = mybir.dt.uint32
+U8 = mybir.dt.uint8
+E4M3X4 = mybir.dt.float8_e4m3fn_x4
+E5M2X4 = mybir.dt.float8_e5m2_x4
+ACT = mybir.ActivationFunctionType
+ALU = mybir.AluOpType
+
+B, IN, H = 512, 896, 1024
+LN_EPS = 1e-5
+DIV_EPS = 1e-6
+
+P = 128
+PACK = 4
+K_PASS = P * PACK
+TOK_TILES = B // P
+GATES = 4
+PASSES_PER_GATE = H // K_PASS
+PASSES = GATES * PASSES_PER_GATE
+N_MX = 512
+N_STARTS = (0, IN - N_MX)
+W_PIECES = ((0, 512), (512, 256), (768, 128))
+W_PASSES_AT_START = 2
+W_PASSES_PER_TILE = 3
+
+FLOPS = 2 * B * GATES * H * IN
+BYTES = (GATES + 2) * B * H * 4 + 3 * B * H * 2 + GATES * H * IN * 2 + H * 2 + B * IN * 4
+
+
+def tile_slstmcell_t_v_kernel(
+    tc, x, h_prev, c_prev, n_prev, m_prev, Wi, bi, Wf, bf, Wo, bo, Wz, bz, ln_gamma, ln_beta,
+    gates, c_t, n_t, grad_out, out,
+):
+    nc = tc.nc
+    gate_row = {"o": 2, "f": 1, "i": 0, "z": 3}
+    place = {"o": 0, "f": 1, "i": 2, "z": 3}
+    weight_at = (Wo, Wf, Wi, Wz)
+
+    with ExitStack() as ctx:
+        const = ctx.enter_context(tc.tile_pool(name="const", bufs=1))
+        w_stage = ctx.enter_context(tc.tile_pool(name="w_stage", bufs=2))
+        w_keep = ctx.enter_context(tc.tile_pool(name="w_keep", bufs=1))
+        norm_in = ctx.enter_context(tc.tile_pool(name="norm_in", bufs=TOK_TILES))
+        tok_in = ctx.enter_context(tc.tile_pool(name="tok_in", bufs=2))
+        work = ctx.enter_context(tc.tile_pool(name="work", bufs=1))
+        stats = ctx.enter_context(tc.tile_pool(name="stats", bufs=2))
+        dg_stage = ctx.enter_context(tc.tile_pool(name="dg_stage", bufs=2))
+        dg_keep = ctx.enter_context(tc.tile_pool(name="dg_keep", bufs=3))
+        out_stage = ctx.enter_context(tc.tile_pool(name="out_stage", bufs=2))
+        psum_t = ctx.enter_context(tc.psum_pool(name="psum_t", bufs=2))
+        psum_acc = ctx.enter_context(tc.psum_pool(name="psum_acc", bufs=2))
+
+        identity = const.tile([P, P], F32, name="identity")
+        make_identity(nc, identity[:])
+        minus_half = const.tile([P, 1], F32, name="minus_half")
+        nc.vector.memset(minus_half[:], -0.5)
+
+        w_codes = w_keep.tile([P, PASSES, IN], U32, name="w_codes", align_bytes=64)
+        w_scales = w_keep.tile([P, PASSES, IN], U8, name="w_scales", align_bytes=64)
+
+        def load_weight_pass(c):
+            weight = weight_at[c // PASSES_PER_GATE]
+            first_row = K_PASS * (c % PASSES_PER_GATE)
+            raw = w_stage.tile([P, PACK, IN], BF16, name="w_raw")
+            for u in range(2):
+                rows = weight[first_row + 2 * P * u : first_row + 2 * P * (u + 1), 0:IN]
+                nc.sync.dma_start(out=raw[:, 2 * u : 2 * u + 2, :], in_=rows.rearrange("(p e) n -> p e n", e=2))
+            return raw
+
+        def quantise_weight_pass(c, raw):
+            grouped = w_stage.tile([P, IN, PACK], BF16, name="w_grouped", align_bytes=64)
+            copy = nc.vector.tensor_copy if c < W_PASSES_AT_START else nc.scalar.copy
+            for n0, width in W_PIECES:
+                copy(
+                    out=grouped[:, n0 : n0 + width, :].rearrange("p (c i) v -> p c v i", i=4),
+                    in_=raw[:, :, n0 : n0 + width].rearrange("p v (c i) -> p c v i", i=4),
+                )
+            for n0, width in W_PIECES:
+                nc.vector.quantize_mx(
+                    out=w_codes[:, c, n0 : n0 + width].bitcast(E4M3X4),
+                    scales=w_scales[:, c, n0 : n0 + width],
+                    in_=grouped[:, n0 : n0 + width, :].rearrange("p n v -> p (n v)"),
+                )
+
+        def load(pool, source, dtype, name):
+            loaded = pool.tile([P, H], dtype, name=name)
+            nc.sync.dma_start(out=loaded[:], in_=source)
+            return loaded
+
+        def load_token_tile(t):
+            rows = slice(P * t, P * (t + 1))
+            return {
+                "o": load(tok_in, gates[gate_row["o"], rows, :], F32, "gate_o"),
+                "c_t": load(tok_in, c_t[rows, :], F32, "cell"),
+                "grad": load(tok_in, grad_out[rows, :], BF16, "grad"),
+                "z": load(tok_in, gates[gate_row["z"], rows, :], F32, "gate_z"),
+                "n_prev": load(tok_in, n_prev[rows, :], BF16, "n_before"),
+                "c_prev": load(tok_in, c_prev[rows, :], BF16, "c_before"),
+                "f": load(tok_in, gates[gate_row["f"], rows, :], F32, "gate_f"),
+                "i": load(tok_in, gates[gate_row["i"], rows, :], F32, "gate_i"),
+            }
+
+        def activations(tok):
+            nc.scalar.activation(out=tok["q"][:], in_=tok["q"][:], func=ACT.Exp, scale=-1.0)
+            nc.scalar.activation(out=tok["o"][:], in_=tok["o"][:], func=ACT.Tanh, scale=0.5)
+            nc.scalar.activation(out=tok["z"][:], in_=tok["z"][:], func=ACT.Tanh)
+            nc.scalar.activation(out=tok["f"][:], in_=tok["f"][:], func=ACT.Tanh, scale=0.5)
+            nc.scalar.activation(out=tok["f"][:], in_=tok["f"][:], func=ACT.Square)
+            nc.scalar.activation(out=tok["i"][:], in_=tok["i"][:], func=ACT.Exp)
+            tok["zz"] = tok_in.tile([P, H], F32, name="z_squared")
+            nc.scalar.activation(out=tok["zz"][:], in_=tok["z"][:], func=ACT.Square)
+
+        def full(name):
+            return work.tile([P, H], F32, name=name)
+
+        def column(name):
+            return stats.tile([P, 1], F32, name=name)
+
+        def layer_norm_backward(tok):
+            r, h2, dy, line, dhn = full("r"), full("h2"), full("dy"), full("line"), full("dhn")
+            sum_h2, sum_dy, sum_dyh, sum_sq = column("sum_h2"), column("sum_dy"), column("sum_dyh"), column("sum_sq")
+            nc.vector.tensor_mul(out=r[:], in0=tok["c_t"][:], in1=tok["q"][:])
+            nc.vector.scalar_tensor_tensor(
+                out=h2[:], in0=tok["o"][:], scalar=1.0, in1=r[:], op0=ALU.add, op1=ALU.mult, accum_out=sum_h2[:]
+            )
+            nc.vector.scalar_tensor_tensor(
+                out=dy[:], in0=tok["grad"][:], scalar=1.0, in1=gamma[:], op0=ALU.mult, op1=ALU.mult,
+                accum_out=sum_dy[:],
+            )
+            nc.vector.scalar_tensor_tensor(
+                out=dhn[:], in0=dy[:], scalar=1.0, in1=h2[:], op0=ALU.mult, op1=ALU.mult, accum_out=sum_dyh[:]
+            )
+            minus_mean_h2 = column("minus_mean_h2")
+            nc.vector.tensor_scalar_mul(out=minus_mean_h2[:], in0=sum_h2[:], scalar1=-1.0 / H)
+            nc.scalar.activation(
+                out=line[:], in_=h2[:], func=ACT.Square, bias=minus_mean_h2[:], accum_out=sum_sq[:]
+            )
+            minus_mean_dy = column("minus_mean_dy")
+            nc.vector.tensor_scalar_mul(out=minus_mean_dy[:], in0=sum_dy[:], scalar1=-1.0 / H)
+            cov, var_eps, inv_var = column("cov"), column("var_eps"), column("inv_var")
+            nc.vector.scalar_tensor_tensor(
+                out=cov[:], in0=sum_dy[:], scalar=minus_mean_h2[:], in1=sum_dyh[:], op0=ALU.mult, op1=ALU.add
+            )
+            nc.vector.tensor_scalar(
+                out=var_eps[:], in0=sum_sq[:], scalar1=0.25 / H, scalar2=LN_EPS, op0=ALU.mult, op1=ALU.add
+            )
+            nc.vector.reciprocal(out=inv_var[:], in_=var_eps[:])
+            slope, offset = column("slope"), column("offset")
+            nc.vector.scalar_tensor_tensor(
+                out=slope[:], in0=cov[:], scalar=-0.25 / H, in1=inv_var[:], op0=ALU.mult, op1=ALU.mult
+            )
+            nc.vector.scalar_tensor_tensor(
+                out=offset[:], in0=slope[:], scalar=minus_mean_h2[:], in1=minus_mean_dy[:], op0=ALU.mult, op1=ALU.add
+            )
+            nc.scalar.activation(out=line[:], in_=h2[:], func=ACT.Identity, scale=slope[:], bias=offset[:])
+            nc.vector.tensor_add(out=dhn[:], in0=dy[:], in1=line[:])
+            rstd, minus_quarter_rstd = column("rstd"), column("minus_quarter_rstd")
+            nc.gpsimd.tensor_tensor(out=rstd[:], in0=var_eps[:], in1=minus_half[:], op=ALU.pow)
+            nc.gpsimd.tensor_scalar(
+                out=minus_quarter_rstd[:], in0=rstd[:], scalar1=-0.25, scalar2=0.0, op0=ALU.mult, op1=ALU.add
+            )
+            return {"r": r, "h2": h2, "dhn": dhn, "rstd": rstd, "minus_quarter_rstd": minus_quarter_rstd}
+
+        def quantise_gradient(s, dg, dg_codes, dg_scales):
+            words = dg[:].bitcast(F32)
+            flipped = psum_t.tile([P, PASSES_PER_GATE, 2, P], F32, name="flipped")
+            for half in range(PASSES_PER_GATE):
+                for u in range(2):
+                    first = (2 * half + u) * P
+                    nc.tensor.transpose(flipped[:, half, u, :], words[:, first : first + P], identity[:])
+            grouped = dg_stage.tile([P, PASSES_PER_GATE, P, PACK], BF16, name="dg_grouped", align_bytes=64)
+            nc.scalar.copy(out=grouped[:].bitcast(F32), in_=flipped[:].rearrange("p c u t -> p c t u"))
+            passes = slice(PASSES_PER_GATE * s, PASSES_PER_GATE * (s + 1))
+            nc.vector.quantize_mx(
+                out=dg_codes[:, passes, :].rearrange("p c t -> p (c t)").bitcast(E5M2X4),
+                scales=dg_scales[:, passes, :].rearrange("p c t -> p (c t)"),
+                in_=grouped[:].rearrange("p c t v -> p (c t v)"),
+            )
+
+        def multiply_and_store(t, dg_codes, dg_scales):
+            acc = [psum_acc.tile([P, N_MX], F32, name="acc_low"), psum_acc.tile([P, N_MX], F32, name="acc_high")]
+            for c in range(PASSES):
+                for window, n0 in enumerate(N_STARTS):
+                    nc.tensor.matmul_mx(
+                        out=acc[window][:],
+                        lhsT=dg_codes[:, c, :].bitcast(E5M2X4),
+                        lhsT_scale=dg_scales[:, c, :],
+                        rhs=w_codes[:, c, n0 : n0 + N_MX].bitcast(E4M3X4),
+                        rhs_scale=w_scales[:, c, n0 : n0 + N_MX],
+                        start=(c == 0),
+                        stop=(c == PASSES - 1),
+                    )
+            result = out_stage.tile([P, IN], F32, name="result")
+            nc.scalar.copy(out=result[:, 0:N_MX], in_=acc[0][:])
+            nc.scalar.copy(out=result[:, N_MX:IN], in_=acc[1][:, 2 * N_MX - IN : N_MX])
+            nc.sync.dma_start(out=out[P * t : P * (t + 1), :], in_=result[:])
+
+        def gate_factors(tok, norm):
+            a2, r_minus_z, rn, minus_cn, u, w = (
+                full("a2"), full("r_minus_z"), full("rn"), full("minus_cn"), full("u"), full("w"),
+            )
+            r, h2 = norm["r"], norm["h2"]
+            nc.vector.scalar_tensor_tensor(
+                out=a2[:], in0=tok["o"][:], scalar=1.0, in1=tok["q"][:], op0=ALU.add, op1=ALU.mult
+            )
+            nc.vector.tensor_sub(out=r_minus_z[:], in0=r[:], in1=tok["z"][:])
+            nc.vector.tensor_mul(out=rn[:], in0=r[:], in1=tok["n_prev"][:])
+            nc.vector.tensor_sub(out=minus_cn[:], in0=rn[:], in1=tok["c_prev"][:])
+            nc.vector.scalar_tensor_tensor(
+                out=u[:], in0=tok["f"][:], scalar=1.0, in1=minus_cn[:], op0=ALU.subtract, op1=ALU.mult
+            )
+            nc.vector.scalar_tensor_tensor(
+                out=w[:], in0=tok["o"][:], scalar=1.0, in1=h2[:], op0=ALU.subtract, op1=ALU.mult
+            )
+            return {"a2": a2, "r_minus_z": r_minus_z, "u": u, "w": w}
+
+        def gate_gradients(tok, norm, fac):
+            dhn = norm["dhn"]
+            dg_codes = dg_keep.tile([P, PASSES, P], U32, name="dg_codes", align_bytes=64)
+            dg_scales = dg_keep.tile([P, PASSES, P], U8, name="dg_scales", align_bytes=64)
+            dgo, dgf, dgi, dgz = (
+                work.tile([P, H], BF16, name="dgo"), work.tile([P, H], BF16, name="dgf"),
+                work.tile([P, H], BF16, name="dgi"), work.tile([P, H], BF16, name="dgz"),
+            )
+            dc2, minus_dci = full("dc2"), full("minus_dci")
+            nc.vector.scalar_tensor_tensor(
+                out=dgo[:], in0=fac["w"][:], scalar=norm["minus_quarter_rstd"][:], in1=dhn[:],
+                op0=ALU.mult, op1=ALU.mult,
+            )
+            quantise_gradient(place["o"], dgo, dg_codes, dg_scales)
+            nc.vector.scalar_tensor_tensor(
+                out=dc2[:], in0=dhn[:], scalar=norm["rstd"][:], in1=fac["a2"][:], op0=ALU.mult, op1=ALU.mult
+            )
+            nc.vector.scalar_tensor_tensor(
+                out=dgf[:], in0=fac["u"][:], scalar=0.125, in1=dc2[:], op0=ALU.mult, op1=ALU.mult
+            )
+            quantise_gradient(place["f"], dgf, dg_codes, dg_scales)
+            nc.vector.scalar_tensor_tensor(
+                out=minus_dci[:], in0=dc2[:], scalar=-0.5, in1=tok["i"][:], op0=ALU.mult, op1=ALU.mult
+            )
+            nc.vector.tensor_mul(out=dgi[:], in0=minus_dci[:], in1=fac["r_minus_z"][:])
+            quantise_gradient(place["i"], dgi, dg_codes, dg_scales)
+            nc.vector.scalar_tensor_tensor(
+                out=dgz[:], in0=tok["zz"][:], scalar=1.0, in1=minus_dci[:], op0=ALU.subtract, op1=ALU.mult
+            )
+            quantise_gradient(place["z"], dgz, dg_codes, dg_scales)
+            return dg_codes, dg_scales
+
+        w_raw = {0: load_weight_pass(0)}
+        q_of = [load(norm_in, n_t[P * t : P * (t + 1), :], F32, "q") for t in range(TOK_TILES)]
+        w_raw[1] = load_weight_pass(1)
+        tok_of = {0: load_token_tile(0)}
+        gamma = const.tile([P, H], BF16, name="gamma")
+        nc.sync.dma_start(out=gamma[:], in_=ln_gamma.partition_broadcast(P))
+        for t in range(TOK_TILES):
+            nc.scalar.activation(out=q_of[t][:], in_=q_of[t][:], func=ACT.Ln, bias=DIV_EPS)
+        for c in range(W_PASSES_AT_START):
+            quantise_weight_pass(c, w_raw[c])
+        tok_of[0]["q"] = q_of[0]
+        activations(tok_of[0])
+        next_pass = W_PASSES_AT_START
+        quantised = {}
+        for t in range(TOK_TILES):
+            tok = tok_of[t]
+            norm = layer_norm_backward(tok)
+            fac = gate_factors(tok, norm)
+            if t + 1 < TOK_TILES:
+                tok_of[t + 1] = load_token_tile(t + 1)
+                tok_of[t + 1]["q"] = q_of[t + 1]
+                activations(tok_of[t + 1])
+            for c in range(next_pass, min(PASSES, next_pass + W_PASSES_PER_TILE)):
+                quantise_weight_pass(c, load_weight_pass(c))
+            next_pass = min(PASSES, next_pass + W_PASSES_PER_TILE)
+            quantised[t] = gate_gradients(tok, norm, fac)
+            if t >= 1:
+                multiply_and_store(t - 1, quantised[t - 1][0], quantised[t - 1][1])
+        multiply_and_store(TOK_TILES - 1, quantised[TOK_TILES - 1][0], quantised[TOK_TILES - 1][1])

@@ -26,8 +26,6 @@ PASSES = GATES * PASSES_PER_GATE
 N_MX = 512
 N_STARTS = (0, IN - N_MX)
 W_PIECES = ((0, 512), (512, 256), (768, 128))
-W_PASSES_AT_START = 2
-W_PASSES_PER_TILE = 3
 
 FLOPS = 2 * B * GATES * H * IN
 BYTES = (GATES + 2) * B * H * 4 + 3 * B * H * 2 + GATES * H * IN * 2 + H * 2 + B * IN * 4
@@ -38,13 +36,13 @@ def tile_slstmcell_t_v_kernel(
     gates, c_t, n_t, grad_out, out,
 ):
     nc = tc.nc
-    gate_row = {"o": 2, "f": 1, "i": 0, "z": 3}
-    place = {"o": 0, "f": 1, "i": 2, "z": 3}
     weight_at = (Wo, Wf, Wi, Wz)
+    gate_row = {"o": 2, "f": 1, "i": 0, "z": 3}
 
     with ExitStack() as ctx:
+        ctx.enter_context(tc.manual_schedule())
         const = ctx.enter_context(tc.tile_pool(name="const", bufs=1))
-        w_stage = ctx.enter_context(tc.tile_pool(name="w_stage", bufs=2))
+        w_stage = ctx.enter_context(tc.tile_pool(name="w_stage", bufs=PASSES_PER_GATE))
         w_keep = ctx.enter_context(tc.tile_pool(name="w_keep", bufs=1))
         norm_in = ctx.enter_context(tc.tile_pool(name="norm_in", bufs=TOK_TILES))
         tok_in = ctx.enter_context(tc.tile_pool(name="tok_in", bufs=2))
@@ -54,38 +52,52 @@ def tile_slstmcell_t_v_kernel(
         dg_keep = ctx.enter_context(tc.tile_pool(name="dg_keep", bufs=3))
         out_stage = ctx.enter_context(tc.tile_pool(name="out_stage", bufs=2))
         psum_t = ctx.enter_context(tc.psum_pool(name="psum_t", bufs=2))
-        psum_acc = ctx.enter_context(tc.psum_pool(name="psum_acc", bufs=2))
+        psum_acc = ctx.enter_context(tc.psum_pool(name="psum_acc", bufs=3))
 
         identity = const.tile([P, P], F32, name="identity")
         make_identity(nc, identity[:])
         minus_half = const.tile([P, 1], F32, name="minus_half")
         nc.vector.memset(minus_half[:], -0.5)
+        gamma_rows = const.tile([P, H], BF16, name="gamma_rows")
+        ones = const.tile([P, P], BF16, name="ones")
+        gamma = const.tile([P, H], BF16, name="gamma")
+        nc.vector.memset(gamma_rows[:], 0.0)
+        nc.vector.memset(ones[:], 1.0)
+        nc.sync.dma_start(out=gamma_rows[0:1, :], in_=ln_gamma.unsqueeze(0))
 
         w_codes = w_keep.tile([P, PASSES, IN], U32, name="w_codes", align_bytes=64)
         w_scales = w_keep.tile([P, PASSES, IN], U8, name="w_scales", align_bytes=64)
+        w_raw = {}
+        w_grouped = {}
 
         def load_weight_pass(c):
             weight = weight_at[c // PASSES_PER_GATE]
             first_row = K_PASS * (c % PASSES_PER_GATE)
-            raw = w_stage.tile([P, PACK, IN], BF16, name="w_raw")
+            w_raw[c] = w_stage.tile([P, PACK, IN], BF16, name="w_raw")
+            w_grouped[c] = w_stage.tile([P, IN, PACK], BF16, name="w_grouped", align_bytes=64)
             for u in range(2):
                 rows = weight[first_row + 2 * P * u : first_row + 2 * P * (u + 1), 0:IN]
-                nc.sync.dma_start(out=raw[:, 2 * u : 2 * u + 2, :], in_=rows.rearrange("(p e) n -> p e n", e=2))
-            return raw
+                nc.sync.dma_start(out=w_raw[c][:, 2 * u : 2 * u + 2, :], in_=rows.rearrange("(p e) n -> p e n", e=2))
 
-        def quantise_weight_pass(c, raw):
-            grouped = w_stage.tile([P, IN, PACK], BF16, name="w_grouped", align_bytes=64)
-            copy = nc.vector.tensor_copy if c < W_PASSES_AT_START else nc.scalar.copy
-            for n0, width in W_PIECES:
+        def weight_share(s, quarter):
+            c = PASSES_PER_GATE * s + quarter // 2
+            return c, (W_PIECES[:1] if quarter % 2 == 0 else W_PIECES[1:])
+
+        def regroup_weights(copy, s, quarter):
+            c, pieces = weight_share(s, quarter)
+            for n0, width in pieces:
                 copy(
-                    out=grouped[:, n0 : n0 + width, :].rearrange("p (c i) v -> p c v i", i=4),
-                    in_=raw[:, :, n0 : n0 + width].rearrange("p v (c i) -> p c v i", i=4),
+                    out=w_grouped[c][:, n0 : n0 + width, :].rearrange("p (c i) v -> p c v i", i=4),
+                    in_=w_raw[c][:, :, n0 : n0 + width].rearrange("p v (c i) -> p c v i", i=4),
                 )
-            for n0, width in W_PIECES:
+
+        def quantise_weights(s, quarter):
+            c, pieces = weight_share(s, quarter)
+            for n0, width in pieces:
                 nc.vector.quantize_mx(
                     out=w_codes[:, c, n0 : n0 + width].bitcast(E4M3X4),
                     scales=w_scales[:, c, n0 : n0 + width],
-                    in_=grouped[:, n0 : n0 + width, :].rearrange("p n v -> p (n v)"),
+                    in_=w_grouped[c][:, n0 : n0 + width, :].rearrange("p n v -> p (n v)"),
                 )
 
         def load(pool, source, dtype, name):
@@ -96,6 +108,7 @@ def tile_slstmcell_t_v_kernel(
         def load_token_tile(t):
             rows = slice(P * t, P * (t + 1))
             return {
+                "q": log_n[t],
                 "o": load(tok_in, gates[gate_row["o"], rows, :], F32, "gate_o"),
                 "c_t": load(tok_in, c_t[rows, :], F32, "cell"),
                 "grad": load(tok_in, grad_out[rows, :], BF16, "grad"),
@@ -106,15 +119,8 @@ def tile_slstmcell_t_v_kernel(
                 "i": load(tok_in, gates[gate_row["i"], rows, :], F32, "gate_i"),
             }
 
-        def activations(tok):
-            nc.scalar.activation(out=tok["q"][:], in_=tok["q"][:], func=ACT.Exp, scale=-1.0)
-            nc.scalar.activation(out=tok["o"][:], in_=tok["o"][:], func=ACT.Tanh, scale=0.5)
-            nc.scalar.activation(out=tok["z"][:], in_=tok["z"][:], func=ACT.Tanh)
-            nc.scalar.activation(out=tok["f"][:], in_=tok["f"][:], func=ACT.Tanh, scale=0.5)
-            nc.scalar.activation(out=tok["f"][:], in_=tok["f"][:], func=ACT.Square)
-            nc.scalar.activation(out=tok["i"][:], in_=tok["i"][:], func=ACT.Exp)
-            tok["zz"] = tok_in.tile([P, H], F32, name="z_squared")
-            nc.scalar.activation(out=tok["zz"][:], in_=tok["z"][:], func=ACT.Square)
+        def in_place(tile_, func, scale=1.0):
+            nc.scalar.activation(out=tile_[:], in_=tile_[:], func=func, scale=scale)
 
         def full(name):
             return work.tile([P, H], F32, name=name)
@@ -122,162 +128,200 @@ def tile_slstmcell_t_v_kernel(
         def column(name):
             return stats.tile([P, 1], F32, name=name)
 
-        def layer_norm_backward(tok):
-            r, h2, dy, line, dhn = full("r"), full("h2"), full("dy"), full("line"), full("dhn")
-            sum_h2, sum_dy, sum_dyh, sum_sq = column("sum_h2"), column("sum_dy"), column("sum_dyh"), column("sum_sq")
-            nc.vector.tensor_mul(out=r[:], in0=tok["c_t"][:], in1=tok["q"][:])
+        def fused(out_, in0, op0, scalar, op1, in1, accum_out=None):
             nc.vector.scalar_tensor_tensor(
-                out=h2[:], in0=tok["o"][:], scalar=1.0, in1=r[:], op0=ALU.add, op1=ALU.mult, accum_out=sum_h2[:]
+                out=out_[:], in0=in0[:], scalar=scalar, in1=in1[:], op0=op0, op1=op1, accum_out=accum_out
             )
-            nc.vector.scalar_tensor_tensor(
-                out=dy[:], in0=tok["grad"][:], scalar=1.0, in1=gamma[:], op0=ALU.mult, op1=ALU.mult,
-                accum_out=sum_dy[:],
-            )
-            nc.vector.scalar_tensor_tensor(
-                out=dhn[:], in0=dy[:], scalar=1.0, in1=h2[:], op0=ALU.mult, op1=ALU.mult, accum_out=sum_dyh[:]
-            )
-            minus_mean_h2 = column("minus_mean_h2")
-            nc.vector.tensor_scalar_mul(out=minus_mean_h2[:], in0=sum_h2[:], scalar1=-1.0 / H)
-            nc.scalar.activation(
-                out=line[:], in_=h2[:], func=ACT.Square, bias=minus_mean_h2[:], accum_out=sum_sq[:]
-            )
-            minus_mean_dy = column("minus_mean_dy")
-            nc.vector.tensor_scalar_mul(out=minus_mean_dy[:], in0=sum_dy[:], scalar1=-1.0 / H)
-            cov, var_eps, inv_var = column("cov"), column("var_eps"), column("inv_var")
-            nc.vector.scalar_tensor_tensor(
-                out=cov[:], in0=sum_dy[:], scalar=minus_mean_h2[:], in1=sum_dyh[:], op0=ALU.mult, op1=ALU.add
-            )
-            nc.vector.tensor_scalar(
-                out=var_eps[:], in0=sum_sq[:], scalar1=0.25 / H, scalar2=LN_EPS, op0=ALU.mult, op1=ALU.add
-            )
-            nc.vector.reciprocal(out=inv_var[:], in_=var_eps[:])
-            slope, offset = column("slope"), column("offset")
-            nc.vector.scalar_tensor_tensor(
-                out=slope[:], in0=cov[:], scalar=-0.25 / H, in1=inv_var[:], op0=ALU.mult, op1=ALU.mult
-            )
-            nc.vector.scalar_tensor_tensor(
-                out=offset[:], in0=slope[:], scalar=minus_mean_h2[:], in1=minus_mean_dy[:], op0=ALU.mult, op1=ALU.add
-            )
-            nc.scalar.activation(out=line[:], in_=h2[:], func=ACT.Identity, scale=slope[:], bias=offset[:])
-            nc.vector.tensor_add(out=dhn[:], in0=dy[:], in1=line[:])
-            rstd, minus_quarter_rstd = column("rstd"), column("minus_quarter_rstd")
-            nc.gpsimd.tensor_tensor(out=rstd[:], in0=var_eps[:], in1=minus_half[:], op=ALU.pow)
-            nc.gpsimd.tensor_scalar(
-                out=minus_quarter_rstd[:], in0=rstd[:], scalar1=-0.25, scalar2=0.0, op0=ALU.mult, op1=ALU.add
-            )
-            return {"r": r, "h2": h2, "dhn": dhn, "rstd": rstd, "minus_quarter_rstd": minus_quarter_rstd}
 
-        def quantise_gradient(s, dg, dg_codes, dg_scales):
+        dg_codes, dg_scales = {}, {}
+        dg_flipped = {}
+        dg_grouped = {}
+        acc = {}
+
+        def transpose_gradient(t, s, dg):
             words = dg[:].bitcast(F32)
-            flipped = psum_t.tile([P, PASSES_PER_GATE, 2, P], F32, name="flipped")
+            dg_flipped[t, s] = psum_t.tile([P, PASSES_PER_GATE, 2, P], F32, name="dg_flipped")
             for half in range(PASSES_PER_GATE):
                 for u in range(2):
                     first = (2 * half + u) * P
-                    nc.tensor.transpose(flipped[:, half, u, :], words[:, first : first + P], identity[:])
-            grouped = dg_stage.tile([P, PASSES_PER_GATE, P, PACK], BF16, name="dg_grouped", align_bytes=64)
-            nc.scalar.copy(out=grouped[:].bitcast(F32), in_=flipped[:].rearrange("p c u t -> p c t u"))
-            passes = slice(PASSES_PER_GATE * s, PASSES_PER_GATE * (s + 1))
-            nc.vector.quantize_mx(
-                out=dg_codes[:, passes, :].rearrange("p c t -> p (c t)").bitcast(E5M2X4),
-                scales=dg_scales[:, passes, :].rearrange("p c t -> p (c t)"),
-                in_=grouped[:].rearrange("p c t v -> p (c t v)"),
+                    nc.tensor.transpose(dg_flipped[t, s][:, half, u, :], words[:, first : first + P], identity[:])
+
+        def regroup_gradient(t, s):
+            dg_grouped[t, s] = dg_stage.tile([P, PASSES_PER_GATE, P, PACK], BF16, name="dg_grouped", align_bytes=64)
+            nc.scalar.copy(
+                out=dg_grouped[t, s][:].bitcast(F32), in_=dg_flipped[t, s][:].rearrange("p c u t -> p c t u")
             )
 
-        def multiply_and_store(t, dg_codes, dg_scales):
-            acc = [psum_acc.tile([P, N_MX], F32, name="acc_low"), psum_acc.tile([P, N_MX], F32, name="acc_high")]
-            for c in range(PASSES):
+        def quantise_gradient(t, s):
+            passes = slice(PASSES_PER_GATE * s, PASSES_PER_GATE * (s + 1))
+            nc.vector.quantize_mx(
+                out=dg_codes[t][:, passes, :].rearrange("p c t -> p (c t)").bitcast(E5M2X4),
+                scales=dg_scales[t][:, passes, :].rearrange("p c t -> p (c t)"),
+                in_=dg_grouped[t, s][:].rearrange("p c t v -> p (c t v)"),
+            )
+
+        def multiply(t, s):
+            if s == 0:
+                acc[t] = [psum_acc.tile([P, N_MX], F32, name="acc_low"), psum_acc.tile([P, N_MX], F32, name="acc_high")]
+            for c in range(PASSES_PER_GATE * s, PASSES_PER_GATE * (s + 1)):
                 for window, n0 in enumerate(N_STARTS):
                     nc.tensor.matmul_mx(
-                        out=acc[window][:],
-                        lhsT=dg_codes[:, c, :].bitcast(E5M2X4),
-                        lhsT_scale=dg_scales[:, c, :],
+                        out=acc[t][window][:],
+                        lhsT=dg_codes[t][:, c, :].bitcast(E5M2X4),
+                        lhsT_scale=dg_scales[t][:, c, :],
                         rhs=w_codes[:, c, n0 : n0 + N_MX].bitcast(E4M3X4),
                         rhs_scale=w_scales[:, c, n0 : n0 + N_MX],
                         start=(c == 0),
                         stop=(c == PASSES - 1),
                     )
+
+        def store(t):
             result = out_stage.tile([P, IN], F32, name="result")
-            nc.scalar.copy(out=result[:, 0:N_MX], in_=acc[0][:])
-            nc.scalar.copy(out=result[:, N_MX:IN], in_=acc[1][:, 2 * N_MX - IN : N_MX])
+            nc.scalar.copy(out=result[:, 0:N_MX], in_=acc[t][0][:])
+            nc.scalar.copy(out=result[:, N_MX:IN], in_=acc[t][1][:, 2 * N_MX - IN : N_MX])
             nc.sync.dma_start(out=out[P * t : P * (t + 1), :], in_=result[:])
 
-        def gate_factors(tok, norm):
-            a2, r_minus_z, rn, minus_cn, u, w = (
-                full("a2"), full("r_minus_z"), full("rn"), full("minus_cn"), full("u"), full("w"),
-            )
-            r, h2 = norm["r"], norm["h2"]
-            nc.vector.scalar_tensor_tensor(
-                out=a2[:], in0=tok["o"][:], scalar=1.0, in1=tok["q"][:], op0=ALU.add, op1=ALU.mult
-            )
-            nc.vector.tensor_sub(out=r_minus_z[:], in0=r[:], in1=tok["z"][:])
-            nc.vector.tensor_mul(out=rn[:], in0=r[:], in1=tok["n_prev"][:])
-            nc.vector.tensor_sub(out=minus_cn[:], in0=rn[:], in1=tok["c_prev"][:])
-            nc.vector.scalar_tensor_tensor(
-                out=u[:], in0=tok["f"][:], scalar=1.0, in1=minus_cn[:], op0=ALU.subtract, op1=ALU.mult
-            )
-            nc.vector.scalar_tensor_tensor(
-                out=w[:], in0=tok["o"][:], scalar=1.0, in1=h2[:], op0=ALU.subtract, op1=ALU.mult
-            )
-            return {"a2": a2, "r_minus_z": r_minus_z, "u": u, "w": w}
+        def scalar_spare_work(t, k):
+            if t + 1 < GATES:
+                regroup_weights(nc.scalar.copy, t + 1, k)
+            elif k < t:
+                store(k)
 
-        def gate_gradients(tok, norm, fac):
-            dhn = norm["dhn"]
-            dg_codes = dg_keep.tile([P, PASSES, P], U32, name="dg_codes", align_bytes=64)
-            dg_scales = dg_keep.tile([P, PASSES, P], U8, name="dg_scales", align_bytes=64)
-            dgo, dgf, dgi, dgz = (
-                work.tile([P, H], BF16, name="dgo"), work.tile([P, H], BF16, name="dgf"),
-                work.tile([P, H], BF16, name="dgi"), work.tile([P, H], BF16, name="dgz"),
-            )
-            dc2, minus_dci = full("dc2"), full("minus_dci")
-            nc.vector.scalar_tensor_tensor(
-                out=dgo[:], in0=fac["w"][:], scalar=norm["minus_quarter_rstd"][:], in1=dhn[:],
-                op0=ALU.mult, op1=ALU.mult,
-            )
-            quantise_gradient(place["o"], dgo, dg_codes, dg_scales)
-            nc.vector.scalar_tensor_tensor(
-                out=dc2[:], in0=dhn[:], scalar=norm["rstd"][:], in1=fac["a2"][:], op0=ALU.mult, op1=ALU.mult
-            )
-            nc.vector.scalar_tensor_tensor(
-                out=dgf[:], in0=fac["u"][:], scalar=0.125, in1=dc2[:], op0=ALU.mult, op1=ALU.mult
-            )
-            quantise_gradient(place["f"], dgf, dg_codes, dg_scales)
-            nc.vector.scalar_tensor_tensor(
-                out=minus_dci[:], in0=dc2[:], scalar=-0.5, in1=tok["i"][:], op0=ALU.mult, op1=ALU.mult
-            )
-            nc.vector.tensor_mul(out=dgi[:], in0=minus_dci[:], in1=fac["r_minus_z"][:])
-            quantise_gradient(place["i"], dgi, dg_codes, dg_scales)
-            nc.vector.scalar_tensor_tensor(
-                out=dgz[:], in0=tok["zz"][:], scalar=1.0, in1=minus_dci[:], op0=ALU.subtract, op1=ALU.mult
-            )
-            quantise_gradient(place["z"], dgz, dg_codes, dg_scales)
-            return dg_codes, dg_scales
+        def finish_turn(t):
+            quantise_gradient(t, GATES - 1)
+            if t + 1 < GATES:
+                quantise_weights(t + 1, 3)
+                for earlier in range(t + 1):
+                    multiply(earlier, t + 1)
+            else:
+                multiply(t, GATES - 1)
 
-        w_raw = {0: load_weight_pass(0)}
-        q_of = [load(norm_in, n_t[P * t : P * (t + 1), :], F32, "q") for t in range(TOK_TILES)]
-        w_raw[1] = load_weight_pass(1)
-        tok_of = {0: load_token_tile(0)}
-        gamma = const.tile([P, H], BF16, name="gamma")
-        nc.sync.dma_start(out=gamma[:], in_=ln_gamma.partition_broadcast(P))
-        for t in range(TOK_TILES):
-            nc.scalar.activation(out=q_of[t][:], in_=q_of[t][:], func=ACT.Ln, bias=DIV_EPS)
-        for c in range(W_PASSES_AT_START):
-            quantise_weight_pass(c, w_raw[c])
-        tok_of[0]["q"] = q_of[0]
-        activations(tok_of[0])
-        next_pass = W_PASSES_AT_START
-        quantised = {}
-        for t in range(TOK_TILES):
+        def turn(t):
             tok = tok_of[t]
-            norm = layer_norm_backward(tok)
-            fac = gate_factors(tok, norm)
-            if t + 1 < TOK_TILES:
-                tok_of[t + 1] = load_token_tile(t + 1)
-                tok_of[t + 1]["q"] = q_of[t + 1]
-                activations(tok_of[t + 1])
-            for c in range(next_pass, min(PASSES, next_pass + W_PASSES_PER_TILE)):
-                quantise_weight_pass(c, load_weight_pass(c))
-            next_pass = min(PASSES, next_pass + W_PASSES_PER_TILE)
-            quantised[t] = gate_gradients(tok, norm, fac)
+            next_place = t + 1
+            more_weights = next_place < GATES
+
+            r, h2 = full("r"), full("h2")
+            sum_h2, minus_mean_h2, sum_sq = column("sum_h2"), column("minus_mean_h2"), column("sum_sq")
+            nc.vector.tensor_mul(out=r[:], in0=tok["c_t"][:], in1=tok["q"][:])
+            fused(h2, tok["o"], ALU.add, 1.0, ALU.mult, r, accum_out=sum_h2[:])
+            nc.vector.tensor_scalar_mul(out=minus_mean_h2[:], in0=sum_h2[:], scalar1=-1.0 / H)
+            line = full("line")
+            nc.scalar.activation(out=line[:], in_=h2[:], func=ACT.Square, bias=minus_mean_h2[:], accum_out=sum_sq[:])
+            if t > 0:
+                finish_turn(t - 1)
+
+            dy, dhn = full("dy"), full("dhn")
+            sum_dy, sum_dyh, minus_mean_dy, cov = column("sum_dy"), column("sum_dyh"), column("minus_mean_dy"), column("cov")
+            fused(dy, tok["grad"], ALU.mult, 1.0, ALU.mult, gamma, accum_out=sum_dy[:])
+            fused(dhn, dy, ALU.mult, 1.0, ALU.mult, h2, accum_out=sum_dyh[:])
+            nc.vector.tensor_scalar_mul(out=minus_mean_dy[:], in0=sum_dy[:], scalar1=-1.0 / H)
+            fused(cov, sum_dy, ALU.mult, minus_mean_h2[:], ALU.add, sum_dyh)
+
+            in_place(tok["z"], ACT.Tanh)
+            in_place(tok["f"], ACT.Tanh, scale=0.5)
+            in_place(tok["f"], ACT.Square)
+            in_place(tok["i"], ACT.Exp)
+
+            var_eps, inv_var, slope, offset = column("var_eps"), column("inv_var"), column("slope"), column("offset")
+            rstd, minus_quarter_rstd = column("rstd"), column("minus_quarter_rstd")
+            a2, rn, minus_cn = full("a2"), full("rn"), full("minus_cn")
+            nc.vector.tensor_scalar(
+                out=var_eps[:], in0=sum_sq[:], scalar1=0.25 / H, scalar2=LN_EPS, op0=ALU.mult, op1=ALU.add
+            )
+            nc.gpsimd.tensor_tensor(out=rstd[:], in0=var_eps[:], in1=minus_half[:], op=ALU.pow)
+            nc.gpsimd.tensor_scalar(
+                out=minus_quarter_rstd[:], in0=rstd[:], scalar1=-0.25, scalar2=0.0, op0=ALU.mult, op1=ALU.add
+            )
+            fused(a2, tok["o"], ALU.add, 1.0, ALU.mult, tok["q"])
+            nc.vector.reciprocal(out=inv_var[:], in_=var_eps[:])
+            nc.vector.tensor_mul(out=rn[:], in0=r[:], in1=tok["n_prev"][:])
+            fused(slope, cov, ALU.mult, -0.25 / H, ALU.mult, inv_var)
+            nc.vector.tensor_sub(out=minus_cn[:], in0=rn[:], in1=tok["c_prev"][:])
+            fused(offset, slope, ALU.mult, minus_mean_h2[:], ALU.add, minus_mean_dy)
+            nc.scalar.activation(out=line[:], in_=h2[:], func=ACT.Identity, scale=slope[:], bias=offset[:])
+            z_squared = tok_in.tile([P, H], F32, name="z_squared")
+            nc.scalar.activation(out=z_squared[:], in_=tok["z"][:], func=ACT.Square)
+            scalar_spare_work(t, 0)
+            r_minus_z, forget_term, output_term = full("r_minus_z"), full("forget_term"), full("output_term")
+            nc.vector.tensor_sub(out=r_minus_z[:], in0=r[:], in1=tok["z"][:])
+            fused(forget_term, tok["f"], ALU.subtract, 1.0, ALU.mult, minus_cn)
+            fused(output_term, tok["o"], ALU.subtract, 1.0, ALU.mult, h2)
+            nc.vector.tensor_add(out=dhn[:], in0=dy[:], in1=line[:])
+
+            dg_codes[t] = dg_keep.tile([P, PASSES, P], U32, name="dg_codes", align_bytes=64)
+            dg_scales[t] = dg_keep.tile([P, PASSES, P], U8, name="dg_scales", align_bytes=64)
+            dgo, dgf = work.tile([P, H], BF16, name="dgo"), work.tile([P, H], BF16, name="dgf")
+            dgi, dgz = work.tile([P, H], BF16, name="dgi"), work.tile([P, H], BF16, name="dgz")
+            dc2, minus_dci = full("dc2"), full("minus_dci")
+
+            fused(dgo, output_term, ALU.mult, minus_quarter_rstd[:], ALU.mult, dhn)
+            transpose_gradient(t, 0, dgo)
+            scalar_spare_work(t, 1)
+            regroup_gradient(t, 0)
+
+            fused(dc2, dhn, ALU.mult, rstd[:], ALU.mult, a2)
+            fused(dgf, forget_term, ALU.mult, 0.125, ALU.mult, dc2)
+            transpose_gradient(t, 1, dgf)
+            scalar_spare_work(t, 2)
+            regroup_gradient(t, 1)
+            quantise_gradient(t, 0)
+            multiply(t, 0)
+            if more_weights:
+                quantise_weights(next_place, 0)
+
+            fused(minus_dci, dc2, ALU.mult, -0.5, ALU.mult, tok["i"])
+            nc.vector.tensor_mul(out=dgi[:], in0=minus_dci[:], in1=r_minus_z[:])
+            transpose_gradient(t, 2, dgi)
+            scalar_spare_work(t, 3)
+            regroup_gradient(t, 2)
+            quantise_gradient(t, 1)
             if t >= 1:
-                multiply_and_store(t - 1, quantised[t - 1][0], quantised[t - 1][1])
-        multiply_and_store(TOK_TILES - 1, quantised[TOK_TILES - 1][0], quantised[TOK_TILES - 1][1])
+                multiply(t, 1)
+            if more_weights:
+                quantise_weights(next_place, 1)
+
+            fused(dgz, z_squared, ALU.subtract, 1.0, ALU.mult, minus_dci)
+            transpose_gradient(t, 3, dgz)
+            if t + 1 < TOK_TILES:
+                in_place(tok_of[t + 1]["q"], ACT.Exp, scale=-1.0)
+            regroup_gradient(t, 3)
+            quantise_gradient(t, 2)
+            if t >= 2:
+                multiply(t, 2)
+            if more_weights:
+                quantise_weights(next_place, 2)
+            if t + 1 < TOK_TILES:
+                in_place(tok_of[t + 1]["o"], ACT.Tanh, scale=0.5)
+
+            if t + 2 < GATES:
+                for c in range(PASSES_PER_GATE * (t + 2), PASSES_PER_GATE * (t + 3)):
+                    load_weight_pass(c)
+            if t + 2 < TOK_TILES:
+                tok_of[t + 2] = load_token_tile(t + 2)
+
+        load_weight_pass(0)
+        log_n = [load(norm_in, n_t[P * t : P * (t + 1), :], F32, "log_n") for t in range(TOK_TILES)]
+        load_weight_pass(1)
+        tok_of = {0: load_token_tile(0)}
+        for t in range(TOK_TILES):
+            nc.scalar.activation(out=log_n[t][:], in_=log_n[t][:], func=ACT.Ln, bias=DIV_EPS)
+        in_place(tok_of[0]["q"], ACT.Exp, scale=-1.0)
+        in_place(tok_of[0]["o"], ACT.Tanh, scale=0.5)
+        for first_quarter in (0, 2):
+            for quarter in (first_quarter, first_quarter + 1):
+                regroup_weights(nc.vector.tensor_copy, 0, quarter)
+            for quarter in (first_quarter, first_quarter + 1):
+                quantise_weights(0, quarter)
+            if first_quarter == 0:
+                for n0 in range(0, H, N_MX):
+                    spread = psum_t.tile([P, N_MX], F32, name="gamma_spread", tag="dg_flipped")
+                    nc.tensor.matmul(out=spread[:], lhsT=ones[:], rhs=gamma_rows[:, n0 : n0 + N_MX], start=True, stop=True)
+                    nc.vector.tensor_copy(out=gamma[:, n0 : n0 + N_MX], in_=spread[:])
+        load_weight_pass(2)
+        load_weight_pass(3)
+        tok_of[1] = load_token_tile(1)
+        for t in range(TOK_TILES):
+            turn(t)
+        finish_turn(TOK_TILES - 1)
+        store(TOK_TILES - 1)

@@ -63,7 +63,6 @@ def tile_slstmcell_t_v_kernel(
         gamma = const.tile([P, H], BF16, name="gamma")
         nc.vector.memset(gamma_rows[:], 0.0)
         nc.vector.memset(ones[:], 1.0)
-        nc.sync.dma_start(out=gamma_rows[0:1, :], in_=ln_gamma.unsqueeze(0))
 
         w_codes = w_keep.tile([P, PASSES, IN], U32, name="w_codes", align_bytes=64)
         w_scales = w_keep.tile([P, PASSES, IN], U8, name="w_scales", align_bytes=64)
@@ -184,115 +183,108 @@ def tile_slstmcell_t_v_kernel(
         def scalar_spare_work(t, k):
             if t + 1 < GATES:
                 regroup_weights(nc.scalar.copy, t + 1, k)
-            elif k < t:
-                store(k)
+            elif k >= 1:
+                store(k - 1)
 
         def finish_turn(t):
-            quantise_gradient(t, GATES - 1)
+            quantise_gradient(t, 2)
+            if t >= 2:
+                multiply(t, 2)
+            quantise_gradient(t, 3)
             if t + 1 < GATES:
                 quantise_weights(t + 1, 3)
                 for earlier in range(t + 1):
                     multiply(earlier, t + 1)
             else:
-                multiply(t, GATES - 1)
+                multiply(t, 3)
 
         def turn(t):
             tok = tok_of[t]
             next_place = t + 1
             more_weights = next_place < GATES
 
-            r, h2 = full("r"), full("h2")
-            sum_h2, minus_mean_h2, sum_sq = column("sum_h2"), column("minus_mean_h2"), column("sum_sq")
+            r, dy, h2 = full("r"), full("dy"), full("h2")
+            sum_dy, sum_h2, minus_mean_h2 = column("sum_dy"), column("sum_h2"), column("minus_mean_h2")
             nc.vector.tensor_mul(out=r[:], in0=tok["c_t"][:], in1=tok["q"][:])
+            fused(dy, tok["grad"], ALU.mult, 1.0, ALU.mult, gamma, accum_out=sum_dy[:])
             fused(h2, tok["o"], ALU.add, 1.0, ALU.mult, r, accum_out=sum_h2[:])
             nc.vector.tensor_scalar_mul(out=minus_mean_h2[:], in0=sum_h2[:], scalar1=-1.0 / H)
-            line = full("line")
+            line, sum_sq = full("line"), column("sum_sq")
             nc.scalar.activation(out=line[:], in_=h2[:], func=ACT.Square, bias=minus_mean_h2[:], accum_out=sum_sq[:])
-            if t > 0:
-                finish_turn(t - 1)
-
-            dy, dhn = full("dy"), full("dhn")
-            sum_dy, sum_dyh, minus_mean_dy, cov = column("sum_dy"), column("sum_dyh"), column("minus_mean_dy"), column("cov")
-            fused(dy, tok["grad"], ALU.mult, 1.0, ALU.mult, gamma, accum_out=sum_dy[:])
-            fused(dhn, dy, ALU.mult, 1.0, ALU.mult, h2, accum_out=sum_dyh[:])
-            nc.vector.tensor_scalar_mul(out=minus_mean_dy[:], in0=sum_dy[:], scalar1=-1.0 / H)
-            fused(cov, sum_dy, ALU.mult, minus_mean_h2[:], ALU.add, sum_dyh)
-
-            in_place(tok["z"], ACT.Tanh)
             in_place(tok["f"], ACT.Tanh, scale=0.5)
+            in_place(tok["z"], ACT.Tanh)
             in_place(tok["f"], ACT.Square)
             in_place(tok["i"], ACT.Exp)
 
+            dhn, a2, rn, minus_cn, output_term = full("dhn"), full("a2"), full("rn"), full("minus_cn"), full("output_term")
+            sum_dyh, minus_mean_dy, cov = column("sum_dyh"), column("minus_mean_dy"), column("cov")
             var_eps, inv_var, slope, offset = column("var_eps"), column("inv_var"), column("slope"), column("offset")
             rstd, minus_quarter_rstd = column("rstd"), column("minus_quarter_rstd")
-            a2, rn, minus_cn = full("a2"), full("rn"), full("minus_cn")
+            fused(a2, tok["o"], ALU.add, 1.0, ALU.mult, tok["q"])
+            fused(dhn, dy, ALU.mult, 1.0, ALU.mult, h2, accum_out=sum_dyh[:])
             nc.vector.tensor_scalar(
                 out=var_eps[:], in0=sum_sq[:], scalar1=0.25 / H, scalar2=LN_EPS, op0=ALU.mult, op1=ALU.add
             )
+            nc.vector.tensor_scalar_mul(out=minus_mean_dy[:], in0=sum_dy[:], scalar1=-1.0 / H)
             nc.gpsimd.tensor_tensor(out=rstd[:], in0=var_eps[:], in1=minus_half[:], op=ALU.pow)
             nc.gpsimd.tensor_scalar(
                 out=minus_quarter_rstd[:], in0=rstd[:], scalar1=-0.25, scalar2=0.0, op0=ALU.mult, op1=ALU.add
             )
-            fused(a2, tok["o"], ALU.add, 1.0, ALU.mult, tok["q"])
-            nc.vector.reciprocal(out=inv_var[:], in_=var_eps[:])
             nc.vector.tensor_mul(out=rn[:], in0=r[:], in1=tok["n_prev"][:])
+            nc.vector.reciprocal(out=inv_var[:], in_=var_eps[:])
+            fused(cov, sum_dy, ALU.mult, minus_mean_h2[:], ALU.add, sum_dyh)
+            fused(output_term, tok["o"], ALU.subtract, 1.0, ALU.mult, h2)
             fused(slope, cov, ALU.mult, -0.25 / H, ALU.mult, inv_var)
             nc.vector.tensor_sub(out=minus_cn[:], in0=rn[:], in1=tok["c_prev"][:])
             fused(offset, slope, ALU.mult, minus_mean_h2[:], ALU.add, minus_mean_dy)
             nc.scalar.activation(out=line[:], in_=h2[:], func=ACT.Identity, scale=slope[:], bias=offset[:])
             z_squared = tok_in.tile([P, H], F32, name="z_squared")
             nc.scalar.activation(out=z_squared[:], in_=tok["z"][:], func=ACT.Square)
-            scalar_spare_work(t, 0)
-            r_minus_z, forget_term, output_term = full("r_minus_z"), full("forget_term"), full("output_term")
+            r_minus_z = full("r_minus_z")
             nc.vector.tensor_sub(out=r_minus_z[:], in0=r[:], in1=tok["z"][:])
-            fused(forget_term, tok["f"], ALU.subtract, 1.0, ALU.mult, minus_cn)
-            fused(output_term, tok["o"], ALU.subtract, 1.0, ALU.mult, h2)
-            nc.vector.tensor_add(out=dhn[:], in0=dy[:], in1=line[:])
+            if t > 0:
+                finish_turn(t - 1)
+            scalar_spare_work(t, 0)
+            scalar_spare_work(t, 1)
+            if t + 1 < TOK_TILES:
+                in_place(tok_of[t + 1]["q"], ACT.Exp, scale=-1.0)
 
             dg_codes[t] = dg_keep.tile([P, PASSES, P], U32, name="dg_codes", align_bytes=64)
             dg_scales[t] = dg_keep.tile([P, PASSES, P], U8, name="dg_scales", align_bytes=64)
             dgo, dgf = work.tile([P, H], BF16, name="dgo"), work.tile([P, H], BF16, name="dgf")
             dgi, dgz = work.tile([P, H], BF16, name="dgi"), work.tile([P, H], BF16, name="dgz")
-            dc2, minus_dci = full("dc2"), full("minus_dci")
-
+            forget_term, dc2, minus_dci = full("forget_term"), full("dc2"), full("minus_dci")
+            nc.vector.tensor_add(out=dhn[:], in0=dy[:], in1=line[:])
+            fused(forget_term, tok["f"], ALU.subtract, 1.0, ALU.mult, minus_cn)
+            fused(dc2, dhn, ALU.mult, rstd[:], ALU.mult, a2)
             fused(dgo, output_term, ALU.mult, minus_quarter_rstd[:], ALU.mult, dhn)
             transpose_gradient(t, 0, dgo)
-            scalar_spare_work(t, 1)
             regroup_gradient(t, 0)
-
-            fused(dc2, dhn, ALU.mult, rstd[:], ALU.mult, a2)
+            scalar_spare_work(t, 2)
+            fused(minus_dci, dc2, ALU.mult, -0.5, ALU.mult, tok["i"])
             fused(dgf, forget_term, ALU.mult, 0.125, ALU.mult, dc2)
             transpose_gradient(t, 1, dgf)
-            scalar_spare_work(t, 2)
             regroup_gradient(t, 1)
-            quantise_gradient(t, 0)
-            multiply(t, 0)
+            if t + 1 < TOK_TILES:
+                in_place(tok_of[t + 1]["o"], ACT.Tanh, scale=0.5)
             if more_weights:
                 quantise_weights(next_place, 0)
-
-            fused(minus_dci, dc2, ALU.mult, -0.5, ALU.mult, tok["i"])
+            quantise_gradient(t, 0)
+            multiply(t, 0)
             nc.vector.tensor_mul(out=dgi[:], in0=minus_dci[:], in1=r_minus_z[:])
             transpose_gradient(t, 2, dgi)
-            scalar_spare_work(t, 3)
             regroup_gradient(t, 2)
+            if more_weights:
+                quantise_weights(next_place, 1)
+            fused(dgz, z_squared, ALU.subtract, 1.0, ALU.mult, minus_dci)
+            transpose_gradient(t, 3, dgz)
+            regroup_gradient(t, 3)
+            scalar_spare_work(t, 3)
             quantise_gradient(t, 1)
             if t >= 1:
                 multiply(t, 1)
             if more_weights:
-                quantise_weights(next_place, 1)
-
-            fused(dgz, z_squared, ALU.subtract, 1.0, ALU.mult, minus_dci)
-            transpose_gradient(t, 3, dgz)
-            if t + 1 < TOK_TILES:
-                in_place(tok_of[t + 1]["q"], ACT.Exp, scale=-1.0)
-            regroup_gradient(t, 3)
-            quantise_gradient(t, 2)
-            if t >= 2:
-                multiply(t, 2)
-            if more_weights:
                 quantise_weights(next_place, 2)
-            if t + 1 < TOK_TILES:
-                in_place(tok_of[t + 1]["o"], ACT.Tanh, scale=0.5)
 
             if t + 2 < GATES:
                 for c in range(PASSES_PER_GATE * (t + 2), PASSES_PER_GATE * (t + 3)):
@@ -301,6 +293,7 @@ def tile_slstmcell_t_v_kernel(
                 tok_of[t + 2] = load_token_tile(t + 2)
 
         load_weight_pass(0)
+        nc.sync.dma_start(out=gamma_rows[0:1, :], in_=ln_gamma.unsqueeze(0))
         log_n = [load(norm_in, n_t[P * t : P * (t + 1), :], F32, "log_n") for t in range(TOK_TILES)]
         load_weight_pass(1)
         tok_of = {0: load_token_tile(0)}

@@ -21,11 +21,15 @@ PACK = 4
 K_PASS = P * PACK
 TOK_TILES = B // P
 GATES = 4
-PASSES_PER_GATE = H // K_PASS
-PASSES = GATES * PASSES_PER_GATE
+HALVES = H // K_PASS
+PASSES = GATES * HALVES
 N_MX = 512
 N_STARTS = (0, IN - N_MX)
-W_PIECES = ((0, 512), (512, 256), (768, 128))
+W_SHARES = ((0, 512), (512, 512), (1024, 512), (1536, 256))
+W_CALLS = ((0, 1024), (1024, 512), (1536, 256))
+W_FRONT = 1024
+PE_START = 5
+PE_SLOTS = (2, 6, 10, 14)
 
 FLOPS = 2 * B * GATES * H * IN
 BYTES = (GATES + 2) * B * H * 4 + 3 * B * H * 2 + GATES * H * IN * 2 + H * 2 + B * IN * 4
@@ -36,26 +40,28 @@ def tile_slstmcell_t_v_kernel(
     gates, c_t, n_t, grad_out, out,
 ):
     nc = tc.nc
-    weight_at = (Wo, Wf, Wi, Wz)
+    weight_at = (Wo, Wi, Wf, Wz)
+    PLACE_O, PLACE_I, PLACE_F, PLACE_Z = 0, 1, 2, 3
     gate_row = {"o": 2, "f": 1, "i": 0, "z": 3}
 
     with ExitStack() as ctx:
         ctx.enter_context(tc.manual_schedule())
         const = ctx.enter_context(tc.tile_pool(name="const", bufs=1))
-        w_stage = ctx.enter_context(tc.tile_pool(name="w_stage", bufs=PASSES_PER_GATE))
+        w_stage = ctx.enter_context(tc.tile_pool(name="w_stage", bufs=4))
+        w_group = ctx.enter_context(tc.tile_pool(name="w_group", bufs=1))
         w_keep = ctx.enter_context(tc.tile_pool(name="w_keep", bufs=1))
-        norm_in = ctx.enter_context(tc.tile_pool(name="norm_in", bufs=TOK_TILES))
+        norm = ctx.enter_context(tc.tile_pool(name="norm", bufs=1))
         tok_in = ctx.enter_context(tc.tile_pool(name="tok_in", bufs=2))
+        tok_once = ctx.enter_context(tc.tile_pool(name="tok_once", bufs=1))
         work = ctx.enter_context(tc.tile_pool(name="work", bufs=1))
+        work2 = ctx.enter_context(tc.tile_pool(name="work2", bufs=2))
+        feat = ctx.enter_context(tc.tile_pool(name="feat", bufs=1))
         stats = ctx.enter_context(tc.tile_pool(name="stats", bufs=2))
-        dg_stage = ctx.enter_context(tc.tile_pool(name="dg_stage", bufs=2))
-        dg_keep = ctx.enter_context(tc.tile_pool(name="dg_keep", bufs=3))
-        out_stage = ctx.enter_context(tc.tile_pool(name="out_stage", bufs=2))
-        psum_t = ctx.enter_context(tc.psum_pool(name="psum_t", bufs=2))
-        psum_acc = ctx.enter_context(tc.psum_pool(name="psum_acc", bufs=3))
+        dg_keep = ctx.enter_context(tc.tile_pool(name="dg_keep", bufs=TOK_TILES))
+        out_stage = ctx.enter_context(tc.tile_pool(name="out_stage", bufs=1))
+        rot = ctx.enter_context(tc.psum_pool(name="rot", bufs=4))
+        psum_acc = ctx.enter_context(tc.psum_pool(name="psum_acc", bufs=2))
 
-        identity = const.tile([P, P], F32, name="identity")
-        make_identity(nc, identity[:])
         minus_half = const.tile([P, 1], F32, name="minus_half")
         nc.vector.memset(minus_half[:], -0.5)
         gamma_rows = const.tile([P, H], BF16, name="gamma_rows")
@@ -63,258 +69,438 @@ def tile_slstmcell_t_v_kernel(
         gamma = const.tile([P, H], BF16, name="gamma")
         nc.vector.memset(gamma_rows[:], 0.0)
         nc.vector.memset(ones[:], 1.0)
+        identity = const.tile([P, P], F32, name="identity")
+        make_identity(nc, identity[:])
 
         w_codes = w_keep.tile([P, PASSES, IN], U32, name="w_codes", align_bytes=64)
         w_scales = w_keep.tile([P, PASSES, IN], U8, name="w_scales", align_bytes=64)
         w_raw = {}
-        w_grouped = {}
+        w_front, w_back = {}, {}
 
         def load_weight_pass(c):
-            weight = weight_at[c // PASSES_PER_GATE]
-            first_row = K_PASS * (c % PASSES_PER_GATE)
+            weight = weight_at[c // HALVES]
+            first_row = K_PASS * (c % HALVES)
             w_raw[c] = w_stage.tile([P, PACK, IN], BF16, name="w_raw")
-            w_grouped[c] = w_stage.tile([P, IN, PACK], BF16, name="w_grouped", align_bytes=64)
-            for u in range(2):
-                rows = weight[first_row + 2 * P * u : first_row + 2 * P * (u + 1), 0:IN]
-                nc.sync.dma_start(out=w_raw[c][:, 2 * u : 2 * u + 2, :], in_=rows.rearrange("(p e) n -> p e n", e=2))
+            rows = weight[first_row : first_row + K_PASS, 0:IN]
+            nc.sync.dma_start(out=w_raw[c][:], in_=rows.rearrange("(j p) n -> p j n", p=P))
 
-        def weight_share(s, quarter):
-            c = PASSES_PER_GATE * s + quarter // 2
-            return c, (W_PIECES[:1] if quarter % 2 == 0 else W_PIECES[1:])
+        def grouped_columns(s, first, width):
+            if s not in w_front:
+                w_front[s] = w_group.tile([P, W_FRONT, PACK], BF16, name="w_front", align_bytes=64)
+                w_back[s] = w_group.tile([P, HALVES * IN - W_FRONT, PACK], BF16, name="w_back", align_bytes=64)
+            if first < W_FRONT:
+                return w_front[s][:, first : first + width, :]
+            return w_back[s][:, first - W_FRONT : first - W_FRONT + width, :]
 
-        def regroup_weights(copy, s, quarter):
-            c, pieces = weight_share(s, quarter)
-            for n0, width in pieces:
-                copy(
-                    out=w_grouped[c][:, n0 : n0 + width, :].rearrange("p (c i) v -> p c v i", i=4),
-                    in_=w_raw[c][:, :, n0 : n0 + width].rearrange("p v (c i) -> p c v i", i=4),
-                )
+        def regroup_weights(copy, s, share):
+            first, width = share
+            for c in range(HALVES):
+                low, high = max(first, IN * c), min(first + width, IN * (c + 1))
+                if low < high:
+                    copy(
+                        out=grouped_columns(s, low, high - low).rearrange("p (c i) v -> p c v i", i=4),
+                        in_=w_raw[HALVES * s + c][:, :, low - IN * c : high - IN * c].rearrange(
+                            "p v (c i) -> p c v i", i=4
+                        ),
+                    )
 
-        def quantise_weights(s, quarter):
-            c, pieces = weight_share(s, quarter)
-            for n0, width in pieces:
-                nc.vector.quantize_mx(
-                    out=w_codes[:, c, n0 : n0 + width].bitcast(E4M3X4),
-                    scales=w_scales[:, c, n0 : n0 + width],
-                    in_=w_grouped[c][:, n0 : n0 + width, :].rearrange("p n v -> p (n v)"),
-                )
+        def quantise_weights(s, call):
+            first, width = call
+            passes = slice(HALVES * s, HALVES * (s + 1))
+            nc.vector.quantize_mx(
+                out=w_codes[:, passes, :].rearrange("p c n -> p (c n)")[:, first : first + width].bitcast(E4M3X4),
+                scales=w_scales[:, passes, :].rearrange("p c n -> p (c n)")[:, first : first + width],
+                in_=grouped_columns(s, first, width).rearrange("p n v -> p (n v)"),
+            )
 
-        def load(pool, source, dtype, name):
-            loaded = pool.tile([P, H], dtype, name=name)
-            nc.sync.dma_start(out=loaded[:], in_=source)
-            return loaded
+        tok_of = {t: {} for t in range(TOK_TILES)}
+        val = {}
 
-        def load_token_tile(t):
+        def load_inputs(t, names):
             rows = slice(P * t, P * (t + 1))
-            return {
-                "q": log_n[t],
-                "o": load(tok_in, gates[gate_row["o"], rows, :], F32, "gate_o"),
-                "c_t": load(tok_in, c_t[rows, :], F32, "cell"),
-                "grad": load(tok_in, grad_out[rows, :], BF16, "grad"),
-                "z": load(tok_in, gates[gate_row["z"], rows, :], F32, "gate_z"),
-                "n_prev": load(tok_in, n_prev[rows, :], BF16, "n_before"),
-                "c_prev": load(tok_in, c_prev[rows, :], BF16, "c_before"),
-                "f": load(tok_in, gates[gate_row["f"], rows, :], F32, "gate_f"),
-                "i": load(tok_in, gates[gate_row["i"], rows, :], F32, "gate_i"),
-            }
+            for name in names:
+                if name in gate_row:
+                    tile_, source = tok_in.tile([P, H], F32, name="gate_" + name), gates[gate_row[name], rows, :]
+                elif name == "c_t":
+                    tile_, source = tok_in.tile([P, H], F32, name="cell"), c_t[rows, :]
+                elif name == "q":
+                    tile_, source = norm.tile([P, H], F32, name="log_n", tag="slot%d" % t), n_t[rows, :]
+                elif name == "grad":
+                    tile_, source = tok_in.tile([P, H], BF16, name="grad"), grad_out[rows, :]
+                elif name == "n_prev":
+                    tile_, source = tok_once.tile([P, H], BF16, name="n_before"), n_prev[rows, :]
+                else:
+                    tile_, source = tok_once.tile([P, H], BF16, name="c_before"), c_prev[rows, :]
+                nc.sync.dma_start(out=tile_[:], in_=source)
+                tok_of[t][name] = tile_
 
         def in_place(tile_, func, scale=1.0):
             nc.scalar.activation(out=tile_[:], in_=tile_[:], func=func, scale=scale)
 
-        def full(name):
-            return work.tile([P, H], F32, name=name)
-
         def column(name):
             return stats.tile([P, 1], F32, name=name)
 
-        def fused(out_, in0, op0, scalar, op1, in1, accum_out=None):
+        def stt(out_, in0, op0, scalar, op1, in1, accum_out=None):
             nc.vector.scalar_tensor_tensor(
-                out=out_[:], in0=in0[:], scalar=scalar, in1=in1[:], op0=op0, op1=op1, accum_out=accum_out
+                out=out_, in0=in0, scalar=scalar, in1=in1, op0=op0, op1=op1, accum_out=accum_out
             )
+
+        def act_ln(t):
+            nc.scalar.activation(out=tok_of[t]["q"][:], in_=tok_of[t]["q"][:], func=ACT.Ln, bias=DIV_EPS)
+
+        def act_q(t):
+            in_place(tok_of[t]["q"], ACT.Exp, scale=-1.0)
+
+        def act_o(t):
+            in_place(tok_of[t]["o"], ACT.Tanh, scale=0.5)
+
+        def act_f(t):
+            in_place(tok_of[t]["f"], ACT.Tanh, scale=0.5)
+
+        def act_f2(t):
+            in_place(tok_of[t]["f"], ACT.Square)
+
+        def act_z(t):
+            in_place(tok_of[t]["z"], ACT.Tanh, scale=-1.0)
+
+        def act_z2(t):
+            val["zsq", t] = work2.tile([P, H], F32, name="z_squared", tag="zsq")
+            nc.scalar.activation(out=val["zsq", t][:], in_=tok_of[t]["z"][:], func=ACT.Square)
+
+        def act_i(t):
+            in_place(tok_of[t]["i"], ACT.Exp)
+
+        def make_r(eng, t):
+            if t == 0:
+                val["r", t] = work2.tile([P, H], F32, name="r_first", tag="zsq")
+            else:
+                val["r", t] = norm.tile([P, H], F32, name="r", tag="slot%d" % (t - 1))
+            eng.tensor_tensor(out=val["r", t][:], in0=tok_of[t]["c_t"][:], in1=tok_of[t]["q"][:], op=ALU.mult)
+
+        def make_rn(eng, t):
+            val["mcn", t] = work2.tile([P, H], F32, name="mcn")
+            eng.tensor_tensor(out=val["mcn", t][:], in0=val["r", t][:], in1=tok_of[t]["n_prev"][:], op=ALU.mult)
+
+        def make_mcn(eng, t):
+            eng.tensor_tensor(out=val["mcn", t][:], in0=val["mcn", t][:], in1=tok_of[t]["c_prev"][:], op=ALU.subtract)
+
+        def make_dy(t):
+            val["dy", t] = work2.tile([P, H], F32, name="dy")
+            val["sum_dy", t], val["mmdy", t] = column("sum_dy"), column("mmdy")
+            stt(val["dy", t][:], tok_of[t]["grad"][:], ALU.mult, 1.0, ALU.mult, gamma[:], accum_out=val["sum_dy", t][:])
+            nc.gpsimd.tensor_scalar(
+                out=val["mmdy", t][:], in0=val["sum_dy", t][:], scalar1=-1.0 / H, scalar2=0.0, op0=ALU.mult, op1=ALU.add
+            )
+
+        def make_h2(t):
+            val["h2", t] = work.tile([P, H], F32, name="h2")
+            val["sum_h2", t], val["mm", t] = column("sum_h2"), column("mm")
+            stt(val["h2", t][:], tok_of[t]["o"][:], ALU.add, 1.0, ALU.mult, val["r", t][:], accum_out=val["sum_h2", t][:])
+            nc.vector.tensor_scalar_mul(out=val["mm", t][:], in0=val["sum_h2", t][:], scalar1=-1.0 / H)
+
+        def make_dyh(t):
+            junk = work.tile([P, H], F32, name="junk_products", tag="u")
+            val["sum_dyh", t] = column("sum_dyh")
+            stt(junk[:], val["dy", t][:], ALU.mult, 1.0, ALU.mult, val["h2", t][:], accum_out=val["sum_dyh", t][:])
+
+        def act_square(t):
+            junk = feat.tile([P, H], F32, name="junk_squares", tag="uT")
+            val["sum_sq", t] = column("sum_sq")
+            nc.scalar.activation(
+                out=junk[:], in_=val["h2", t][:], func=ACT.Square, bias=val["mm", t][:], accum_out=val["sum_sq", t][:]
+            )
+
+        def half_columns(c):
+            return slice(N_MX * c, N_MX * (c + 1))
+
+        def statistics(t):
+            var_eps, inv_var, cov = column("var_eps"), column("inv_var"), column("cov")
+            slope, offset, rstd, r_offset = column("slope"), column("offset"), column("rstd"), column("r_offset")
+            mm = val["mm", t]
+            diag_r = stats.tile([P, P], F32, name="diag_r")
+            diag_s = stats.tile([P, P], F32, name="diag_s")
+            nc.vector.tensor_scalar(
+                out=var_eps[:], in0=val["sum_sq", t][:], scalar1=0.25 / H, scalar2=LN_EPS, op0=ALU.mult, op1=ALU.add
+            )
+            nc.gpsimd.tensor_tensor(out=rstd[:], in0=var_eps[:], in1=minus_half[:], op=ALU.pow)
+            stt(cov[:], val["sum_dy", t][:], ALU.mult, mm[:], ALU.add, val["sum_dyh", t][:])
+            nc.vector.reciprocal(out=inv_var[:], in_=var_eps[:])
+            stt(slope[:], cov[:], ALU.mult, -0.25 / H, ALU.mult, inv_var[:])
+            stt(offset[:], slope[:], ALU.mult, mm[:], ALU.add, val["mmdy", t][:])
+            nc.vector.tensor_scalar_mul(out=diag_r[:], in0=identity[:], scalar1=rstd[:])
+            banks = [rot.tile([P, N_MX], F32, name="dh", tag="bank") for c in range(HALVES)]
+            for c in range(HALVES):
+                nc.tensor.matmul(out=banks[c][:], lhsT=diag_r[:], rhs=val["dy", t][:, half_columns(c)], start=True, stop=False)
+            nc.vector.tensor_scalar(
+                out=diag_s[:], in0=identity[:], scalar1=slope[:], scalar2=rstd[:], op0=ALU.mult, op1=ALU.mult
+            )
+            for c in range(HALVES):
+                nc.tensor.matmul(out=banks[c][:], lhsT=diag_s[:], rhs=val["h2", t][:, half_columns(c)], start=False, stop=True)
+            nc.gpsimd.tensor_tensor(out=r_offset[:], in0=offset[:], in1=rstd[:], op=ALU.mult)
+            val["dh", t], val["r_offset", t] = banks, r_offset
+
+        def make_u(t, c):
+            if c == 0:
+                val["u", t] = work.tile([P, H], F32, name="u")
+            stt(
+                val["u", t][:, half_columns(c)], val["dh", t][c][:], ALU.add, val["r_offset", t][:], ALU.mult,
+                tok_of[t]["q"][:, half_columns(c)],
+            )
+
+        def flip(source, c):
+            bank = rot.tile([P, PACK, P], F32, name="bank")
+            for j in range(PACK):
+                first = (PACK * c + j) * P
+                nc.tensor.transpose(bank[:, j, :], source[:, first : first + P], identity[:])
+            return bank[:].rearrange("p j k -> p k j")
+
+        def flip_sum(first_source, second_source, c):
+            bank = rot.tile([P, PACK, P], F32, name="bank")
+            for j in range(PACK):
+                columns = slice((PACK * c + j) * P, (PACK * c + j + 1) * P)
+                nc.tensor.matmul(
+                    out=bank[:, j, :], lhsT=first_source[:, columns], rhs=identity[:], is_transpose=True, start=True, stop=False
+                )
+                nc.tensor.matmul(
+                    out=bank[:, j, :], lhsT=second_source[:, columns], rhs=identity[:], is_transpose=True, start=False, stop=True
+                )
+            return bank[:].rearrange("p j k -> p k j")
+
+        def flip_and_copy_u(t, c):
+            if c == 0:
+                val["uT", t] = feat.tile([P, HALVES, P, PACK], F32, name="uT")
+            nc.scalar.copy(out=val["uT", t][:, c], in_=flip(val["u", t], c))
 
         dg_codes, dg_scales = {}, {}
-        dg_flipped = {}
-        dg_grouped = {}
         acc = {}
+        passes_done = {}
 
-        def transpose_gradient(t, s, dg):
-            words = dg[:].bitcast(F32)
-            dg_flipped[t, s] = psum_t.tile([P, PASSES_PER_GATE, 2, P], F32, name="dg_flipped")
-            for half in range(PASSES_PER_GATE):
-                for u in range(2):
-                    first = (2 * half + u) * P
-                    nc.tensor.transpose(dg_flipped[t, s][:, half, u, :], words[:, first : first + P], identity[:])
-
-        def regroup_gradient(t, s):
-            dg_grouped[t, s] = dg_stage.tile([P, PASSES_PER_GATE, P, PACK], BF16, name="dg_grouped", align_bytes=64)
-            nc.scalar.copy(
-                out=dg_grouped[t, s][:].bitcast(F32), in_=dg_flipped[t, s][:].rearrange("p c u t -> p c t u")
-            )
-
-        def quantise_gradient(t, s):
-            passes = slice(PASSES_PER_GATE * s, PASSES_PER_GATE * (s + 1))
+        def quantise_half(t, c):
             nc.vector.quantize_mx(
-                out=dg_codes[t][:, passes, :].rearrange("p c t -> p (c t)").bitcast(E5M2X4),
-                scales=dg_scales[t][:, passes, :].rearrange("p c t -> p (c t)"),
-                in_=dg_grouped[t, s][:].rearrange("p c t v -> p (c t v)"),
+                out=dg_codes[t][:, c].rearrange("p s k -> p (s k)").bitcast(E5M2X4),
+                scales=dg_scales[t][:, c].rearrange("p s k -> p (s k)"),
+                in_=val["dgT", t][:, c].rearrange("p s k j -> p (s k j)"),
             )
 
-        def multiply(t, s):
-            if s == 0:
-                acc[t] = [psum_acc.tile([P, N_MX], F32, name="acc_low"), psum_acc.tile([P, N_MX], F32, name="acc_high")]
-            for c in range(PASSES_PER_GATE * s, PASSES_PER_GATE * (s + 1)):
-                for window, n0 in enumerate(N_STARTS):
-                    nc.tensor.matmul_mx(
-                        out=acc[t][window][:],
-                        lhsT=dg_codes[t][:, c, :].bitcast(E5M2X4),
-                        lhsT_scale=dg_scales[t][:, c, :],
-                        rhs=w_codes[:, c, n0 : n0 + N_MX].bitcast(E4M3X4),
-                        rhs_scale=w_scales[:, c, n0 : n0 + N_MX],
-                        start=(c == 0),
-                        stop=(c == PASSES - 1),
-                    )
+        def quantise_pass(t, c, s):
+            nc.vector.quantize_mx(
+                out=dg_codes[t][:, c, s].bitcast(E5M2X4),
+                scales=dg_scales[t][:, c, s],
+                in_=val["dgT", t][:, c, s].rearrange("p k j -> p (k j)"),
+            )
 
-        def store(t):
+        def multiply(t, s, c):
+            if t not in acc:
+                acc[t] = [psum_acc.tile([P, N_MX], F32, name="acc_low"), psum_acc.tile([P, N_MX], F32, name="acc_high")]
+                passes_done[t] = 0
+            for side, n0 in enumerate(N_STARTS):
+                nc.tensor.matmul_mx(
+                    out=acc[t][side][:],
+                    lhsT=dg_codes[t][:, c, s].bitcast(E5M2X4),
+                    lhsT_scale=dg_scales[t][:, c, s],
+                    rhs=w_codes[:, HALVES * s + c, n0 : n0 + N_MX].bitcast(E4M3X4),
+                    rhs_scale=w_scales[:, HALVES * s + c, n0 : n0 + N_MX],
+                    start=(passes_done[t] == 0),
+                    stop=(passes_done[t] == PASSES - 1),
+                )
+            passes_done[t] += 1
+
+        def store(t, second_copy):
             result = out_stage.tile([P, IN], F32, name="result")
             nc.scalar.copy(out=result[:, 0:N_MX], in_=acc[t][0][:])
-            nc.scalar.copy(out=result[:, N_MX:IN], in_=acc[t][1][:, 2 * N_MX - IN : N_MX])
+            second_copy(out=result[:, N_MX:IN], in_=acc[t][1][:, 2 * N_MX - IN : N_MX])
             nc.sync.dma_start(out=out[P * t : P * (t + 1), :], in_=result[:])
 
-        def scalar_spare_work(t, k):
-            if t + 1 < GATES:
-                regroup_weights(nc.scalar.copy, t + 1, k)
-            elif k >= 1:
-                store(k - 1)
+        pe_jobs = []
 
-        def finish_turn(t):
-            quantise_gradient(t, 2)
-            if t >= 2:
-                multiply(t, 2)
-            quantise_gradient(t, 3)
-            if t + 1 < GATES:
-                quantise_weights(t + 1, 3)
-                for earlier in range(t + 1):
-                    multiply(earlier, t + 1)
-            else:
-                multiply(t, 3)
+        def push(t, places, halves):
+            for s in places:
+                for c in halves:
+                    pe_jobs.append((t, s, c))
 
-        def turn(t):
+        def pe_fill(n):
+            for count in range(n):
+                if pe_jobs:
+                    job = pe_jobs.pop(0)
+                    if job[0] == "store":
+                        store(job[1], nc.scalar.copy)
+                    else:
+                        multiply(*job)
+
+        s_jobs = []
+
+        def s_fill(n):
+            for count in range(n):
+                if s_jobs:
+                    s, k = s_jobs.pop(0)
+                    regroup_weights(nc.scalar.copy, s, W_SHARES[k])
+
+        def products(t, hooks):
             tok = tok_of[t]
-            next_place = t + 1
-            more_weights = next_place < GATES
+            dgT = val["dgT", t]
+            uT = val["uT", t]
+            bank, tile_of = {}, {}
 
-            r, dy, h2 = full("r"), full("dy"), full("h2")
-            sum_dy, sum_h2, minus_mean_h2 = column("sum_dy"), column("sum_h2"), column("minus_mean_h2")
-            nc.vector.tensor_mul(out=r[:], in0=tok["c_t"][:], in1=tok["q"][:])
-            fused(dy, tok["grad"], ALU.mult, 1.0, ALU.mult, gamma, accum_out=sum_dy[:])
-            fused(h2, tok["o"], ALU.add, 1.0, ALU.mult, r, accum_out=sum_h2[:])
-            nc.vector.tensor_scalar_mul(out=minus_mean_h2[:], in0=sum_h2[:], scalar1=-1.0 / H)
-            line, sum_sq = full("line"), column("sum_sq")
-            nc.scalar.activation(out=line[:], in_=h2[:], func=ACT.Square, bias=minus_mean_h2[:], accum_out=sum_sq[:])
-            in_place(tok["f"], ACT.Tanh, scale=0.5)
-            in_place(tok["z"], ACT.Tanh)
-            in_place(tok["f"], ACT.Square)
-            in_place(tok["i"], ACT.Exp)
+            def fill(name, c):
+                if name == "rz":
+                    bank[name, c] = flip_sum(val["r", t], tok["z"], c)
+                else:
+                    source = {"to": tok["o"], "i": tok["i"], "ct": tok["c_t"], "tf2": tok["f"], "mcn": val["mcn", t],
+                              "zsq": val["zsq", t]}[name]
+                    bank[name, c] = flip(source, c)
 
-            dhn, a2, rn, minus_cn, output_term = full("dhn"), full("a2"), full("rn"), full("minus_cn"), full("output_term")
-            sum_dyh, minus_mean_dy, cov = column("sum_dyh"), column("minus_mean_dy"), column("cov")
-            var_eps, inv_var, slope, offset = column("var_eps"), column("inv_var"), column("slope"), column("offset")
-            rstd, minus_quarter_rstd = column("rstd"), column("minus_quarter_rstd")
-            fused(a2, tok["o"], ALU.add, 1.0, ALU.mult, tok["q"])
-            fused(dhn, dy, ALU.mult, 1.0, ALU.mult, h2, accum_out=sum_dyh[:])
-            nc.vector.tensor_scalar(
-                out=var_eps[:], in0=sum_sq[:], scalar1=0.25 / H, scalar2=LN_EPS, op0=ALU.mult, op1=ALU.add
+            def chain(name, c):
+                tile_of[name, c] = feat.tile([P, P, PACK], F32, name=name)
+                return tile_of[name, c][:]
+
+            def op(name, c):
+                if name == "dc":
+                    stt(chain("dcT", c), bank["to", c], ALU.add, 1.0, ALU.mult, uT[:, c])
+                elif name == "mdci":
+                    stt(chain("mdciT", c), bank["i", c], ALU.mult, -0.5, ALU.mult, tile_of["dcT", c][:])
+                elif name == "e":
+                    stt(chain("eT", c), bank["ct", c], ALU.mult, -0.25, ALU.mult, tile_of["dcT", c][:])
+                elif name == "g":
+                    stt(chain("gT", c), bank["tf2", c], ALU.subtract, 1.0, ALU.mult, tile_of["dcT", c][:])
+                elif name == "dgi":
+                    nc.vector.tensor_tensor(out=dgT[:, c, PLACE_I], in0=bank["rz", c], in1=tile_of["mdciT", c][:], op=ALU.mult)
+                elif name == "dgo":
+                    stt(dgT[:, c, PLACE_O], bank["to", c], ALU.subtract, 1.0, ALU.mult, tile_of["eT", c][:])
+                elif name == "dgf":
+                    stt(dgT[:, c, PLACE_F], bank["mcn", c], ALU.mult, 0.125, ALU.mult, tile_of["gT", c][:])
+                else:
+                    stt(dgT[:, c, PLACE_Z], bank["zsq", c], ALU.subtract, 1.0, ALU.mult, tile_of["mdciT", c][:])
+
+            order = (
+                ((("to", 0), ("i", 0), ("ct", 0), ("tf2", 0)), ("dc", 0)),
+                ((), ("mdci", 0)),
+                ((("rz", 0),), ("e", 0)),
+                ((("mcn", 0),), ("g", 0)),
+                ((("to", 1),), ("dgi", 0)),
+                ((("zsq", 0),), ("dgo", 0)),
+                ((("i", 1),), ("dgf", 0)),
+                ((("ct", 1),), ("dc", 1)),
+                ((), ("dgz", 0)),
+                ((("tf2", 1),), ("mdci", 1)),
+                ((("rz", 1),), ("e", 1)),
+                ((("mcn", 1),), ("g", 1)),
+                ((), ("dgi", 1)),
+                ((("zsq", 1),), ("dgo", 1)),
+                ((), ("dgf", 1)),
+                ((), ("dgz", 1)),
             )
-            nc.vector.tensor_scalar_mul(out=minus_mean_dy[:], in0=sum_dy[:], scalar1=-1.0 / H)
-            nc.gpsimd.tensor_tensor(out=rstd[:], in0=var_eps[:], in1=minus_half[:], op=ALU.pow)
-            nc.gpsimd.tensor_scalar(
-                out=minus_quarter_rstd[:], in0=rstd[:], scalar1=-0.25, scalar2=0.0, op0=ALU.mult, op1=ALU.add
-            )
-            nc.vector.tensor_mul(out=rn[:], in0=r[:], in1=tok["n_prev"][:])
-            nc.vector.reciprocal(out=inv_var[:], in_=var_eps[:])
-            fused(cov, sum_dy, ALU.mult, minus_mean_h2[:], ALU.add, sum_dyh)
-            fused(output_term, tok["o"], ALU.subtract, 1.0, ALU.mult, h2)
-            fused(slope, cov, ALU.mult, -0.25 / H, ALU.mult, inv_var)
-            nc.vector.tensor_sub(out=minus_cn[:], in0=rn[:], in1=tok["c_prev"][:])
-            fused(offset, slope, ALU.mult, minus_mean_h2[:], ALU.add, minus_mean_dy)
-            nc.scalar.activation(out=line[:], in_=h2[:], func=ACT.Identity, scale=slope[:], bias=offset[:])
-            z_squared = tok_in.tile([P, H], F32, name="z_squared")
-            nc.scalar.activation(out=z_squared[:], in_=tok["z"][:], func=ACT.Square)
-            r_minus_z = full("r_minus_z")
-            nc.vector.tensor_sub(out=r_minus_z[:], in0=r[:], in1=tok["z"][:])
-            if t > 0:
-                finish_turn(t - 1)
-            scalar_spare_work(t, 0)
-            scalar_spare_work(t, 1)
-            if t + 1 < TOK_TILES:
-                in_place(tok_of[t + 1]["q"], ACT.Exp, scale=-1.0)
+            for n, (fills, product) in enumerate(order):
+                for name, c in fills:
+                    fill(name, c)
+                op(*product)
+                if n in hooks:
+                    hooks[n]()
 
-            dg_codes[t] = dg_keep.tile([P, PASSES, P], U32, name="dg_codes", align_bytes=64)
-            dg_scales[t] = dg_keep.tile([P, PASSES, P], U8, name="dg_scales", align_bytes=64)
-            dgo, dgf = work.tile([P, H], BF16, name="dgo"), work.tile([P, H], BF16, name="dgf")
-            dgi, dgz = work.tile([P, H], BF16, name="dgi"), work.tile([P, H], BF16, name="dgz")
-            forget_term, dc2, minus_dci = full("forget_term"), full("dc2"), full("minus_dci")
-            nc.vector.tensor_add(out=dhn[:], in0=dy[:], in1=line[:])
-            fused(forget_term, tok["f"], ALU.subtract, 1.0, ALU.mult, minus_cn)
-            fused(dc2, dhn, ALU.mult, rstd[:], ALU.mult, a2)
-            fused(dgo, output_term, ALU.mult, minus_quarter_rstd[:], ALU.mult, dhn)
-            transpose_gradient(t, 0, dgo)
-            regroup_gradient(t, 0)
-            scalar_spare_work(t, 2)
-            fused(minus_dci, dc2, ALU.mult, -0.5, ALU.mult, tok["i"])
-            fused(dgf, forget_term, ALU.mult, 0.125, ALU.mult, dc2)
-            transpose_gradient(t, 1, dgf)
-            regroup_gradient(t, 1)
-            if t + 1 < TOK_TILES:
-                in_place(tok_of[t + 1]["o"], ACT.Tanh, scale=0.5)
-            if more_weights:
-                quantise_weights(next_place, 0)
-            quantise_gradient(t, 0)
-            multiply(t, 0)
-            nc.vector.tensor_mul(out=dgi[:], in0=minus_dci[:], in1=r_minus_z[:])
-            transpose_gradient(t, 2, dgi)
-            regroup_gradient(t, 2)
-            if more_weights:
-                quantise_weights(next_place, 1)
-            fused(dgz, z_squared, ALU.subtract, 1.0, ALU.mult, minus_dci)
-            transpose_gradient(t, 3, dgz)
-            regroup_gradient(t, 3)
-            scalar_spare_work(t, 3)
-            quantise_gradient(t, 1)
-            if t >= 1:
-                multiply(t, 1)
-            if more_weights:
-                quantise_weights(next_place, 2)
-
-            if t + 2 < GATES:
-                for c in range(PASSES_PER_GATE * (t + 2), PASSES_PER_GATE * (t + 3)):
-                    load_weight_pass(c)
-            if t + 2 < TOK_TILES:
-                tok_of[t + 2] = load_token_tile(t + 2)
-
-        load_weight_pass(0)
         nc.sync.dma_start(out=gamma_rows[0:1, :], in_=ln_gamma.unsqueeze(0))
-        log_n = [load(norm_in, n_t[P * t : P * (t + 1), :], F32, "log_n") for t in range(TOK_TILES)]
-        load_weight_pass(1)
-        tok_of = {0: load_token_tile(0)}
         for t in range(TOK_TILES):
-            nc.scalar.activation(out=log_n[t][:], in_=log_n[t][:], func=ACT.Ln, bias=DIV_EPS)
-        in_place(tok_of[0]["q"], ACT.Exp, scale=-1.0)
-        in_place(tok_of[0]["o"], ACT.Tanh, scale=0.5)
-        for first_quarter in (0, 2):
-            for quarter in (first_quarter, first_quarter + 1):
-                regroup_weights(nc.vector.tensor_copy, 0, quarter)
-            for quarter in (first_quarter, first_quarter + 1):
-                quantise_weights(0, quarter)
-            if first_quarter == 0:
-                for n0 in range(0, H, N_MX):
-                    spread = psum_t.tile([P, N_MX], F32, name="gamma_spread", tag="dg_flipped")
-                    nc.tensor.matmul(out=spread[:], lhsT=ones[:], rhs=gamma_rows[:, n0 : n0 + N_MX], start=True, stop=True)
-                    nc.vector.tensor_copy(out=gamma[:, n0 : n0 + N_MX], in_=spread[:])
+            load_inputs(t, ("q",))
+        load_weight_pass(0)
+        load_inputs(0, ("c_t", "o", "grad", "z", "n_prev", "c_prev", "i", "f"))
+        load_inputs(1, ("grad", "c_t"))
+        load_weight_pass(1)
+        load_inputs(1, ("z", "n_prev", "o", "c_prev", "i", "f"))
         load_weight_pass(2)
         load_weight_pass(3)
-        tok_of[1] = load_token_tile(1)
+
         for t in range(TOK_TILES):
-            turn(t)
-        finish_turn(TOK_TILES - 1)
-        store(TOK_TILES - 1)
+            act_ln(t)
+        act_q(0)
+        act_o(0)
+        act_z(0)
+        for n0 in range(0, H, N_MX):
+            spread = rot.tile([P, N_MX], F32, name="gamma_spread", tag="bank")
+            nc.tensor.matmul(out=spread[:], lhsT=ones[:], rhs=gamma_rows[:, n0 : n0 + N_MX], start=True, stop=True)
+            nc.vector.tensor_copy(out=gamma[:, n0 : n0 + N_MX], in_=spread[:])
+        regroup_weights(nc.vector.tensor_copy, 0, (0, 512))
+        regroup_weights(nc.vector.tensor_copy, 0, (512, 384))
+        for call in ((0, 512), (512, 256), (768, 128)):
+            quantise_weights(0, call)
+        make_r(nc.vector, 0)
+
+        for t in range(TOK_TILES):
+            last = t == TOK_TILES - 1
+            make_h2(t)
+            act_square(t)
+            if t == 0:
+                make_dy(0)
+            make_dyh(t)
+            pe_fill(PE_START)
+            if t == 0:
+                act_z2(0)
+                act_i(0)
+                make_rn(nc.vector, 0)
+            else:
+                regroup_weights(nc.scalar.copy, t, W_SHARES[0])
+                regroup_weights(nc.scalar.copy, t, W_SHARES[1])
+            statistics(t)
+            if t == 0:
+                make_mcn(nc.vector, 0)
+                regroup_weights(nc.vector.tensor_copy, 0, (896, 128))
+                regroup_weights(nc.vector.tensor_copy, 0, (1024, 512))
+                regroup_weights(nc.vector.tensor_copy, 0, (1536, 256))
+                for call in ((896, 128), (1024, 512), (1536, 256)):
+                    quantise_weights(0, call)
+                act_f(0)
+                act_f2(0)
+            else:
+                for c in range(HALVES):
+                    quantise_half(t - 1, c)
+                regroup_weights(nc.vector.tensor_copy, t, W_SHARES[3])
+                for call in (W_CALLS[1], W_CALLS[2], W_CALLS[0]):
+                    quantise_weights(t, call)
+                for earlier in range(t - 1):
+                    push(earlier, (t,), (0, 1))
+                    if last:
+                        pe_jobs.append(("store", earlier))
+                push(t - 1, range(t + 1), (0, 1))
+                if last:
+                    pe_jobs.append(("store", t - 1))
+            if not last:
+                act_q(t + 1)
+                act_z(t + 1)
+                make_dy(t + 1)
+            make_u(t, 0)
+            flip_and_copy_u(t, 0)
+            make_u(t, 1)
+            flip_and_copy_u(t, 1)
+            val["dgT", t] = work2.tile([P, HALVES, GATES, P, PACK], BF16, name="dgT", align_bytes=64)
+            dg_codes[t] = dg_keep.tile([P, HALVES, GATES, P], U32, name="dg_codes", align_bytes=64)
+            dg_scales[t] = dg_keep.tile([P, HALVES, GATES, P], U8, name="dg_scales", align_bytes=64)
+            if not last:
+                make_r(nc.gpsimd, t + 1)
+                make_rn(nc.gpsimd, t + 1)
+                make_mcn(nc.gpsimd, t + 1)
+                act_o(t + 1)
+                act_i(t + 1)
+                act_f(t + 1)
+                act_f2(t + 1)
+                act_z2(t + 1)
+                regroup_weights(nc.scalar.copy, t + 1, W_SHARES[2])
+                products(t, {n: (lambda: pe_fill(2)) for n in PE_SLOTS})
+                if t + 2 < TOK_TILES:
+                    load_inputs(t + 2, ("grad", "c_t", "z", "n_prev", "o", "c_prev", "i", "f"))
+                if t + 2 < GATES:
+                    load_weight_pass(HALVES * (t + 2))
+                    load_weight_pass(HALVES * (t + 2) + 1)
+            else:
+                def after_first_half():
+                    quantise_half(t, 0)
+                    push(t, range(GATES), (0,))
+
+                def finish(s):
+                    quantise_pass(t, 1, s)
+                    multiply(t, s, 1)
+
+                hooks = {n: (lambda: pe_fill(2)) for n in PE_SLOTS}
+                hooks[9] = after_first_half
+                hooks[12] = lambda: (pe_fill(100), finish(PLACE_I))
+                hooks[13] = lambda: finish(PLACE_O)
+                hooks[14] = lambda: finish(PLACE_F)
+                hooks[15] = lambda: finish(PLACE_Z)
+                products(t, hooks)
+        store(TOK_TILES - 1, nc.vector.tensor_copy)

@@ -28,8 +28,8 @@ N_STARTS = (0, IN - N_MX)
 W_SHARES = ((0, 512), (512, 512), (1024, 512), (1536, 256))
 W_CALLS = ((0, 1024), (1024, 512), (1536, 256))
 W_FRONT = 1024
-PE_START = 5
-PE_SLOTS = (2, 6, 10, 14)
+W_BUFS = 4
+PE_SLOTS = (1, 4, 7)
 
 FLOPS = 2 * B * GATES * H * IN
 BYTES = (GATES + 2) * B * H * 4 + 3 * B * H * 2 + GATES * H * IN * 2 + H * 2 + B * IN * 4
@@ -47,18 +47,19 @@ def tile_slstmcell_t_v_kernel(
     with ExitStack() as ctx:
         ctx.enter_context(tc.manual_schedule())
         const = ctx.enter_context(tc.tile_pool(name="const", bufs=1))
-        w_stage = ctx.enter_context(tc.tile_pool(name="w_stage", bufs=4))
+        w_stage = ctx.enter_context(tc.tile_pool(name="w_stage", bufs=W_BUFS))
         w_group = ctx.enter_context(tc.tile_pool(name="w_group", bufs=1))
         w_keep = ctx.enter_context(tc.tile_pool(name="w_keep", bufs=1))
         norm = ctx.enter_context(tc.tile_pool(name="norm", bufs=1))
         tok_in = ctx.enter_context(tc.tile_pool(name="tok_in", bufs=2))
         tok_once = ctx.enter_context(tc.tile_pool(name="tok_once", bufs=1))
+        tok_three = ctx.enter_context(tc.tile_pool(name="tok_three", bufs=3))
+        spare = ctx.enter_context(tc.tile_pool(name="spare", bufs=4))
         work = ctx.enter_context(tc.tile_pool(name="work", bufs=1))
         work2 = ctx.enter_context(tc.tile_pool(name="work2", bufs=2))
         feat = ctx.enter_context(tc.tile_pool(name="feat", bufs=1))
         stats = ctx.enter_context(tc.tile_pool(name="stats", bufs=2))
-        dg_keep = ctx.enter_context(tc.tile_pool(name="dg_keep", bufs=TOK_TILES))
-        out_stage = ctx.enter_context(tc.tile_pool(name="out_stage", bufs=1))
+        dg_keep = ctx.enter_context(tc.tile_pool(name="dg_keep", bufs=3))
         rot = ctx.enter_context(tc.psum_pool(name="rot", bufs=4))
         psum_acc = ctx.enter_context(tc.psum_pool(name="psum_acc", bufs=2))
 
@@ -122,7 +123,7 @@ def tile_slstmcell_t_v_kernel(
                 if name in gate_row:
                     tile_, source = tok_in.tile([P, H], F32, name="gate_" + name), gates[gate_row[name], rows, :]
                 elif name == "c_t":
-                    tile_, source = tok_in.tile([P, H], F32, name="cell"), c_t[rows, :]
+                    tile_, source = tok_three.tile([P, H], F32, name="cell"), c_t[rows, :]
                 elif name == "q":
                     tile_, source = norm.tile([P, H], F32, name="log_n", tag="slot%d" % t), n_t[rows, :]
                 elif name == "grad":
@@ -164,17 +165,17 @@ def tile_slstmcell_t_v_kernel(
             in_place(tok_of[t]["z"], ACT.Tanh, scale=-1.0)
 
         def act_z2(t):
-            val["zsq", t] = work2.tile([P, H], F32, name="z_squared", tag="zsq")
+            val["zsq", t] = spare.tile([P, H], F32, name="z_squared", tag="spare")
             nc.scalar.activation(out=val["zsq", t][:], in_=tok_of[t]["z"][:], func=ACT.Square)
 
         def act_i(t):
             in_place(tok_of[t]["i"], ACT.Exp)
 
         def make_r(eng, t):
-            if t == 0:
-                val["r", t] = work2.tile([P, H], F32, name="r_first", tag="zsq")
+            if t < 2:
+                val["r", t] = spare.tile([P, H], F32, name="r_first", tag="spare")
             else:
-                val["r", t] = norm.tile([P, H], F32, name="r", tag="slot%d" % (t - 1))
+                val["r", t] = norm.tile([P, H], F32, name="r", tag="slot%d" % (t - 2))
             eng.tensor_tensor(out=val["r", t][:], in0=tok_of[t]["c_t"][:], in1=tok_of[t]["q"][:], op=ALU.mult)
 
         def make_rn(eng, t):
@@ -185,67 +186,53 @@ def tile_slstmcell_t_v_kernel(
             eng.tensor_tensor(out=val["mcn", t][:], in0=val["mcn", t][:], in1=tok_of[t]["c_prev"][:], op=ALU.subtract)
 
         def make_dy(t):
-            val["dy", t] = work2.tile([P, H], F32, name="dy")
-            val["sum_dy", t], val["mmdy", t] = column("sum_dy"), column("mmdy")
+            val["dy", t], val["sum_dy", t] = work.tile([P, H], F32, name="dy"), column("sum_dy")
             stt(val["dy", t][:], tok_of[t]["grad"][:], ALU.mult, 1.0, ALU.mult, gamma[:], accum_out=val["sum_dy", t][:])
-            nc.gpsimd.tensor_scalar(
-                out=val["mmdy", t][:], in0=val["sum_dy", t][:], scalar1=-1.0 / H, scalar2=0.0, op0=ALU.mult, op1=ALU.add
-            )
 
         def make_h2(t):
             val["h2", t] = work.tile([P, H], F32, name="h2")
-            val["sum_h2", t], val["mm", t] = column("sum_h2"), column("mm")
+            val["sum_h2", t], val["mm", t], val["sum_sq", t] = column("sum_h2"), column("mm"), column("sum_sq")
             stt(val["h2", t][:], tok_of[t]["o"][:], ALU.add, 1.0, ALU.mult, val["r", t][:], accum_out=val["sum_h2", t][:])
             nc.vector.tensor_scalar_mul(out=val["mm", t][:], in0=val["sum_h2", t][:], scalar1=-1.0 / H)
-
-        def make_dyh(t):
-            junk = work.tile([P, H], F32, name="junk_products", tag="u")
-            val["sum_dyh", t] = column("sum_dyh")
-            stt(junk[:], val["dy", t][:], ALU.mult, 1.0, ALU.mult, val["h2", t][:], accum_out=val["sum_dyh", t][:])
-
-        def act_square(t):
-            junk = feat.tile([P, H], F32, name="junk_squares", tag="uT")
-            val["sum_sq", t] = column("sum_sq")
+            junk = work.tile([P, H], F32, name="junk_squares", tag="u")
             nc.scalar.activation(
                 out=junk[:], in_=val["h2", t][:], func=ACT.Square, bias=val["mm", t][:], accum_out=val["sum_sq", t][:]
             )
 
+        def make_dyh(t):
+            junk = work.tile([P, H], F32, name="junk_products", tag="x")
+            val["sum_dyh", t] = column("sum_dyh")
+            stt(junk[:], val["dy", t][:], ALU.mult, 1.0, ALU.mult, val["h2", t][:], accum_out=val["sum_dyh", t][:])
+
+        def variance(t):
+            val["var_eps", t], val["rstd", t] = column("var_eps"), column("rstd")
+            nc.vector.tensor_scalar(
+                out=val["var_eps", t][:], in0=val["sum_sq", t][:], scalar1=0.25 / H, scalar2=LN_EPS, op0=ALU.mult, op1=ALU.add
+            )
+            nc.gpsimd.tensor_tensor(out=val["rstd", t][:], in0=val["var_eps", t][:], in1=minus_half[:], op=ALU.pow)
+
+        def act_qr(t):
+            nc.scalar.activation(out=tok_of[t]["q"][:], in_=tok_of[t]["q"][:], func=ACT.Identity, scale=val["rstd", t][:])
+
+        def slope_and_offset(t):
+            cov, inv_var, mmdy = column("cov"), column("inv_var"), column("mmdy")
+            val["slope", t], val["offset", t] = column("slope"), column("offset")
+            stt(cov[:], val["sum_dy", t][:], ALU.mult, val["mm", t][:], ALU.add, val["sum_dyh", t][:])
+            nc.vector.reciprocal(out=inv_var[:], in_=val["var_eps", t][:])
+            nc.vector.tensor_scalar_mul(out=mmdy[:], in0=val["sum_dy", t][:], scalar1=-1.0 / H)
+            stt(val["slope", t][:], cov[:], ALU.mult, -0.25 / H, ALU.mult, inv_var[:])
+            stt(val["offset", t][:], val["slope", t][:], ALU.mult, val["mm", t][:], ALU.add, mmdy[:])
+
+        def make_x(t):
+            val["x", t] = work.tile([P, H], F32, name="x")
+            stt(val["x", t][:], val["h2", t][:], ALU.mult, val["slope", t][:], ALU.add, val["dy", t][:])
+
         def half_columns(c):
             return slice(N_MX * c, N_MX * (c + 1))
 
-        def statistics(t):
-            var_eps, inv_var, cov = column("var_eps"), column("inv_var"), column("cov")
-            slope, offset, rstd, r_offset = column("slope"), column("offset"), column("rstd"), column("r_offset")
-            mm = val["mm", t]
-            diag_r = stats.tile([P, P], F32, name="diag_r")
-            diag_s = stats.tile([P, P], F32, name="diag_s")
-            nc.vector.tensor_scalar(
-                out=var_eps[:], in0=val["sum_sq", t][:], scalar1=0.25 / H, scalar2=LN_EPS, op0=ALU.mult, op1=ALU.add
-            )
-            nc.gpsimd.tensor_tensor(out=rstd[:], in0=var_eps[:], in1=minus_half[:], op=ALU.pow)
-            stt(cov[:], val["sum_dy", t][:], ALU.mult, mm[:], ALU.add, val["sum_dyh", t][:])
-            nc.vector.reciprocal(out=inv_var[:], in_=var_eps[:])
-            stt(slope[:], cov[:], ALU.mult, -0.25 / H, ALU.mult, inv_var[:])
-            stt(offset[:], slope[:], ALU.mult, mm[:], ALU.add, val["mmdy", t][:])
-            nc.vector.tensor_scalar_mul(out=diag_r[:], in0=identity[:], scalar1=rstd[:])
-            banks = [rot.tile([P, N_MX], F32, name="dh", tag="bank") for c in range(HALVES)]
-            for c in range(HALVES):
-                nc.tensor.matmul(out=banks[c][:], lhsT=diag_r[:], rhs=val["dy", t][:, half_columns(c)], start=True, stop=False)
-            nc.vector.tensor_scalar(
-                out=diag_s[:], in0=identity[:], scalar1=slope[:], scalar2=rstd[:], op0=ALU.mult, op1=ALU.mult
-            )
-            for c in range(HALVES):
-                nc.tensor.matmul(out=banks[c][:], lhsT=diag_s[:], rhs=val["h2", t][:, half_columns(c)], start=False, stop=True)
-            nc.gpsimd.tensor_tensor(out=r_offset[:], in0=offset[:], in1=rstd[:], op=ALU.mult)
-            val["dh", t], val["r_offset", t] = banks, r_offset
-
-        def make_u(t, c):
-            if c == 0:
-                val["u", t] = work.tile([P, H], F32, name="u")
-            stt(
-                val["u", t][:, half_columns(c)], val["dh", t][c][:], ALU.add, val["r_offset", t][:], ALU.mult,
-                tok_of[t]["q"][:, half_columns(c)],
-            )
+        def make_u(t):
+            val["u", t] = work.tile([P, H], F32, name="u")
+            stt(val["u", t][:], val["x", t][:], ALU.add, val["offset", t][:], ALU.mult, tok_of[t]["q"][:])
 
         def flip(source, c):
             bank = rot.tile([P, PACK, P], F32, name="bank")
@@ -306,7 +293,7 @@ def tile_slstmcell_t_v_kernel(
             passes_done[t] += 1
 
         def store(t, second_copy):
-            result = out_stage.tile([P, IN], F32, name="result")
+            result = w_stage.tile([P, IN], F32, name="result", tag="w_raw")
             nc.scalar.copy(out=result[:, 0:N_MX], in_=acc[t][0][:])
             second_copy(out=result[:, N_MX:IN], in_=acc[t][1][:, 2 * N_MX - IN : N_MX])
             nc.sync.dma_start(out=out[P * t : P * (t + 1), :], in_=result[:])
@@ -371,39 +358,45 @@ def tile_slstmcell_t_v_kernel(
                 else:
                     stt(dgT[:, c, PLACE_Z], bank["zsq", c], ALU.subtract, 1.0, ALU.mult, tile_of["mdciT", c][:])
 
+            for name in ("to", "ct", "i", "tf2"):
+                fill(name, 0)
             order = (
-                ((("to", 0), ("i", 0), ("ct", 0), ("tf2", 0)), ("dc", 0)),
-                ((), ("mdci", 0)),
-                ((("rz", 0),), ("e", 0)),
-                ((("mcn", 0),), ("g", 0)),
-                ((("to", 1),), ("dgi", 0)),
-                ((("zsq", 0),), ("dgo", 0)),
-                ((("i", 1),), ("dgf", 0)),
-                ((("ct", 1),), ("dc", 1)),
-                ((), ("dgz", 0)),
-                ((("tf2", 1),), ("mdci", 1)),
-                ((("rz", 1),), ("e", 1)),
-                ((("mcn", 1),), ("g", 1)),
-                ((), ("dgi", 1)),
-                ((("zsq", 1),), ("dgo", 1)),
-                ((), ("dgf", 1)),
-                ((), ("dgz", 1)),
+                (("dc", 0), ()), (("e", 0), ("rz", 0)), (("mdci", 0), ("mcn", 0)), (("dgo", 0), ("to", 1)),
+                (("g", 0), ("zsq", 0)), (("dgi", 0), ("ct", 1)), (("dgf", 0), ("i", 1)), (("dc", 1), ()),
+                (("dgz", 0), ("tf2", 1)), (("e", 1), ("rz", 1)), (("mdci", 1), ("mcn", 1)), (("dgo", 1), ("zsq", 1)),
+                (("g", 1), ()), (("dgi", 1), ()), (("dgf", 1), ()), (("dgz", 1), ()),
             )
-            for n, (fills, product) in enumerate(order):
-                for name, c in fills:
-                    fill(name, c)
+            for n, (product, next_fill) in enumerate(order):
                 op(*product)
+                if next_fill:
+                    fill(*next_fill)
                 if n in hooks:
                     hooks[n]()
+
+        def gate_activations(t):
+            act_i(t)
+            act_f(t)
+            act_f2(t)
+            act_z(t)
+            act_z2(t)
+
+        def new_gradient_tiles(t):
+            val["dgT", t] = work2.tile([P, HALVES, GATES, P, PACK], BF16, name="dgT", align_bytes=64)
+            dg_codes[t] = dg_keep.tile([P, HALVES, GATES, P], U32, name="dg_codes", align_bytes=64)
+            dg_scales[t] = dg_keep.tile([P, HALVES, GATES, P], U8, name="dg_scales", align_bytes=64)
 
         nc.sync.dma_start(out=gamma_rows[0:1, :], in_=ln_gamma.unsqueeze(0))
         for t in range(TOK_TILES):
             load_inputs(t, ("q",))
         load_weight_pass(0)
-        load_inputs(0, ("c_t", "o", "grad", "z", "n_prev", "c_prev", "i", "f"))
-        load_inputs(1, ("grad", "c_t"))
+        load_inputs(0, ("c_t", "o", "grad"))
+        load_inputs(1, ("c_t",))
+        load_inputs(0, ("n_prev", "c_prev"))
+        load_inputs(1, ("o", "grad"))
+        load_inputs(0, ("z", "i", "f"))
         load_weight_pass(1)
-        load_inputs(1, ("z", "n_prev", "o", "c_prev", "i", "f"))
+        load_inputs(2, ("c_t",))
+        load_inputs(1, ("n_prev", "c_prev", "z", "i", "f"))
         load_weight_pass(2)
         load_weight_pass(3)
 
@@ -411,7 +404,7 @@ def tile_slstmcell_t_v_kernel(
             act_ln(t)
         act_q(0)
         act_o(0)
-        act_z(0)
+        act_q(1)
         for n0 in range(0, H, N_MX):
             spread = rot.tile([P, N_MX], F32, name="gamma_spread", tag="bank")
             nc.tensor.matmul(out=spread[:], lhsT=ones[:], rhs=gamma_rows[:, n0 : n0 + N_MX], start=True, stop=True)
@@ -421,86 +414,110 @@ def tile_slstmcell_t_v_kernel(
         for call in ((0, 512), (512, 256), (768, 128)):
             quantise_weights(0, call)
         make_r(nc.vector, 0)
+        make_dy(0)
+        make_h2(0)
+        act_o(1)
+        make_r(nc.vector, 1)
+        make_dyh(0)
+        variance(0)
+        act_qr(0)
+        act_q(2)
+        make_rn(nc.vector, 0)
+        slope_and_offset(0)
+        make_mcn(nc.vector, 0)
+        make_x(0)
+        regroup_weights(nc.vector.tensor_copy, 0, (896, 128))
+        make_u(0)
+        for c in range(HALVES):
+            flip_and_copy_u(0, c)
+        act_i(0)
+        act_f(0)
+        make_dy(1)
+        regroup_weights(nc.vector.tensor_copy, 0, (1024, 512))
+        make_h2(1)
+        act_f2(0)
+        act_z(0)
+        act_z2(0)
+        regroup_weights(nc.vector.tensor_copy, 0, (1536, 256))
+        make_dyh(1)
+        for call in ((896, 128), (1024, 512), (1536, 256)):
+            quantise_weights(0, call)
+        variance(1)
 
         for t in range(TOK_TILES):
-            last = t == TOK_TILES - 1
-            make_h2(t)
-            act_square(t)
-            if t == 0:
-                make_dy(0)
-            make_dyh(t)
-            pe_fill(PE_START)
-            if t == 0:
-                act_z2(0)
-                act_i(0)
-                make_rn(nc.vector, 0)
-            else:
-                regroup_weights(nc.scalar.copy, t, W_SHARES[0])
-                regroup_weights(nc.scalar.copy, t, W_SHARES[1])
-            statistics(t)
-            if t == 0:
-                make_mcn(nc.vector, 0)
-                regroup_weights(nc.vector.tensor_copy, 0, (896, 128))
-                regroup_weights(nc.vector.tensor_copy, 0, (1024, 512))
-                regroup_weights(nc.vector.tensor_copy, 0, (1536, 256))
-                for call in ((896, 128), (1024, 512), (1536, 256)):
-                    quantise_weights(0, call)
-                act_f(0)
-                act_f2(0)
-            else:
-                for c in range(HALVES):
-                    quantise_half(t - 1, c)
-                regroup_weights(nc.vector.tensor_copy, t, W_SHARES[3])
-                for call in (W_CALLS[1], W_CALLS[2], W_CALLS[0]):
-                    quantise_weights(t, call)
-                for earlier in range(t - 1):
-                    push(earlier, (t,), (0, 1))
-                    if last:
-                        pe_jobs.append(("store", earlier))
-                push(t - 1, range(t + 1), (0, 1))
-                if last:
-                    pe_jobs.append(("store", t - 1))
-            if not last:
-                act_q(t + 1)
-                act_z(t + 1)
-                make_dy(t + 1)
-            make_u(t, 0)
-            flip_and_copy_u(t, 0)
-            make_u(t, 1)
-            flip_and_copy_u(t, 1)
-            val["dgT", t] = work2.tile([P, HALVES, GATES, P, PACK], BF16, name="dgT", align_bytes=64)
-            dg_codes[t] = dg_keep.tile([P, HALVES, GATES, P], U32, name="dg_codes", align_bytes=64)
-            dg_scales[t] = dg_keep.tile([P, HALVES, GATES, P], U8, name="dg_scales", align_bytes=64)
-            if not last:
-                make_r(nc.gpsimd, t + 1)
+            new_gradient_tiles(t)
+            if t + 2 < TOK_TILES:
+                make_r(nc.gpsimd, t + 2)
+            if t + 1 < TOK_TILES:
                 make_rn(nc.gpsimd, t + 1)
                 make_mcn(nc.gpsimd, t + 1)
-                act_o(t + 1)
-                act_i(t + 1)
-                act_f(t + 1)
-                act_f2(t + 1)
-                act_z2(t + 1)
+                act_qr(t + 1)
+                gate_activations(t + 1)
                 regroup_weights(nc.scalar.copy, t + 1, W_SHARES[2])
-                products(t, {n: (lambda: pe_fill(2)) for n in PE_SLOTS})
-                if t + 2 < TOK_TILES:
-                    load_inputs(t + 2, ("grad", "c_t", "z", "n_prev", "o", "c_prev", "i", "f"))
-                if t + 2 < GATES:
-                    load_weight_pass(HALVES * (t + 2))
-                    load_weight_pass(HALVES * (t + 2) + 1)
+                products(t, {})
             else:
                 def after_first_half():
                     quantise_half(t, 0)
                     push(t, range(GATES), (0,))
+                    pe_fill(1)
 
                 def finish(s):
+                    pe_fill(1)
                     quantise_pass(t, 1, s)
                     multiply(t, s, 1)
 
                 hooks = {n: (lambda: pe_fill(2)) for n in PE_SLOTS}
-                hooks[9] = after_first_half
-                hooks[12] = lambda: (pe_fill(100), finish(PLACE_I))
-                hooks[13] = lambda: finish(PLACE_O)
-                hooks[14] = lambda: finish(PLACE_F)
-                hooks[15] = lambda: finish(PLACE_Z)
+                hooks.update({8: after_first_half, 9: lambda: pe_fill(1), 10: lambda: pe_fill(1),
+                              11: lambda: finish(PLACE_O), 13: lambda: finish(PLACE_I),
+                              14: lambda: finish(PLACE_F), 15: lambda: finish(PLACE_Z)})
                 products(t, hooks)
+                break
+            if t + 2 < TOK_TILES:
+                load_inputs(t + 2, ("o", "grad"))
+            if t + 3 < TOK_TILES:
+                load_inputs(t + 3, ("c_t",))
+            if t + 2 < GATES:
+                load_weight_pass(HALVES * (t + 2))
+                load_weight_pass(HALVES * (t + 2) + 1)
+            if t + 2 < TOK_TILES:
+                load_inputs(t + 2, ("n_prev", "c_prev", "z", "i", "f"))
+            pe_fill(100)
+            if t + 2 < TOK_TILES:
+                act_o(t + 2)
+            if t + 3 < TOK_TILES:
+                act_q(t + 3)
+            slope_and_offset(t + 1)
+            if t == 0:
+                regroup_weights(nc.vector.tensor_copy, 1, W_SHARES[0])
+                regroup_weights(nc.vector.tensor_copy, 1, W_SHARES[1])
+            quantise_weights(t + 1, W_CALLS[0])
+            if t + 2 < GATES:
+                regroup_weights(nc.scalar.copy, t + 2, W_SHARES[0])
+            regroup_weights(nc.vector.tensor_copy, t + 1, W_SHARES[3])
+            quantise_weights(t + 1, W_CALLS[1])
+            quantise_weights(t + 1, W_CALLS[2])
+            for earlier in range(t):
+                push(earlier, (t + 1,), (0, 1))
+                if t + 1 == GATES - 1:
+                    pe_jobs.append(("store", earlier))
+            pe_fill(100)
+            make_x(t + 1)
+            quantise_half(t, 0)
+            push(t, range(t + 2), (0,))
+            pe_fill(100)
+            make_u(t + 1)
+            if t + 2 < GATES:
+                regroup_weights(nc.scalar.copy, t + 2, W_SHARES[1])
+            for c in range(HALVES):
+                flip_and_copy_u(t + 1, c)
+            if t + 2 < TOK_TILES:
+                make_dy(t + 2)
+                make_h2(t + 2)
+            quantise_half(t, 1)
+            push(t, range(t + 2), (1,))
+            if t + 1 == GATES - 1:
+                pe_jobs.append(("store", t))
+            if t + 2 < TOK_TILES:
+                make_dyh(t + 2)
+                variance(t + 2)
         store(TOK_TILES - 1, nc.vector.tensor_copy)

@@ -193,6 +193,8 @@ def tile_slstmcell_t_v_kernel(
             val["h2", t] = work.tile([P, H], F32, name="h2")
             val["sum_h2", t], val["mm", t], val["sum_sq", t] = column("sum_h2"), column("mm"), column("sum_sq")
             stt(val["h2", t][:], tok_of[t]["o"][:], ALU.add, 1.0, ALU.mult, val["r", t][:], accum_out=val["sum_h2", t][:])
+
+        def make_squares(t):
             nc.vector.tensor_scalar_mul(out=val["mm", t][:], in0=val["sum_h2", t][:], scalar1=-1.0 / H)
             junk = work.tile([P, H], F32, name="junk_squares", tag="u")
             nc.scalar.activation(
@@ -214,14 +216,22 @@ def tile_slstmcell_t_v_kernel(
         def act_qr(t):
             nc.scalar.activation(out=tok_of[t]["q"][:], in_=tok_of[t]["q"][:], func=ACT.Identity, scale=val["rstd", t][:])
 
-        def slope_and_offset(t):
-            cov, inv_var, mmdy = column("cov"), column("inv_var"), column("mmdy")
-            val["slope", t], val["offset", t] = column("slope"), column("offset")
-            stt(cov[:], val["sum_dy", t][:], ALU.mult, val["mm", t][:], ALU.add, val["sum_dyh", t][:])
-            nc.vector.reciprocal(out=inv_var[:], in_=val["var_eps", t][:])
-            nc.vector.tensor_scalar_mul(out=mmdy[:], in0=val["sum_dy", t][:], scalar1=-1.0 / H)
-            stt(val["slope", t][:], cov[:], ALU.mult, -0.25 / H, ALU.mult, inv_var[:])
-            stt(val["offset", t][:], val["slope", t][:], ALU.mult, val["mm", t][:], ALU.add, mmdy[:])
+        def gpsimd_qr(t):
+            nc.gpsimd.tensor_scalar(
+                out=tok_of[t]["q"][:], in0=tok_of[t]["q"][:], scalar1=val["rstd", t][:], scalar2=0.0, op0=ALU.mult, op1=ALU.add
+            )
+
+        def slope_and_offset(t, step):
+            if step == 0:
+                for name in ("cov", "inv_var", "mmdy", "slope", "offset"):
+                    val[name, t] = column(name)
+                stt(val["cov", t][:], val["sum_dy", t][:], ALU.mult, val["mm", t][:], ALU.add, val["sum_dyh", t][:])
+                nc.vector.reciprocal(out=val["inv_var", t][:], in_=val["var_eps", t][:])
+                nc.vector.tensor_scalar_mul(out=val["mmdy", t][:], in0=val["sum_dy", t][:], scalar1=-1.0 / H)
+            elif step == 1:
+                stt(val["slope", t][:], val["cov", t][:], ALU.mult, -0.25 / H, ALU.mult, val["inv_var", t][:])
+            else:
+                stt(val["offset", t][:], val["slope", t][:], ALU.mult, val["mm", t][:], ALU.add, val["mmdy", t][:])
 
         def make_x(t):
             val["x", t] = work.tile([P, H], F32, name="x")
@@ -322,11 +332,13 @@ def tile_slstmcell_t_v_kernel(
                     s, k = s_jobs.pop(0)
                     regroup_weights(nc.scalar.copy, s, W_SHARES[k])
 
-        def products(t, hooks):
+        banks_of, tiles_of = {}, {}
+
+        def products(t, first, last, hooks):
             tok = tok_of[t]
             dgT = val["dgT", t]
             uT = val["uT", t]
-            bank, tile_of = {}, {}
+            bank, tile_of = banks_of.setdefault(t, {}), tiles_of.setdefault(t, {})
 
             def fill(name, c):
                 if name == "rz":
@@ -358,15 +370,17 @@ def tile_slstmcell_t_v_kernel(
                 else:
                     stt(dgT[:, c, PLACE_Z], bank["zsq", c], ALU.subtract, 1.0, ALU.mult, tile_of["mdciT", c][:])
 
-            for name in ("to", "ct", "i", "tf2"):
-                fill(name, 0)
+            if first == 0:
+                for name in ("to", "ct", "i", "tf2"):
+                    fill(name, 0)
             order = (
                 (("dc", 0), ()), (("e", 0), ("rz", 0)), (("mdci", 0), ("mcn", 0)), (("dgo", 0), ("to", 1)),
                 (("g", 0), ("zsq", 0)), (("dgi", 0), ("ct", 1)), (("dgf", 0), ("i", 1)), (("dc", 1), ()),
                 (("dgz", 0), ("tf2", 1)), (("e", 1), ("rz", 1)), (("mdci", 1), ("mcn", 1)), (("dgo", 1), ("zsq", 1)),
                 (("g", 1), ()), (("dgi", 1), ()), (("dgf", 1), ()), (("dgz", 1), ()),
             )
-            for n, (product, next_fill) in enumerate(order):
+            for n in range(first, last):
+                product, next_fill = order[n]
                 op(*product)
                 if next_fill:
                     fill(*next_fill)
@@ -416,15 +430,18 @@ def tile_slstmcell_t_v_kernel(
         make_r(nc.vector, 0)
         make_dy(0)
         make_h2(0)
-        act_o(1)
         make_r(nc.vector, 1)
+        make_squares(0)
+        act_o(1)
         make_dyh(0)
         variance(0)
         act_qr(0)
         act_q(2)
+        slope_and_offset(0, 0)
         make_rn(nc.vector, 0)
-        slope_and_offset(0)
+        slope_and_offset(0, 1)
         make_mcn(nc.vector, 0)
+        slope_and_offset(0, 2)
         make_x(0)
         regroup_weights(nc.vector.tensor_copy, 0, (896, 128))
         make_u(0)
@@ -435,26 +452,30 @@ def tile_slstmcell_t_v_kernel(
         make_dy(1)
         regroup_weights(nc.vector.tensor_copy, 0, (1024, 512))
         make_h2(1)
+        regroup_weights(nc.vector.tensor_copy, 0, (1536, 256))
+        make_squares(1)
         act_f2(0)
         act_z(0)
         act_z2(0)
-        regroup_weights(nc.vector.tensor_copy, 0, (1536, 256))
+        new_gradient_tiles(0)
+        products(0, 0, 1, {})
         make_dyh(1)
         for call in ((896, 128), (1024, 512), (1536, 256)):
             quantise_weights(0, call)
         variance(1)
 
         for t in range(TOK_TILES):
-            new_gradient_tiles(t)
+            if t + 1 < TOK_TILES:
+                gpsimd_qr(t + 1)
             if t + 2 < TOK_TILES:
                 make_r(nc.gpsimd, t + 2)
             if t + 1 < TOK_TILES:
                 make_rn(nc.gpsimd, t + 1)
                 make_mcn(nc.gpsimd, t + 1)
-                act_qr(t + 1)
                 gate_activations(t + 1)
                 regroup_weights(nc.scalar.copy, t + 1, W_SHARES[2])
-                products(t, {})
+                regroup_weights(nc.scalar.copy, t + 1, W_SHARES[3])
+                products(t, 1, 16, {})
             else:
                 def after_first_half():
                     quantise_half(t, 0)
@@ -470,7 +491,7 @@ def tile_slstmcell_t_v_kernel(
                 hooks.update({8: after_first_half, 9: lambda: pe_fill(1), 10: lambda: pe_fill(1),
                               11: lambda: finish(PLACE_O), 13: lambda: finish(PLACE_I),
                               14: lambda: finish(PLACE_F), 15: lambda: finish(PLACE_Z)})
-                products(t, hooks)
+                products(t, 1, 16, hooks)
                 break
             if t + 2 < TOK_TILES:
                 load_inputs(t + 2, ("o", "grad"))
@@ -486,15 +507,16 @@ def tile_slstmcell_t_v_kernel(
                 act_o(t + 2)
             if t + 3 < TOK_TILES:
                 act_q(t + 3)
-            slope_and_offset(t + 1)
+            slope_and_offset(t + 1, 0)
             if t == 0:
                 regroup_weights(nc.vector.tensor_copy, 1, W_SHARES[0])
                 regroup_weights(nc.vector.tensor_copy, 1, W_SHARES[1])
             quantise_weights(t + 1, W_CALLS[0])
             if t + 2 < GATES:
                 regroup_weights(nc.scalar.copy, t + 2, W_SHARES[0])
-            regroup_weights(nc.vector.tensor_copy, t + 1, W_SHARES[3])
+            slope_and_offset(t + 1, 1)
             quantise_weights(t + 1, W_CALLS[1])
+            slope_and_offset(t + 1, 2)
             quantise_weights(t + 1, W_CALLS[2])
             for earlier in range(t):
                 push(earlier, (t + 1,), (0, 1))
@@ -517,6 +539,10 @@ def tile_slstmcell_t_v_kernel(
             push(t, range(t + 2), (1,))
             if t + 1 == GATES - 1:
                 pe_jobs.append(("store", t))
+            if t + 2 < TOK_TILES:
+                make_squares(t + 2)
+            new_gradient_tiles(t + 1)
+            products(t + 1, 0, 1, {})
             if t + 2 < TOK_TILES:
                 make_dyh(t + 2)
                 variance(t + 2)

@@ -404,11 +404,11 @@ def tile_slstmcell_t_v_kernel(
             load_inputs(t, ("q",))
         load_weight_pass(0)
         load_inputs(0, ("c_t", "o", "grad"))
+        load_weight_pass(1)
         load_inputs(1, ("c_t",))
         load_inputs(0, ("n_prev", "c_prev"))
         load_inputs(1, ("o", "grad"))
         load_inputs(0, ("z", "i", "f"))
-        load_weight_pass(1)
         load_inputs(2, ("c_t",))
         load_inputs(1, ("n_prev", "c_prev", "z", "i", "f"))
         load_weight_pass(2)
@@ -419,6 +419,8 @@ def tile_slstmcell_t_v_kernel(
         act_q(0)
         act_o(0)
         act_q(1)
+        regroup_weights(nc.scalar.copy, 0, (896, 128))
+        regroup_weights(nc.scalar.copy, 0, (1024, 512))
         for n0 in range(0, H, N_MX):
             spread = rot.tile([P, N_MX], F32, name="gamma_spread", tag="bank")
             nc.tensor.matmul(out=spread[:], lhsT=ones[:], rhs=gamma_rows[:, n0 : n0 + N_MX], start=True, stop=True)
@@ -437,31 +439,30 @@ def tile_slstmcell_t_v_kernel(
         variance(0)
         act_qr(0)
         act_q(2)
+        act_i(0)
+        act_z(0)
         slope_and_offset(0, 0)
         make_rn(nc.vector, 0)
         slope_and_offset(0, 1)
         make_mcn(nc.vector, 0)
         slope_and_offset(0, 2)
         make_x(0)
-        regroup_weights(nc.vector.tensor_copy, 0, (896, 128))
+        quantise_weights(0, (896, 128))
         make_u(0)
         for c in range(HALVES):
             flip_and_copy_u(0, c)
-        act_i(0)
         act_f(0)
         make_dy(1)
-        regroup_weights(nc.vector.tensor_copy, 0, (1024, 512))
-        make_h2(1)
         regroup_weights(nc.vector.tensor_copy, 0, (1536, 256))
+        make_h2(1)
+        quantise_weights(0, (1024, 512))
         make_squares(1)
         act_f2(0)
-        act_z(0)
         act_z2(0)
         new_gradient_tiles(0)
         products(0, 0, 1, {})
         make_dyh(1)
-        for call in ((896, 128), (1024, 512), (1536, 256)):
-            quantise_weights(0, call)
+        quantise_weights(0, (1536, 256))
         variance(1)
 
         for t in range(TOK_TILES):

@@ -30,6 +30,9 @@ W_CALLS = ((0, 1024), (1024, 512), (1536, 256))
 W_FRONT = 1024
 W_BUFS = 4
 PE_SLOTS = (1, 4, 7)
+ACC_SLOTS = ((6, 7), (4, 5), (6, 7), (4, 5))
+U_SLOTS = ((4, 5), (4, 5), (2, 3), (2, 3))
+SIX_BANKS = (0, 1)
 
 FLOPS = 2 * B * GATES * H * IN
 BYTES = (GATES + 2) * B * H * 4 + 3 * B * H * 2 + GATES * H * IN * 2 + H * 2 + B * IN * 4
@@ -60,8 +63,7 @@ def tile_slstmcell_t_v_kernel(
         feat = ctx.enter_context(tc.tile_pool(name="feat", bufs=1))
         stats = ctx.enter_context(tc.tile_pool(name="stats", bufs=2))
         dg_keep = ctx.enter_context(tc.tile_pool(name="dg_keep", bufs=3))
-        rot = ctx.enter_context(tc.psum_pool(name="rot", bufs=4))
-        psum_acc = ctx.enter_context(tc.psum_pool(name="psum_acc", bufs=2))
+        psum = ctx.enter_context(tc.psum_pool(name="psum", bufs=1))
 
         minus_half = const.tile([P, 1], F32, name="minus_half")
         nc.vector.memset(minus_half[:], -0.5)
@@ -237,22 +239,22 @@ def tile_slstmcell_t_v_kernel(
             val["x", t] = work.tile([P, H], F32, name="x")
             stt(val["x", t][:], val["h2", t][:], ALU.mult, val["slope", t][:], ALU.add, val["dy", t][:])
 
-        def half_columns(c):
-            return slice(N_MX * c, N_MX * (c + 1))
-
         def make_u(t):
             val["u", t] = work.tile([P, H], F32, name="u")
             stt(val["u", t][:], val["x", t][:], ALU.add, val["offset", t][:], ALU.mult, tok_of[t]["q"][:])
 
-        def flip(source, c):
-            bank = rot.tile([P, PACK, P], F32, name="bank")
+        def new_bank(slot):
+            return psum.tile([P, PACK, P], F32, name="bank", tag="bank%d" % slot)
+
+        def flip(source, c, slot):
+            bank = new_bank(slot)
             for j in range(PACK):
                 first = (PACK * c + j) * P
                 nc.tensor.transpose(bank[:, j, :], source[:, first : first + P], identity[:])
             return bank[:].rearrange("p j k -> p k j")
 
-        def flip_sum(first_source, second_source, c):
-            bank = rot.tile([P, PACK, P], F32, name="bank")
+        def flip_sum(first_source, second_source, c, slot):
+            bank = new_bank(slot)
             for j in range(PACK):
                 columns = slice((PACK * c + j) * P, (PACK * c + j + 1) * P)
                 nc.tensor.matmul(
@@ -266,7 +268,7 @@ def tile_slstmcell_t_v_kernel(
         def flip_and_copy_u(t, c):
             if c == 0:
                 val["uT", t] = feat.tile([P, HALVES, P, PACK], F32, name="uT")
-            nc.scalar.copy(out=val["uT", t][:, c], in_=flip(val["u", t], c))
+            nc.scalar.copy(out=val["uT", t][:, c], in_=flip(val["u", t], c, U_SLOTS[t][c]))
 
         dg_codes, dg_scales = {}, {}
         acc = {}
@@ -288,7 +290,7 @@ def tile_slstmcell_t_v_kernel(
 
         def multiply(t, s, c):
             if t not in acc:
-                acc[t] = [psum_acc.tile([P, N_MX], F32, name="acc_low"), psum_acc.tile([P, N_MX], F32, name="acc_high")]
+                acc[t] = [psum.tile([P, N_MX], F32, name="acc", tag="bank%d" % slot) for slot in ACC_SLOTS[t]]
                 passes_done[t] = 0
             for side, n0 in enumerate(N_STARTS):
                 nc.tensor.matmul_mx(
@@ -332,58 +334,81 @@ def tile_slstmcell_t_v_kernel(
                     s, k = s_jobs.pop(0)
                     regroup_weights(nc.scalar.copy, s, W_SHARES[k])
 
+        ORDER = (
+            ("dc", 0), ("e", 0), ("mdci", 0), ("dgo", 0), ("g", 0), ("dgi", 0), ("dgf", 0), ("dc", 1),
+            ("dgz", 0), ("e", 1), ("mdci", 1), ("dgo", 1), ("g", 1), ("dgi", 1), ("dgf", 1), ("dgz", 1),
+        )
+        FILLS = (
+            ("to", 0), ("ct", 0), ("i", 0), ("tf2", 0), ("rz", 0), ("mcn", 0), ("to", 1),
+            ("zsq", 0), ("ct", 1), ("i", 1), ("tf2", 1), ("rz", 1), ("mcn", 1), ("zsq", 1),
+        )
+        LAST_READER = {
+            "to": "dgo", "ct": "e", "i": "mdci", "tf2": "g", "rz": "dgi", "mcn": "dgf", "zsq": "dgz",
+        }
+
+        def bank_plan(banks):
+            fill_slot, fills_after, free_at = [], {}, [(-1, slot) for slot in range(banks)]
+            for name, c in FILLS:
+                free_at.sort()
+                after, slot = free_at.pop(0)
+                fills_after.setdefault(after, []).append(len(fill_slot))
+                fill_slot.append(slot)
+                free_at.append((ORDER.index((LAST_READER[name], c)), slot))
+            return fill_slot, fills_after
+
+        PLANS = {t: bank_plan(6 if t in SIX_BANKS else 4) for t in range(TOK_TILES)}
         banks_of, tiles_of = {}, {}
 
-        def products(t, first, last, hooks):
+        def fill(t, k):
             tok = tok_of[t]
-            dgT = val["dgT", t]
-            uT = val["uT", t]
-            bank, tile_of = banks_of.setdefault(t, {}), tiles_of.setdefault(t, {})
+            name, c = FILLS[k]
+            slot = PLANS[t][0][k]
+            if name == "rz":
+                banks_of[t, name, c] = flip_sum(val["r", t], tok["z"], c, slot)
+            else:
+                source = {"to": tok["o"], "i": tok["i"], "ct": tok["c_t"], "tf2": tok["f"], "mcn": val["mcn", t],
+                          "zsq": val["zsq", t]}[name]
+                banks_of[t, name, c] = flip(source, c, slot)
 
-            def fill(name, c):
-                if name == "rz":
-                    bank[name, c] = flip_sum(val["r", t], tok["z"], c)
-                else:
-                    source = {"to": tok["o"], "i": tok["i"], "ct": tok["c_t"], "tf2": tok["f"], "mcn": val["mcn", t],
-                              "zsq": val["zsq", t]}[name]
-                    bank[name, c] = flip(source, c)
+        def product(t, name, c):
+            dgT, uT = val["dgT", t], val["uT", t]
 
-            def chain(name, c):
-                tile_of[name, c] = feat.tile([P, P, PACK], F32, name=name)
-                return tile_of[name, c][:]
+            def bank(which):
+                return banks_of[t, which, c]
 
-            def op(name, c):
-                if name == "dc":
-                    stt(chain("dcT", c), bank["to", c], ALU.add, 1.0, ALU.mult, uT[:, c])
-                elif name == "mdci":
-                    stt(chain("mdciT", c), bank["i", c], ALU.mult, -0.5, ALU.mult, tile_of["dcT", c][:])
-                elif name == "e":
-                    stt(chain("eT", c), bank["ct", c], ALU.mult, -0.25, ALU.mult, tile_of["dcT", c][:])
-                elif name == "g":
-                    stt(chain("gT", c), bank["tf2", c], ALU.subtract, 1.0, ALU.mult, tile_of["dcT", c][:])
-                elif name == "dgi":
-                    nc.vector.tensor_tensor(out=dgT[:, c, PLACE_I], in0=bank["rz", c], in1=tile_of["mdciT", c][:], op=ALU.mult)
-                elif name == "dgo":
-                    stt(dgT[:, c, PLACE_O], bank["to", c], ALU.subtract, 1.0, ALU.mult, tile_of["eT", c][:])
-                elif name == "dgf":
-                    stt(dgT[:, c, PLACE_F], bank["mcn", c], ALU.mult, 0.125, ALU.mult, tile_of["gT", c][:])
-                else:
-                    stt(dgT[:, c, PLACE_Z], bank["zsq", c], ALU.subtract, 1.0, ALU.mult, tile_of["mdciT", c][:])
+            def made(which):
+                return tiles_of[which, c][:]
 
+            def chain(which):
+                tiles_of[name, c] = feat.tile([P, P, PACK], F32, name=which)
+                return tiles_of[name, c][:]
+
+            if name == "dc":
+                stt(chain("dcT"), bank("to"), ALU.add, 1.0, ALU.mult, uT[:, c])
+            elif name == "mdci":
+                stt(chain("mdciT"), bank("i"), ALU.mult, -0.5, ALU.mult, made("dc"))
+            elif name == "e":
+                stt(chain("eT"), bank("ct"), ALU.mult, -0.25, ALU.mult, made("dc"))
+            elif name == "g":
+                stt(chain("gT"), bank("tf2"), ALU.subtract, 1.0, ALU.mult, made("dc"))
+            elif name == "dgi":
+                nc.vector.tensor_tensor(out=dgT[:, c, PLACE_I], in0=bank("rz"), in1=made("mdci"), op=ALU.mult)
+            elif name == "dgo":
+                stt(dgT[:, c, PLACE_O], bank("to"), ALU.subtract, 1.0, ALU.mult, made("e"))
+            elif name == "dgf":
+                stt(dgT[:, c, PLACE_F], bank("mcn"), ALU.mult, 0.125, ALU.mult, made("g"))
+            else:
+                stt(dgT[:, c, PLACE_Z], bank("zsq"), ALU.subtract, 1.0, ALU.mult, made("mdci"))
+
+        def products(t, first, last, hooks):
+            fills_after = PLANS[t][1]
             if first == 0:
-                for name in ("to", "ct", "i", "tf2"):
-                    fill(name, 0)
-            order = (
-                (("dc", 0), ()), (("e", 0), ("rz", 0)), (("mdci", 0), ("mcn", 0)), (("dgo", 0), ("to", 1)),
-                (("g", 0), ("zsq", 0)), (("dgi", 0), ("ct", 1)), (("dgf", 0), ("i", 1)), (("dc", 1), ()),
-                (("dgz", 0), ("tf2", 1)), (("e", 1), ("rz", 1)), (("mdci", 1), ("mcn", 1)), (("dgo", 1), ("zsq", 1)),
-                (("g", 1), ()), (("dgi", 1), ()), (("dgf", 1), ()), (("dgz", 1), ()),
-            )
+                for k in fills_after[-1]:
+                    fill(t, k)
             for n in range(first, last):
-                product, next_fill = order[n]
-                op(*product)
-                if next_fill:
-                    fill(*next_fill)
+                product(t, *ORDER[n])
+                for k in fills_after.get(n, ()):
+                    fill(t, k)
                 if n in hooks:
                     hooks[n]()
 
@@ -422,7 +447,7 @@ def tile_slstmcell_t_v_kernel(
         regroup_weights(nc.scalar.copy, 0, (896, 128))
         regroup_weights(nc.scalar.copy, 0, (1024, 512))
         for n0 in range(0, H, N_MX):
-            spread = rot.tile([P, N_MX], F32, name="gamma_spread", tag="bank")
+            spread = psum.tile([P, N_MX], F32, name="gamma_spread", tag="bank%d" % (n0 // N_MX))
             nc.tensor.matmul(out=spread[:], lhsT=ones[:], rhs=gamma_rows[:, n0 : n0 + N_MX], start=True, stop=True)
             nc.vector.tensor_copy(out=gamma[:, n0 : n0 + N_MX], in_=spread[:])
         regroup_weights(nc.vector.tensor_copy, 0, (0, 512))

@@ -188,7 +188,7 @@ def tile_slstmcell_t_v_kernel(
             eng.tensor_tensor(out=val["mcn", t][:], in0=val["mcn", t][:], in1=tok_of[t]["c_prev"][:], op=ALU.subtract)
 
         def make_dy(t):
-            val["dy", t], val["sum_dy", t] = work.tile([P, H], F32, name="dy"), column("sum_dy")
+            val["dy", t], val["sum_dy", t] = work2.tile([P, H], F32, name="dy"), column("sum_dy")
             stt(val["dy", t][:], tok_of[t]["grad"][:], ALU.mult, 1.0, ALU.mult, gamma[:], accum_out=val["sum_dy", t][:])
 
         def make_h2(t):
@@ -208,6 +208,13 @@ def tile_slstmcell_t_v_kernel(
             val["sum_dyh", t] = column("sum_dyh")
             stt(junk[:], val["dy", t][:], ALU.mult, 1.0, ALU.mult, val["h2", t][:], accum_out=val["sum_dyh", t][:])
 
+        def make_cov(t):
+            val["cov", t] = column("cov")
+            nc.gpsimd.tensor_scalar(
+                out=val["cov", t][:], in0=val["sum_dy", t][:], scalar1=val["mm", t][:], scalar2=val["sum_dyh", t][:],
+                op0=ALU.mult, op1=ALU.add,
+            )
+
         def variance(t):
             val["var_eps", t], val["rstd", t] = column("var_eps"), column("rstd")
             nc.vector.tensor_scalar(
@@ -225,9 +232,8 @@ def tile_slstmcell_t_v_kernel(
 
         def slope_and_offset(t, step):
             if step == 0:
-                for name in ("cov", "inv_var", "mmdy", "slope", "offset"):
+                for name in ("inv_var", "mmdy", "slope", "offset"):
                     val[name, t] = column(name)
-                stt(val["cov", t][:], val["sum_dy", t][:], ALU.mult, val["mm", t][:], ALU.add, val["sum_dyh", t][:])
                 nc.vector.reciprocal(out=val["inv_var", t][:], in_=val["var_eps", t][:])
                 nc.vector.tensor_scalar_mul(out=val["mmdy", t][:], in0=val["sum_dy", t][:], scalar1=-1.0 / H)
             elif step == 1:
@@ -424,15 +430,17 @@ def tile_slstmcell_t_v_kernel(
             dg_codes[t] = dg_keep.tile([P, HALVES, GATES, P], U32, name="dg_codes", align_bytes=64)
             dg_scales[t] = dg_keep.tile([P, HALVES, GATES, P], U8, name="dg_scales", align_bytes=64)
 
+        for t in range(2):
+            load_inputs(t, ("grad",))
         nc.sync.dma_start(out=gamma_rows[0:1, :], in_=ln_gamma.unsqueeze(0))
         for t in range(TOK_TILES):
             load_inputs(t, ("q",))
         load_weight_pass(0)
-        load_inputs(0, ("c_t", "o", "grad"))
+        load_inputs(0, ("c_t", "o"))
         load_weight_pass(1)
         load_inputs(1, ("c_t",))
         load_inputs(0, ("n_prev", "c_prev"))
-        load_inputs(1, ("o", "grad"))
+        load_inputs(1, ("o",))
         load_inputs(0, ("z", "i", "f"))
         load_inputs(2, ("c_t",))
         load_inputs(1, ("n_prev", "c_prev", "z", "i", "f"))
@@ -450,26 +458,28 @@ def tile_slstmcell_t_v_kernel(
             spread = psum.tile([P, N_MX], F32, name="gamma_spread", tag="bank%d" % (n0 // N_MX))
             nc.tensor.matmul(out=spread[:], lhsT=ones[:], rhs=gamma_rows[:, n0 : n0 + N_MX], start=True, stop=True)
             nc.vector.tensor_copy(out=gamma[:, n0 : n0 + N_MX], in_=spread[:])
+        make_dy(0)
+        make_dy(1)
         regroup_weights(nc.vector.tensor_copy, 0, (0, 512))
         regroup_weights(nc.vector.tensor_copy, 0, (512, 384))
         for call in ((0, 512), (512, 256), (768, 128)):
             quantise_weights(0, call)
         make_r(nc.vector, 0)
-        make_dy(0)
         make_h2(0)
         make_r(nc.vector, 1)
         make_squares(0)
         act_o(1)
         make_dyh(0)
+        make_cov(0)
+        make_rn(nc.vector, 0)
         variance(0)
         act_qr(0)
         act_q(2)
         act_i(0)
         act_z(0)
         slope_and_offset(0, 0)
-        make_rn(nc.vector, 0)
-        slope_and_offset(0, 1)
         make_mcn(nc.vector, 0)
+        slope_and_offset(0, 1)
         slope_and_offset(0, 2)
         make_x(0)
         quantise_weights(0, (896, 128))
@@ -477,31 +487,31 @@ def tile_slstmcell_t_v_kernel(
         for c in range(HALVES):
             flip_and_copy_u(0, c)
         act_f(0)
-        make_dy(1)
         regroup_weights(nc.vector.tensor_copy, 0, (1536, 256))
         make_h2(1)
         quantise_weights(0, (1024, 512))
         make_squares(1)
+        quantise_weights(0, (1536, 256))
         act_f2(0)
         act_z2(0)
         new_gradient_tiles(0)
-        products(0, 0, 1, {})
         make_dyh(1)
-        quantise_weights(0, (1536, 256))
-        variance(1)
+        make_cov(1)
+        products(0, 0, 1, {})
 
         for t in range(TOK_TILES):
-            if t + 1 < TOK_TILES:
-                gpsimd_qr(t + 1)
             if t + 2 < TOK_TILES:
                 make_r(nc.gpsimd, t + 2)
             if t + 1 < TOK_TILES:
                 make_rn(nc.gpsimd, t + 1)
+                products(t, 1, 3, {})
+                variance(t + 1)
+                gpsimd_qr(t + 1)
                 make_mcn(nc.gpsimd, t + 1)
                 gate_activations(t + 1)
                 regroup_weights(nc.scalar.copy, t + 1, W_SHARES[2])
                 regroup_weights(nc.scalar.copy, t + 1, W_SHARES[3])
-                products(t, 1, 16, {})
+                products(t, 3, 16, {})
             else:
                 def after_first_half():
                     quantise_half(t, 0)
@@ -567,9 +577,8 @@ def tile_slstmcell_t_v_kernel(
                 pe_jobs.append(("store", t))
             if t + 2 < TOK_TILES:
                 make_squares(t + 2)
+                make_dyh(t + 2)
+                make_cov(t + 2)
             new_gradient_tiles(t + 1)
             products(t + 1, 0, 1, {})
-            if t + 2 < TOK_TILES:
-                make_dyh(t + 2)
-                variance(t + 2)
         store(TOK_TILES - 1, nc.vector.tensor_copy)

@@ -27,12 +27,10 @@ N_MX = 512
 N_STARTS = (0, IN - N_MX)
 W_SHARES = ((0, 512), (512, 512), (1024, 512), (1536, 256))
 W_CALLS = ((0, 1024), (1024, 512), (1536, 256))
-W_FRONT = 1024
 W_BUFS = 4
-PE_SLOTS = (1, 4, 7)
-ACC_SLOTS = ((6, 7), (4, 5), (6, 7), (4, 5))
-U_SLOTS = ((4, 5), (4, 5), (2, 3), (2, 3))
-SIX_BANKS = (0, 1)
+FLIP_BANKS = ((0, 1, 2, 3), (0, 1, 2, 3), (0, 1, 2, 3), (0, 1, 4, 5))
+ACC_BANKS = ((6, 7), (4, 5), (2, 3), (6, 7))
+U_BANKS = ((2, 3), (2, 3), (2, 3), (0, 1))
 
 FLOPS = 2 * B * GATES * H * IN
 BYTES = (GATES + 2) * B * H * 4 + 3 * B * H * 2 + GATES * H * IN * 2 + H * 2 + B * IN * 4
@@ -51,7 +49,6 @@ def tile_slstmcell_t_v_kernel(
         ctx.enter_context(tc.manual_schedule())
         const = ctx.enter_context(tc.tile_pool(name="const", bufs=1))
         w_stage = ctx.enter_context(tc.tile_pool(name="w_stage", bufs=W_BUFS))
-        w_group = ctx.enter_context(tc.tile_pool(name="w_group", bufs=1))
         w_keep = ctx.enter_context(tc.tile_pool(name="w_keep", bufs=1))
         norm = ctx.enter_context(tc.tile_pool(name="norm", bufs=1))
         tok_in = ctx.enter_context(tc.tile_pool(name="tok_in", bufs=2))
@@ -59,6 +56,7 @@ def tile_slstmcell_t_v_kernel(
         tok_three = ctx.enter_context(tc.tile_pool(name="tok_three", bufs=3))
         spare = ctx.enter_context(tc.tile_pool(name="spare", bufs=4))
         work = ctx.enter_context(tc.tile_pool(name="work", bufs=1))
+        dy_keep = ctx.enter_context(tc.tile_pool(name="dy_keep", bufs=1))
         work2 = ctx.enter_context(tc.tile_pool(name="work2", bufs=2))
         feat = ctx.enter_context(tc.tile_pool(name="feat", bufs=1))
         stats = ctx.enter_context(tc.tile_pool(name="stats", bufs=2))
@@ -69,7 +67,6 @@ def tile_slstmcell_t_v_kernel(
         nc.vector.memset(minus_half[:], -0.5)
         gamma_rows = const.tile([P, H], BF16, name="gamma_rows")
         ones = const.tile([P, P], BF16, name="ones")
-        gamma = const.tile([P, H], BF16, name="gamma")
         nc.vector.memset(gamma_rows[:], 0.0)
         nc.vector.memset(ones[:], 1.0)
         identity = const.tile([P, P], F32, name="identity")
@@ -78,7 +75,6 @@ def tile_slstmcell_t_v_kernel(
         w_codes = w_keep.tile([P, PASSES, IN], U32, name="w_codes", align_bytes=64)
         w_scales = w_keep.tile([P, PASSES, IN], U8, name="w_scales", align_bytes=64)
         w_raw = {}
-        w_front, w_back = {}, {}
 
         def load_weight_pass(c):
             weight = weight_at[c // HALVES]
@@ -87,13 +83,7 @@ def tile_slstmcell_t_v_kernel(
             rows = weight[first_row : first_row + K_PASS, 0:IN]
             nc.sync.dma_start(out=w_raw[c][:], in_=rows.rearrange("(j p) n -> p j n", p=P))
 
-        def grouped_columns(s, first, width):
-            if s not in w_front:
-                w_front[s] = w_group.tile([P, W_FRONT, PACK], BF16, name="w_front", align_bytes=64)
-                w_back[s] = w_group.tile([P, HALVES * IN - W_FRONT, PACK], BF16, name="w_back", align_bytes=64)
-            if first < W_FRONT:
-                return w_front[s][:, first : first + width, :]
-            return w_back[s][:, first - W_FRONT : first - W_FRONT + width, :]
+        w_grouped = w_keep.tile([P, HALVES * IN, PACK], BF16, name="w_grouped", align_bytes=64)
 
         def regroup_weights(copy, s, share):
             first, width = share
@@ -101,7 +91,7 @@ def tile_slstmcell_t_v_kernel(
                 low, high = max(first, IN * c), min(first + width, IN * (c + 1))
                 if low < high:
                     copy(
-                        out=grouped_columns(s, low, high - low).rearrange("p (c i) v -> p c v i", i=4),
+                        out=w_grouped[:, low:high, :].rearrange("p (c i) v -> p c v i", i=4),
                         in_=w_raw[HALVES * s + c][:, :, low - IN * c : high - IN * c].rearrange(
                             "p v (c i) -> p c v i", i=4
                         ),
@@ -113,7 +103,7 @@ def tile_slstmcell_t_v_kernel(
             nc.vector.quantize_mx(
                 out=w_codes[:, passes, :].rearrange("p c n -> p (c n)")[:, first : first + width].bitcast(E4M3X4),
                 scales=w_scales[:, passes, :].rearrange("p c n -> p (c n)")[:, first : first + width],
-                in_=grouped_columns(s, first, width).rearrange("p n v -> p (n v)"),
+                in_=w_grouped[:, first : first + width, :].rearrange("p n v -> p (n v)"),
             )
 
         tok_of = {t: {} for t in range(TOK_TILES)}
@@ -128,8 +118,6 @@ def tile_slstmcell_t_v_kernel(
                     tile_, source = tok_three.tile([P, H], F32, name="cell"), c_t[rows, :]
                 elif name == "q":
                     tile_, source = norm.tile([P, H], F32, name="log_n", tag="slot%d" % t), n_t[rows, :]
-                elif name == "grad":
-                    tile_, source = tok_in.tile([P, H], BF16, name="grad"), grad_out[rows, :]
                 elif name == "n_prev":
                     tile_, source = tok_once.tile([P, H], BF16, name="n_before"), n_prev[rows, :]
                 else:
@@ -181,76 +169,106 @@ def tile_slstmcell_t_v_kernel(
             eng.tensor_tensor(out=val["r", t][:], in0=tok_of[t]["c_t"][:], in1=tok_of[t]["q"][:], op=ALU.mult)
 
         def make_rn(eng, t):
-            val["mcn", t] = work2.tile([P, H], F32, name="mcn")
+            val["mcn", t] = work2.tile([P, H], F32, name="mcn", tag="mcn")
             eng.tensor_tensor(out=val["mcn", t][:], in0=val["r", t][:], in1=tok_of[t]["n_prev"][:], op=ALU.mult)
 
         def make_mcn(eng, t):
             eng.tensor_tensor(out=val["mcn", t][:], in0=val["mcn", t][:], in1=tok_of[t]["c_prev"][:], op=ALU.subtract)
 
+        def load_gradients(first):
+            pair = w_stage.tile([P, 2, H], BF16, name="grad_pair", tag="w_raw")
+            rows = grad_out[P * first : P * (first + 2), :]
+            nc.sync.dma_start(out=pair[:], in_=rows.rearrange("(j p) n -> p j n", p=P))
+            for t in range(2):
+                tok_of[first + t]["grad"] = pair[:, t, :]
+
         def make_dy(t):
-            val["dy", t], val["sum_dy", t] = work2.tile([P, H], F32, name="dy"), column("sum_dy")
-            stt(val["dy", t][:], tok_of[t]["grad"][:], ALU.mult, 1.0, ALU.mult, gamma[:], accum_out=val["sum_dy", t][:])
+            val["dy", t] = dy_keep.tile([P, H], F32, name="dy", tag="dy%d" % t)
+            for c in range(HALVES):
+                half = slice(N_MX * c, N_MX * (c + 1))
+                nc.vector.tensor_tensor(
+                    out=val["dy", t][:, half], in0=tok_of[t]["grad"][:, half], in1=gamma[c][:], op=ALU.mult
+                )
 
         def make_h2(t):
-            val["h2", t] = work.tile([P, H], F32, name="h2")
-            val["sum_h2", t], val["mm", t], val["sum_sq", t] = column("sum_h2"), column("mm"), column("sum_sq")
+            val["h2", t], val["sum_h2", t] = work2.tile([P, H], F32, name="h2"), column("sum_h2")
             stt(val["h2", t][:], tok_of[t]["o"][:], ALU.add, 1.0, ALU.mult, val["r", t][:], accum_out=val["sum_h2", t][:])
 
-        def make_squares(t):
+        def make_mm(t):
+            val["mm", t] = column("mm")
             nc.vector.tensor_scalar_mul(out=val["mm", t][:], in0=val["sum_h2", t][:], scalar1=-1.0 / H)
-            junk = work.tile([P, H], F32, name="junk_squares", tag="u")
+
+        def make_squares(t):
+            junk, val["sum_sq", t] = work.tile([P, H], BF16, name="junk_squares"), column("sum_sq")
             nc.scalar.activation(
                 out=junk[:], in_=val["h2", t][:], func=ACT.Square, bias=val["mm", t][:], accum_out=val["sum_sq", t][:]
             )
 
-        def make_dyh(t):
-            junk = work.tile([P, H], F32, name="junk_products", tag="x")
-            val["sum_dyh", t] = column("sum_dyh")
-            stt(junk[:], val["dy", t][:], ALU.mult, 1.0, ALU.mult, val["h2", t][:], accum_out=val["sum_dyh", t][:])
-
         def make_cov(t):
-            val["cov", t] = column("cov")
+            junk, val["cov", t], val["ncov", t] = work.tile([P, H], BF16, name="junk_products"), column("cov"), column("ncov")
+            stt(junk[:], val["h2", t][:], ALU.add, val["mm", t][:], ALU.mult, val["dy", t][:], accum_out=val["cov", t][:])
             nc.gpsimd.tensor_scalar(
-                out=val["cov", t][:], in0=val["sum_dy", t][:], scalar1=val["mm", t][:], scalar2=val["sum_dyh", t][:],
-                op0=ALU.mult, op1=ALU.add,
+                out=val["ncov", t][:], in0=val["cov", t][:], scalar1=-0.25 / H, scalar2=0.0, op0=ALU.mult, op1=ALU.add
             )
 
         def variance(t):
-            val["var_eps", t], val["rstd", t] = column("var_eps"), column("rstd")
+            val["var_eps", t], val["inv_var", t], val["rstd", t] = column("var_eps"), column("inv_var"), column("rstd")
             nc.vector.tensor_scalar(
                 out=val["var_eps", t][:], in0=val["sum_sq", t][:], scalar1=0.25 / H, scalar2=LN_EPS, op0=ALU.mult, op1=ALU.add
             )
+            nc.vector.reciprocal(out=val["inv_var", t][:], in_=val["var_eps", t][:])
             nc.gpsimd.tensor_tensor(out=val["rstd", t][:], in0=val["var_eps", t][:], in1=minus_half[:], op=ALU.pow)
 
-        def act_qr(t):
-            nc.scalar.activation(out=tok_of[t]["q"][:], in_=tok_of[t]["q"][:], func=ACT.Identity, scale=val["rstd", t][:])
+        def make_qr(eng, t):
+            q = tok_of[t]["q"]
+            eng.tensor_scalar(out=q[:], in0=q[:], scalar1=val["rstd", t][:], scalar2=0.0, op0=ALU.mult, op1=ALU.add)
 
-        def gpsimd_qr(t):
-            nc.gpsimd.tensor_scalar(
-                out=tok_of[t]["q"][:], in0=tok_of[t]["q"][:], scalar1=val["rstd", t][:], scalar2=0.0, op0=ALU.mult, op1=ALU.add
-            )
-
-        def slope_and_offset(t, step):
-            if step == 0:
-                for name in ("inv_var", "mmdy", "slope", "offset"):
-                    val[name, t] = column(name)
-                nc.vector.reciprocal(out=val["inv_var", t][:], in_=val["var_eps", t][:])
-                nc.vector.tensor_scalar_mul(out=val["mmdy", t][:], in0=val["sum_dy", t][:], scalar1=-1.0 / H)
-            elif step == 1:
-                stt(val["slope", t][:], val["cov", t][:], ALU.mult, -0.25 / H, ALU.mult, val["inv_var", t][:])
-            else:
-                stt(val["offset", t][:], val["slope", t][:], ALU.mult, val["mm", t][:], ALU.add, val["mmdy", t][:])
+        def make_slope(t):
+            val["slope", t] = column("slope")
+            nc.vector.tensor_scalar_mul(out=val["slope", t][:], in0=val["ncov", t][:], scalar1=val["inv_var", t][:])
 
         def make_x(t):
-            val["x", t] = work.tile([P, H], F32, name="x")
-            stt(val["x", t][:], val["h2", t][:], ALU.mult, val["slope", t][:], ALU.add, val["dy", t][:])
+            dy, val["sum_x", t] = val["dy", t], column("sum_x")
+            stt(dy[:], val["h2", t][:], ALU.mult, val["slope", t][:], ALU.add, dy[:], accum_out=val["sum_x", t][:])
+
+        def make_offset(t):
+            val["offset", t] = column("offset")
+            nc.vector.tensor_scalar_mul(out=val["offset", t][:], in0=val["sum_x", t][:], scalar1=-1.0 / H)
 
         def make_u(t):
-            val["u", t] = work.tile([P, H], F32, name="u")
-            stt(val["u", t][:], val["x", t][:], ALU.add, val["offset", t][:], ALU.mult, tok_of[t]["q"][:])
+            val["u", t] = val["dy", t]
+            stt(val["u", t][:], val["u", t][:], ALU.add, val["offset", t][:], ALU.mult, tok_of[t]["q"][:])
+
+        def make_dc(t):
+            stt(val["u", t][:], tok_of[t]["o"][:], ALU.add, 2.0, ALU.mult, val["u", t][:])
+
+        def act_o_less_1(t):
+            nc.scalar.activation(out=tok_of[t]["o"][:], in_=tok_of[t]["o"][:], func=ACT.Identity, bias=-1.0)
+
+        def make_rz(t):
+            nc.gpsimd.tensor_tensor(out=val["r", t][:], in0=val["r", t][:], in1=tok_of[t]["z"][:], op=ALU.add)
+
+        def gpsimd_products_o(t):
+            val["dgo"] = work2.tile([P, H], F32, name="dgo", tag="mcn")
+            nc.gpsimd.tensor_tensor(out=val["dgo"][:], in0=val["u", t][:], in1=tok_of[t]["c_t"][:], op=ALU.mult)
+            nc.gpsimd.tensor_tensor(out=val["dgo"][:], in0=val["dgo"][:], in1=tok_of[t]["o"][:], op=ALU.mult)
 
         def new_bank(slot):
             return psum.tile([P, PACK, P], F32, name="bank", tag="bank%d" % slot)
+
+        def make_rz(t):
+            nc.gpsimd.tensor_tensor(out=val["r", t][:], in0=val["r", t][:], in1=tok_of[t]["z"][:], op=ALU.add)
+
+        def make_dc(t):
+            stt(val["u", t][:], tok_of[t]["o"][:], ALU.add, 2.0, ALU.mult, val["u", t][:])
+
+        def act_o_less_1(t):
+            nc.scalar.activation(out=tok_of[t]["o"][:], in_=tok_of[t]["o"][:], func=ACT.Identity, bias=-1.0)
+
+        def gpsimd_products_o(t):
+            val["dgo"] = work2.tile([P, H], F32, name="dgo", tag="mcn")
+            nc.gpsimd.tensor_tensor(out=val["dgo"][:], in0=val["u", t][:], in1=tok_of[t]["c_t"][:], op=ALU.mult)
+            nc.gpsimd.tensor_tensor(out=val["dgo"][:], in0=val["dgo"][:], in1=tok_of[t]["o"][:], op=ALU.mult)
 
         def flip(source, c, slot):
             bank = new_bank(slot)
@@ -274,7 +292,7 @@ def tile_slstmcell_t_v_kernel(
         def flip_and_copy_u(t, c):
             if c == 0:
                 val["uT", t] = feat.tile([P, HALVES, P, PACK], F32, name="uT")
-            nc.scalar.copy(out=val["uT", t][:, c], in_=flip(val["u", t], c, U_SLOTS[t][c]))
+            nc.scalar.copy(out=val["uT", t][:, c], in_=flip(val["u", t], c, U_BANKS[t][c]))
 
         dg_codes, dg_scales = {}, {}
         acc = {}
@@ -296,7 +314,7 @@ def tile_slstmcell_t_v_kernel(
 
         def multiply(t, s, c):
             if t not in acc:
-                acc[t] = [psum.tile([P, N_MX], F32, name="acc", tag="bank%d" % slot) for slot in ACC_SLOTS[t]]
+                acc[t] = [psum.tile([P, N_MX], F32, name="acc", tag="bank%d" % slot) for slot in ACC_BANKS[t]]
                 passes_done[t] = 0
             for side, n0 in enumerate(N_STARTS):
                 nc.tensor.matmul_mx(
@@ -348,32 +366,39 @@ def tile_slstmcell_t_v_kernel(
             ("to", 0), ("ct", 0), ("i", 0), ("tf2", 0), ("rz", 0), ("mcn", 0), ("to", 1),
             ("zsq", 0), ("ct", 1), ("i", 1), ("tf2", 1), ("rz", 1), ("mcn", 1), ("zsq", 1),
         )
-        LAST_READER = {
+        LAST_ORDER = tuple((name, c) for c in range(HALVES) for name in ("mdci", "g", "dgi", "dgf", "dgz"))
+        LAST_FILLS = (("i", 0), ("tf2", 0), ("rz", 0), ("mcn", 0), ("zsq", 0), ("i", 1), ("dgo", 0), ("dgo", 1), ("tf2", 1), ("rz", 1), ("mcn", 1), ("zsq", 1))
+        READER = {
             "to": "dgo", "ct": "e", "i": "mdci", "tf2": "g", "rz": "dgi", "mcn": "dgf", "zsq": "dgz",
         }
 
-        def bank_plan(banks):
-            fill_slot, fills_after, free_at = [], {}, [(-1, slot) for slot in range(banks)]
-            for name, c in FILLS:
+        def bank_plan(order, fills, banks):
+            fill_slot, fills_after, free_at = [], {}, [(-1, slot) for slot in banks]
+            for name, c in fills:
                 free_at.sort()
                 after, slot = free_at.pop(0)
                 fills_after.setdefault(after, []).append(len(fill_slot))
                 fill_slot.append(slot)
-                free_at.append((ORDER.index((LAST_READER[name], c)), slot))
-            return fill_slot, fills_after
+                free_at.append((after + 2 if name == "dgo" else order.index((READER[name], c)), slot))
+            return order, fills, fill_slot, fills_after
 
-        PLANS = {t: bank_plan(6 if t in SIX_BANKS else 4) for t in range(TOK_TILES)}
+        PLANS = [bank_plan(ORDER, FILLS, banks) for banks in FLIP_BANKS[:-1]]
+        PLANS.append(bank_plan(LAST_ORDER, LAST_FILLS, FLIP_BANKS[-1]))
         banks_of, tiles_of = {}, {}
 
         def fill(t, k):
             tok = tok_of[t]
-            name, c = FILLS[k]
-            slot = PLANS[t][0][k]
-            if name == "rz":
+            name, c = PLANS[t][1][k]
+            slot = PLANS[t][2][k]
+            if name == "dgo":
+                nc.scalar.activation(
+                    out=val["dgT", t][:, c, PLACE_O], in_=flip(val["dgo"], c, slot), func=ACT.Copy, scale=-0.25
+                )
+            elif name == "rz" and t < TOK_TILES - 1:
                 banks_of[t, name, c] = flip_sum(val["r", t], tok["z"], c, slot)
             else:
                 source = {"to": tok["o"], "i": tok["i"], "ct": tok["c_t"], "tf2": tok["f"], "mcn": val["mcn", t],
-                          "zsq": val["zsq", t]}[name]
+                          "rz": val["r", t], "zsq": val["zsq", t]}[name]
                 banks_of[t, name, c] = flip(source, c, slot)
 
         def product(t, name, c):
@@ -383,6 +408,8 @@ def tile_slstmcell_t_v_kernel(
                 return banks_of[t, which, c]
 
             def made(which):
+                if which == "dc" and t == TOK_TILES - 1:
+                    return uT[:, c]
                 return tiles_of[which, c][:]
 
             def chain(which):
@@ -407,12 +434,9 @@ def tile_slstmcell_t_v_kernel(
                 stt(dgT[:, c, PLACE_Z], bank("zsq"), ALU.subtract, 1.0, ALU.mult, made("mdci"))
 
         def products(t, first, last, hooks):
-            fills_after = PLANS[t][1]
-            if first == 0:
-                for k in fills_after[-1]:
-                    fill(t, k)
+            order, fills_after = PLANS[t][0], PLANS[t][3]
             for n in range(first, last):
-                product(t, *ORDER[n])
+                product(t, *order[n])
                 for k in fills_after.get(n, ()):
                     fill(t, k)
                 if n in hooks:
@@ -430,21 +454,23 @@ def tile_slstmcell_t_v_kernel(
             dg_codes[t] = dg_keep.tile([P, HALVES, GATES, P], U32, name="dg_codes", align_bytes=64)
             dg_scales[t] = dg_keep.tile([P, HALVES, GATES, P], U8, name="dg_scales", align_bytes=64)
 
-        for t in range(2):
-            load_inputs(t, ("grad",))
+        load_gradients(0)
         nc.sync.dma_start(out=gamma_rows[0:1, :], in_=ln_gamma.unsqueeze(0))
-        for t in range(TOK_TILES):
-            load_inputs(t, ("q",))
+        load_inputs(0, ("q",))
+        load_inputs(1, ("q",))
+        load_inputs(2, ("q",))
+        load_inputs(3, ("q",))
+        load_gradients(2)
         load_weight_pass(0)
-        load_inputs(0, ("c_t", "o"))
+        load_inputs(0, ("c_t", "o",))
         load_weight_pass(1)
         load_inputs(1, ("c_t",))
-        load_inputs(0, ("n_prev", "c_prev"))
+        load_inputs(0, ("n_prev", "c_prev",))
         load_inputs(1, ("o",))
-        load_inputs(0, ("z", "i", "f"))
-        load_inputs(2, ("c_t",))
-        load_inputs(1, ("n_prev", "c_prev", "z", "i", "f"))
         load_weight_pass(2)
+        load_inputs(0, ("z", "i", "f",))
+        load_inputs(2, ("c_t",))
+        load_inputs(1, ("n_prev", "c_prev", "z", "i", "f",))
         load_weight_pass(3)
 
         for t in range(TOK_TILES):
@@ -452,14 +478,15 @@ def tile_slstmcell_t_v_kernel(
         act_q(0)
         act_o(0)
         act_q(1)
-        regroup_weights(nc.scalar.copy, 0, (896, 128))
-        regroup_weights(nc.scalar.copy, 0, (1024, 512))
-        for n0 in range(0, H, N_MX):
-            spread = psum.tile([P, N_MX], F32, name="gamma_spread", tag="bank%d" % (n0 // N_MX))
-            nc.tensor.matmul(out=spread[:], lhsT=ones[:], rhs=gamma_rows[:, n0 : n0 + N_MX], start=True, stop=True)
-            nc.vector.tensor_copy(out=gamma[:, n0 : n0 + N_MX], in_=spread[:])
-        make_dy(0)
-        make_dy(1)
+        regroup_weights(nc.scalar.copy, 0, (896, 640))
+        gamma = []
+        for c in range(HALVES):
+            gamma.append(psum.tile([P, N_MX], F32, name="gamma", tag="bank%d" % c))
+            nc.tensor.matmul(
+                out=gamma[c][:], lhsT=ones[:], rhs=gamma_rows[:, N_MX * c : N_MX * (c + 1)], start=True, stop=True
+            )
+        for t in range(TOK_TILES):
+            make_dy(t)
         regroup_weights(nc.vector.tensor_copy, 0, (0, 512))
         regroup_weights(nc.vector.tensor_copy, 0, (512, 384))
         for call in ((0, 512), (512, 256), (768, 128)):
@@ -467,118 +494,159 @@ def tile_slstmcell_t_v_kernel(
         make_r(nc.vector, 0)
         make_h2(0)
         make_r(nc.vector, 1)
+        make_mm(0)
         make_squares(0)
         act_o(1)
-        make_dyh(0)
-        make_cov(0)
         make_rn(nc.vector, 0)
-        variance(0)
-        act_qr(0)
-        act_q(2)
-        act_i(0)
-        act_z(0)
-        slope_and_offset(0, 0)
+        make_cov(0)
         make_mcn(nc.vector, 0)
-        slope_and_offset(0, 1)
-        slope_and_offset(0, 2)
+        variance(0)
+        make_h2(1)
+        make_slope(0)
+        act_q(2)
+        regroup_weights(nc.scalar.copy, 1, W_SHARES[0])
+        act_i(0)
+        make_mm(1)
+        make_squares(1)
         make_x(0)
+        act_z(0)
+        make_qr(nc.vector, 0)
+        make_offset(0)
         quantise_weights(0, (896, 128))
         make_u(0)
         for c in range(HALVES):
             flip_and_copy_u(0, c)
         act_f(0)
-        regroup_weights(nc.vector.tensor_copy, 0, (1536, 256))
-        make_h2(1)
-        quantise_weights(0, (1024, 512))
-        make_squares(1)
-        quantise_weights(0, (1536, 256))
         act_f2(0)
         act_z2(0)
-        new_gradient_tiles(0)
-        make_dyh(1)
+        regroup_weights(nc.vector.tensor_copy, 0, (1536, 256))
+        quantise_weights(0, (1024, 512))
+        quantise_weights(0, (1536, 256))
         make_cov(1)
+        new_gradient_tiles(0)
+        for k in range(4):
+            fill(0, k)
         products(0, 0, 1, {})
 
-        for t in range(TOK_TILES):
-            if t + 2 < TOK_TILES:
+        for t in range(TOK_TILES - 1):
+            last_but_one = t + 2 == TOK_TILES
+            if not last_but_one:
                 make_r(nc.gpsimd, t + 2)
-            if t + 1 < TOK_TILES:
-                make_rn(nc.gpsimd, t + 1)
-                products(t, 1, 3, {})
-                variance(t + 1)
-                gpsimd_qr(t + 1)
-                make_mcn(nc.gpsimd, t + 1)
-                gate_activations(t + 1)
-                regroup_weights(nc.scalar.copy, t + 1, W_SHARES[2])
-                regroup_weights(nc.scalar.copy, t + 1, W_SHARES[3])
-                products(t, 3, 16, {})
+            make_rn(nc.gpsimd, t + 1)
+            products(t, 1, 3, {})
+            variance(t + 1)
+            make_qr(nc.gpsimd, t + 1)
+            make_mcn(nc.gpsimd, t + 1)
+            if last_but_one:
+                act_z(t + 1)
+                make_rz(t + 1)
+                act_z2(t + 1)
+                act_i(t + 1)
+                act_f(t + 1)
+                act_f2(t + 1)
             else:
-                def after_first_half():
-                    quantise_half(t, 0)
-                    push(t, range(GATES), (0,))
-                    pe_fill(1)
-
-                def finish(s):
-                    pe_fill(1)
-                    quantise_pass(t, 1, s)
-                    multiply(t, s, 1)
-
-                hooks = {n: (lambda: pe_fill(2)) for n in PE_SLOTS}
-                hooks.update({8: after_first_half, 9: lambda: pe_fill(1), 10: lambda: pe_fill(1),
-                              11: lambda: finish(PLACE_O), 13: lambda: finish(PLACE_I),
-                              14: lambda: finish(PLACE_F), 15: lambda: finish(PLACE_Z)})
-                products(t, 1, 16, hooks)
+                gate_activations(t + 1)
+            regroup_weights(nc.scalar.copy, t + 1, W_SHARES[2])
+            regroup_weights(nc.scalar.copy, t + 1, W_SHARES[3])
+            if last_but_one:
+                act_o_less_1(t + 1)
+            products(t, 3, 6, {})
+            make_slope(t + 1)
+            products(t, 6, 16, {})
+            if last_but_one:
                 break
-            if t + 2 < TOK_TILES:
-                load_inputs(t + 2, ("o", "grad"))
+            load_inputs(t + 2, ("o",))
             if t + 3 < TOK_TILES:
                 load_inputs(t + 3, ("c_t",))
-            if t + 2 < GATES:
-                load_weight_pass(HALVES * (t + 2))
-                load_weight_pass(HALVES * (t + 2) + 1)
-            if t + 2 < TOK_TILES:
-                load_inputs(t + 2, ("n_prev", "c_prev", "z", "i", "f"))
-            pe_fill(100)
-            if t + 2 < TOK_TILES:
-                act_o(t + 2)
+            load_weight_pass(HALVES * (t + 2))
+            load_weight_pass(HALVES * (t + 2) + 1)
+            load_inputs(t + 2, ("n_prev", "c_prev", "z", "i", "f"))
+            act_o(t + 2)
             if t + 3 < TOK_TILES:
                 act_q(t + 3)
-            slope_and_offset(t + 1, 0)
-            if t == 0:
-                regroup_weights(nc.vector.tensor_copy, 1, W_SHARES[0])
-                regroup_weights(nc.vector.tensor_copy, 1, W_SHARES[1])
-            quantise_weights(t + 1, W_CALLS[0])
-            if t + 2 < GATES:
-                regroup_weights(nc.scalar.copy, t + 2, W_SHARES[0])
-            slope_and_offset(t + 1, 1)
-            quantise_weights(t + 1, W_CALLS[1])
-            slope_and_offset(t + 1, 2)
-            quantise_weights(t + 1, W_CALLS[2])
-            for earlier in range(t):
-                push(earlier, (t + 1,), (0, 1))
-                if t + 1 == GATES - 1:
-                    pe_jobs.append(("store", earlier))
-            pe_fill(100)
-            make_x(t + 1)
+            s = t + 1
+            fill(s, 0)
+            fill(s, 1)
             quantise_half(t, 0)
-            push(t, range(t + 2), (0,))
+            push(t, range(s), (0,))
             pe_fill(100)
-            make_u(t + 1)
-            if t + 2 < GATES:
-                regroup_weights(nc.scalar.copy, t + 2, W_SHARES[1])
-            for c in range(HALVES):
-                flip_and_copy_u(t + 1, c)
-            if t + 2 < TOK_TILES:
-                make_dy(t + 2)
-                make_h2(t + 2)
+            make_x(s)
             quantise_half(t, 1)
-            push(t, range(t + 2), (1,))
-            if t + 1 == GATES - 1:
-                pe_jobs.append(("store", t))
-            if t + 2 < TOK_TILES:
-                make_squares(t + 2)
-                make_dyh(t + 2)
-                make_cov(t + 2)
-            new_gradient_tiles(t + 1)
-            products(t + 1, 0, 1, {})
-        store(TOK_TILES - 1, nc.vector.tensor_copy)
+            push(t, range(s), (1,))
+            pe_fill(100)
+            make_offset(s)
+            if t == 0:
+                regroup_weights(nc.vector.tensor_copy, 1, W_SHARES[1])
+            quantise_weights(s, W_CALLS[0])
+            for tile_ in range(s):
+                push(tile_, (s,), (0,))
+            pe_fill(100)
+            regroup_weights(nc.scalar.copy, t + 2, W_SHARES[0])
+            make_u(s)
+            for c in range(HALVES):
+                flip_and_copy_u(s, c)
+            fill(s, 2)
+            fill(s, 3)
+            make_h2(t + 2)
+            quantise_weights(s, W_CALLS[1])
+            make_mm(t + 2)
+            make_squares(t + 2)
+            regroup_weights(nc.scalar.copy, t + 2, W_SHARES[1])
+            quantise_weights(s, W_CALLS[2])
+            for tile_ in range(s):
+                push(tile_, (s,), (1,))
+            pe_fill(100)
+            make_cov(t + 2)
+            new_gradient_tiles(s)
+            products(s, 0, 1, {})
+
+        t = TOK_TILES - 1
+        s = GATES - 1
+        quantise_half(t - 1, 0)
+        push(t - 1, range(s), (0,))
+        pe_fill(100)
+        make_x(t)
+        quantise_half(t - 1, 1)
+        push(t - 1, range(s), (1,))
+        pe_fill(100)
+        make_offset(t)
+        quantise_weights(s, W_CALLS[0])
+        for tile_ in range(t):
+            push(tile_, (s,), (0,))
+        pe_fill(100)
+        make_u(t)
+        quantise_weights(s, W_CALLS[1])
+        make_dc(t)
+        gpsimd_products_o(t)
+        quantise_weights(s, W_CALLS[2])
+        for c in range(HALVES):
+            flip_and_copy_u(t, c)
+        for tile_ in (1, 0, 2):
+            push(tile_, (s,), (1,))
+            pe_jobs.append(("store", tile_))
+        pe_fill(2)
+        new_gradient_tiles(t)
+        for k in range(4):
+            fill(t, k)
+
+        def after(places, c, n):
+            for place in places:
+                quantise_pass(t, c, place)
+                push(t, (place,), (c,))
+            pe_fill(n)
+
+        hooks = {
+            0: lambda: pe_fill(1),
+            1: lambda: pe_fill(1),
+            2: lambda: pe_fill(1),
+            3: lambda: after((PLACE_I,), 0, 1),
+            4: lambda: after((PLACE_F,), 0, 1),
+            5: lambda: after((PLACE_Z,), 0, 1),
+            6: lambda: pe_fill(1),
+            7: lambda: after((PLACE_O,), 0, 1),
+            8: lambda: (after((PLACE_I,), 1, 0), after((PLACE_O,), 1, 1)),
+            9: lambda: after((PLACE_F,), 1, 1),
+        }
+        products(t, 0, len(LAST_ORDER), hooks)
+        after((PLACE_Z,), 1, 100)
+        store(t, nc.vector.tensor_copy)

@@ -25,7 +25,7 @@ HALVES = H // K_PASS
 PASSES = GATES * HALVES
 N_MX = 512
 N_STARTS = (0, IN - N_MX)
-W_SHARES = ((0, 512), (512, 512), (1024, 512), (1536, 256))
+W_SHARES = ((0, 512), (512, 512), (1024, 768))
 W_CALLS = ((0, 1024), (1024, 512), (1536, 256))
 W_BUFS = 4
 FLIP_BANKS = ((0, 1, 2, 3), (0, 1, 2, 3), (0, 1, 2, 3), (0, 1, 4, 5))
@@ -212,12 +212,15 @@ def tile_slstmcell_t_v_kernel(
             )
 
         def variance(t):
-            val["var_eps", t], val["inv_var", t], val["rstd", t] = column("var_eps"), column("inv_var"), column("rstd")
+            val["var_eps", t], val["rstd", t] = column("var_eps"), column("rstd")
             nc.vector.tensor_scalar(
                 out=val["var_eps", t][:], in0=val["sum_sq", t][:], scalar1=0.25 / H, scalar2=LN_EPS, op0=ALU.mult, op1=ALU.add
             )
-            nc.vector.reciprocal(out=val["inv_var", t][:], in_=val["var_eps", t][:])
             nc.gpsimd.tensor_tensor(out=val["rstd", t][:], in0=val["var_eps", t][:], in1=minus_half[:], op=ALU.pow)
+
+        def make_inv_var(t):
+            val["inv_var", t] = column("inv_var")
+            nc.vector.reciprocal(out=val["inv_var", t][:], in_=val["var_eps", t][:])
 
         def make_qr(eng, t):
             q = tok_of[t]["q"]
@@ -330,9 +333,11 @@ def tile_slstmcell_t_v_kernel(
 
         def store(t, second_copy):
             result = w_stage.tile([P, IN], F32, name="result", tag="w_raw")
-            nc.scalar.copy(out=result[:, 0:N_MX], in_=acc[t][0][:])
-            second_copy(out=result[:, N_MX:IN], in_=acc[t][1][:, 2 * N_MX - IN : N_MX])
-            nc.sync.dma_start(out=out[P * t : P * (t + 1), :], in_=result[:])
+            low, high = slice(0, N_MX), slice(N_MX, IN)
+            nc.scalar.copy(out=result[:, low], in_=acc[t][0][:])
+            second_copy(out=result[:, high], in_=acc[t][1][:, 2 * N_MX - IN : N_MX])
+            for columns in (low, high):
+                nc.sync.dma_start(out=out[P * t : P * (t + 1), columns], in_=result[:, columns])
 
         pe_jobs = []
 
@@ -445,8 +450,8 @@ def tile_slstmcell_t_v_kernel(
         def gate_activations(t):
             act_i(t)
             act_f(t)
-            act_f2(t)
             act_z(t)
+            act_f2(t)
             act_z2(t)
 
         def new_gradient_tiles(t):
@@ -475,9 +480,9 @@ def tile_slstmcell_t_v_kernel(
 
         for t in range(TOK_TILES):
             act_ln(t)
-        act_q(0)
+        for t in range(3):
+            act_q(t)
         act_o(0)
-        act_q(1)
         regroup_weights(nc.scalar.copy, 0, (896, 640))
         gamma = []
         for c in range(HALVES):
@@ -489,9 +494,9 @@ def tile_slstmcell_t_v_kernel(
             make_dy(t)
         regroup_weights(nc.vector.tensor_copy, 0, (0, 512))
         regroup_weights(nc.vector.tensor_copy, 0, (512, 384))
+        make_r(nc.vector, 0)
         for call in ((0, 512), (512, 256), (768, 128)):
             quantise_weights(0, call)
-        make_r(nc.vector, 0)
         make_h2(0)
         make_r(nc.vector, 1)
         make_mm(0)
@@ -502,24 +507,24 @@ def tile_slstmcell_t_v_kernel(
         make_mcn(nc.vector, 0)
         variance(0)
         make_h2(1)
-        make_slope(0)
-        act_q(2)
+        make_inv_var(0)
         regroup_weights(nc.scalar.copy, 1, W_SHARES[0])
         act_i(0)
+        quantise_weights(0, (896, 128))
+        make_slope(0)
         make_mm(1)
         make_squares(1)
         make_x(0)
         act_z(0)
+        act_f(0)
         make_qr(nc.vector, 0)
         make_offset(0)
-        quantise_weights(0, (896, 128))
+        regroup_weights(nc.vector.tensor_copy, 0, (1536, 256))
         make_u(0)
         for c in range(HALVES):
             flip_and_copy_u(0, c)
-        act_f(0)
         act_f2(0)
         act_z2(0)
-        regroup_weights(nc.vector.tensor_copy, 0, (1536, 256))
         quantise_weights(0, (1024, 512))
         quantise_weights(0, (1536, 256))
         make_cov(1)
@@ -535,22 +540,23 @@ def tile_slstmcell_t_v_kernel(
             make_rn(nc.gpsimd, t + 1)
             products(t, 1, 3, {})
             variance(t + 1)
+            products(t, 3, 4, {})
+            make_inv_var(t + 1)
             make_qr(nc.gpsimd, t + 1)
             make_mcn(nc.gpsimd, t + 1)
             if last_but_one:
                 act_z(t + 1)
                 make_rz(t + 1)
-                act_z2(t + 1)
                 act_i(t + 1)
+                act_z2(t + 1)
                 act_f(t + 1)
+                regroup_weights(nc.scalar.copy, t + 1, W_SHARES[2])
                 act_f2(t + 1)
+                act_o_less_1(t + 1)
             else:
                 gate_activations(t + 1)
-            regroup_weights(nc.scalar.copy, t + 1, W_SHARES[2])
-            regroup_weights(nc.scalar.copy, t + 1, W_SHARES[3])
-            if last_but_one:
-                act_o_less_1(t + 1)
-            products(t, 3, 6, {})
+                regroup_weights(nc.scalar.copy, t + 1, W_SHARES[2])
+            products(t, 4, 6, {})
             make_slope(t + 1)
             products(t, 6, 16, {})
             if last_but_one:

@@ -554,6 +554,8 @@ def tile_slstmcell_t_v_kernel(
                 act_f2(t + 1)
                 act_o_less_1(t + 1)
             else:
+                if t == 0:
+                    regroup_weights(nc.scalar.copy, 1, W_SHARES[1])
                 gate_activations(t + 1)
                 regroup_weights(nc.scalar.copy, t + 1, W_SHARES[2])
             products(t, 4, 6, {})
@@ -581,8 +583,6 @@ def tile_slstmcell_t_v_kernel(
             push(t, range(s), (1,))
             pe_fill(100)
             make_offset(s)
-            if t == 0:
-                regroup_weights(nc.vector.tensor_copy, 1, W_SHARES[1])
             quantise_weights(s, W_CALLS[0])
             for tile_ in range(s):
                 push(tile_, (s,), (0,))

@@ -591,8 +591,6 @@ def tile_slstmcell_t_v_kernel(
             make_u(s)
             for c in range(HALVES):
                 flip_and_copy_u(s, c)
-            fill(s, 2)
-            fill(s, 3)
             make_h2(t + 2)
             quantise_weights(s, W_CALLS[1])
             make_mm(t + 2)
@@ -602,6 +600,8 @@ def tile_slstmcell_t_v_kernel(
             for tile_ in range(s):
                 push(tile_, (s,), (1,))
             pe_fill(100)
+            fill(s, 2)
+            fill(s, 3)
             make_cov(t + 2)
             new_gradient_tiles(s)
             products(s, 0, 1, {})

from contextlib import ExitStack

import concourse.mybir as mybir
from concourse.masks import make_identity

F32 = mybir.dt.float32
BF16 = mybir.dt.bfloat16
U32 = mybir.dt.uint32
U8 = mybir.dt.uint8
E4M3X4 = mybir.dt.float8_e4m3fn_x4
E5M2X4 = mybir.dt.float8_e5m2_x4
ACT = mybir.ActivationFunctionType
ALU = mybir.AluOpType

B, IN, H = 512, 896, 1024
LN_EPS = 1e-5
DIV_EPS = 1e-6

P = 128
PACK = 4
K_PASS = P * PACK
TOK_TILES = B // P
GATES = 4
HALVES = H // K_PASS
PASSES = GATES * HALVES
N_MX = 512
N_STARTS = (0, IN - N_MX)
W_SHARES = ((0, 512), (512, 512), (1024, 768))
W_CALLS = ((0, 1024), (1024, 512), (1536, 256))
W_BUFS = 4
FLIP_BANKS = ((0, 1, 2, 3), (0, 1, 2, 3), (0, 1, 2, 3), (0, 1, 4, 5))
ACC_BANKS = ((6, 7), (4, 5), (2, 3), (6, 7))
U_BANKS = ((2, 3), (2, 3), (2, 3), (0, 1))

FLOPS = 2 * B * GATES * H * IN
BYTES = (GATES + 2) * B * H * 4 + 3 * B * H * 2 + GATES * H * IN * 2 + H * 2 + B * IN * 4


def tile_slstmcell_t_v_kernel(
    tc, x, h_prev, c_prev, n_prev, m_prev, Wi, bi, Wf, bf, Wo, bo, Wz, bz, ln_gamma, ln_beta,
    gates, c_t, n_t, grad_out, out,
):
    nc = tc.nc
    weight_at = (Wo, Wi, Wf, Wz)
    PLACE_O, PLACE_I, PLACE_F, PLACE_Z = 0, 1, 2, 3
    gate_row = {"o": 2, "f": 1, "i": 0, "z": 3}

    with ExitStack() as ctx:
        ctx.enter_context(tc.manual_schedule())
        const = ctx.enter_context(tc.tile_pool(name="const", bufs=1))
        w_stage = ctx.enter_context(tc.tile_pool(name="w_stage", bufs=W_BUFS))
        w_keep = ctx.enter_context(tc.tile_pool(name="w_keep", bufs=1))
        norm = ctx.enter_context(tc.tile_pool(name="norm", bufs=1))
        tok_in = ctx.enter_context(tc.tile_pool(name="tok_in", bufs=2))
        tok_once = ctx.enter_context(tc.tile_pool(name="tok_once", bufs=1))
        tok_three = ctx.enter_context(tc.tile_pool(name="tok_three", bufs=3))
        spare = ctx.enter_context(tc.tile_pool(name="spare", bufs=4))
        work = ctx.enter_context(tc.tile_pool(name="work", bufs=1))
        dy_keep = ctx.enter_context(tc.tile_pool(name="dy_keep", bufs=1))
        work2 = ctx.enter_context(tc.tile_pool(name="work2", bufs=2))
        feat = ctx.enter_context(tc.tile_pool(name="feat", bufs=1))
        stats = ctx.enter_context(tc.tile_pool(name="stats", bufs=2))
        dg_keep = ctx.enter_context(tc.tile_pool(name="dg_keep", bufs=3))
        psum = ctx.enter_context(tc.psum_pool(name="psum", bufs=1))

        minus_half = const.tile([P, 1], F32, name="minus_half")
        nc.vector.memset(minus_half[:], -0.5)
        gamma_rows = const.tile([P, H], BF16, name="gamma_rows")
        ones = const.tile([P, P], BF16, name="ones")
        nc.vector.memset(gamma_rows[:], 0.0)
        nc.vector.memset(ones[:], 1.0)
        identity = const.tile([P, P], F32, name="identity")
        make_identity(nc, identity[:])

        w_codes = w_keep.tile([P, PASSES, IN], U32, name="w_codes", align_bytes=64)
        w_scales = w_keep.tile([P, PASSES, IN], U8, name="w_scales", align_bytes=64)
        w_raw = {}

        def load_weight_pass(c):
            weight = weight_at[c // HALVES]
            first_row = K_PASS * (c % HALVES)
            w_raw[c] = w_stage.tile([P, PACK, IN], BF16, name="w_raw")
            rows = weight[first_row : first_row + K_PASS, 0:IN]
            nc.sync.dma_start(out=w_raw[c][:], in_=rows.rearrange("(j p) n -> p j n", p=P))

        w_grouped = w_keep.tile([P, HALVES * IN, PACK], BF16, name="w_grouped", align_bytes=64)

        def regroup_weights(copy, s, share):
            first, width = share
            for c in range(HALVES):
                low, high = max(first, IN * c), min(first + width, IN * (c + 1))
                if low < high:
                    copy(
                        out=w_grouped[:, low:high, :].rearrange("p (c i) v -> p c v i", i=4),
                        in_=w_raw[HALVES * s + c][:, :, low - IN * c : high - IN * c].rearrange(
                            "p v (c i) -> p c v i", i=4
                        ),
                    )

        def quantise_weights(s, call):
            first, width = call
            passes = slice(HALVES * s, HALVES * (s + 1))
            nc.vector.quantize_mx(
                out=w_codes[:, passes, :].rearrange("p c n -> p (c n)")[:, first : first + width].bitcast(E4M3X4),
                scales=w_scales[:, passes, :].rearrange("p c n -> p (c n)")[:, first : first + width],
                in_=w_grouped[:, first : first + width, :].rearrange("p n v -> p (n v)"),
            )

        tok_of = {t: {} for t in range(TOK_TILES)}
        val = {}

        def load_inputs(t, names):
            rows = slice(P * t, P * (t + 1))
            for name in names:
                if name in gate_row:
                    tile_, source = tok_in.tile([P, H], F32, name="gate_" + name), gates[gate_row[name], rows, :]
                elif name == "c_t":
                    tile_, source = tok_three.tile([P, H], F32, name="cell"), c_t[rows, :]
                elif name == "q":
                    tile_, source = norm.tile([P, H], F32, name="log_n", tag="slot%d" % t), n_t[rows, :]
                elif name == "n_prev":
                    tile_, source = tok_once.tile([P, H], BF16, name="n_before"), n_prev[rows, :]
                else:
                    tile_, source = tok_once.tile([P, H], BF16, name="c_before"), c_prev[rows, :]
                nc.sync.dma_start(out=tile_[:], in_=source)
                tok_of[t][name] = tile_

        def in_place(tile_, func, scale=1.0):
            nc.scalar.activation(out=tile_[:], in_=tile_[:], func=func, scale=scale)

        def column(name):
            return stats.tile([P, 1], F32, name=name)

        def stt(out_, in0, op0, scalar, op1, in1, accum_out=None):
            nc.vector.scalar_tensor_tensor(
                out=out_, in0=in0, scalar=scalar, in1=in1, op0=op0, op1=op1, accum_out=accum_out
            )

        def act_ln(t):
            nc.scalar.activation(out=tok_of[t]["q"][:], in_=tok_of[t]["q"][:], func=ACT.Ln, bias=DIV_EPS)

        def act_q(t):
            in_place(tok_of[t]["q"], ACT.Exp, scale=-1.0)

        def act_o(t):
            in_place(tok_of[t]["o"], ACT.Tanh, scale=0.5)

        def act_f(t):
            in_place(tok_of[t]["f"], ACT.Tanh, scale=0.5)

        def act_f2(t):
            in_place(tok_of[t]["f"], ACT.Square)

        def act_z(t):
            in_place(tok_of[t]["z"], ACT.Tanh, scale=-1.0)

        def act_z2(t):
            val["zsq", t] = spare.tile([P, H], F32, name="z_squared", tag="spare")
            nc.scalar.activation(out=val["zsq", t][:], in_=tok_of[t]["z"][:], func=ACT.Square)

        def act_i(t):
            in_place(tok_of[t]["i"], ACT.Exp)

        def make_r(eng, t):
            if t < 2:
                val["r", t] = spare.tile([P, H], F32, name="r_first", tag="spare")
            else:
                val["r", t] = norm.tile([P, H], F32, name="r", tag="slot%d" % (t - 2))
            eng.tensor_tensor(out=val["r", t][:], in0=tok_of[t]["c_t"][:], in1=tok_of[t]["q"][:], op=ALU.mult)

        def make_rn(eng, t):
            val["mcn", t] = work2.tile([P, H], F32, name="mcn", tag="mcn")
            eng.tensor_tensor(out=val["mcn", t][:], in0=val["r", t][:], in1=tok_of[t]["n_prev"][:], op=ALU.mult)

        def make_mcn(eng, t):
            eng.tensor_tensor(out=val["mcn", t][:], in0=val["mcn", t][:], in1=tok_of[t]["c_prev"][:], op=ALU.subtract)

        def load_gradients(first):
            pair = w_stage.tile([P, 2, H], BF16, name="grad_pair", tag="w_raw")
            rows = grad_out[P * first : P * (first + 2), :]
            nc.sync.dma_start(out=pair[:], in_=rows.rearrange("(j p) n -> p j n", p=P))
            for t in range(2):
                tok_of[first + t]["grad"] = pair[:, t, :]

        def make_dy(t):
            val["dy", t] = dy_keep.tile([P, H], F32, name="dy", tag="dy%d" % t)
            for c in range(HALVES):
                half = slice(N_MX * c, N_MX * (c + 1))
                nc.vector.tensor_tensor(
                    out=val["dy", t][:, half], in0=tok_of[t]["grad"][:, half], in1=gamma[c][:], op=ALU.mult
                )

        def make_h2(t):
            val["h2", t], val["sum_h2", t] = work2.tile([P, H], F32, name="h2"), column("sum_h2")
            stt(val["h2", t][:], tok_of[t]["o"][:], ALU.add, 1.0, ALU.mult, val["r", t][:], accum_out=val["sum_h2", t][:])

        def make_mm(t):
            val["mm", t] = column("mm")
            nc.vector.tensor_scalar_mul(out=val["mm", t][:], in0=val["sum_h2", t][:], scalar1=-1.0 / H)

        def make_squares(t):
            junk, val["sum_sq", t] = work.tile([P, H], BF16, name="junk_squares"), column("sum_sq")
            nc.scalar.activation(
                out=junk[:], in_=val["h2", t][:], func=ACT.Square, bias=val["mm", t][:], accum_out=val["sum_sq", t][:]
            )

        def make_cov(t):
            junk, val["cov", t], val["ncov", t] = work.tile([P, H], BF16, name="junk_products"), column("cov"), column("ncov")
            stt(junk[:], val["h2", t][:], ALU.add, val["mm", t][:], ALU.mult, val["dy", t][:], accum_out=val["cov", t][:])
            nc.gpsimd.tensor_scalar(
                out=val["ncov", t][:], in0=val["cov", t][:], scalar1=-0.25 / H, scalar2=0.0, op0=ALU.mult, op1=ALU.add
            )

        def variance(t):
            val["var_eps", t], val["rstd", t] = column("var_eps"), column("rstd")
            nc.vector.tensor_scalar(
                out=val["var_eps", t][:], in0=val["sum_sq", t][:], scalar1=0.25 / H, scalar2=LN_EPS, op0=ALU.mult, op1=ALU.add
            )
            nc.gpsimd.tensor_tensor(out=val["rstd", t][:], in0=val["var_eps", t][:], in1=minus_half[:], op=ALU.pow)

        def make_inv_var(t):
            val["inv_var", t] = column("inv_var")
            nc.vector.reciprocal(out=val["inv_var", t][:], in_=val["var_eps", t][:])

        def make_qr(eng, t):
            q = tok_of[t]["q"]
            eng.tensor_scalar(out=q[:], in0=q[:], scalar1=val["rstd", t][:], scalar2=0.0, op0=ALU.mult, op1=ALU.add)

        def make_slope(t):
            val["slope", t] = column("slope")
            nc.vector.tensor_scalar_mul(out=val["slope", t][:], in0=val["ncov", t][:], scalar1=val["inv_var", t][:])

        def make_x(t):
            dy, val["sum_x", t] = val["dy", t], column("sum_x")
            stt(dy[:], val["h2", t][:], ALU.mult, val["slope", t][:], ALU.add, dy[:], accum_out=val["sum_x", t][:])

        def make_offset(t):
            val["offset", t] = column("offset")
            nc.vector.tensor_scalar_mul(out=val["offset", t][:], in0=val["sum_x", t][:], scalar1=-1.0 / H)

        def make_u(t):
            val["u", t] = val["dy", t]
            stt(val["u", t][:], val["u", t][:], ALU.add, val["offset", t][:], ALU.mult, tok_of[t]["q"][:])

        def make_dc(t):
            stt(val["u", t][:], tok_of[t]["o"][:], ALU.add, 2.0, ALU.mult, val["u", t][:])

        def act_o_less_1(t):
            nc.scalar.activation(out=tok_of[t]["o"][:], in_=tok_of[t]["o"][:], func=ACT.Identity, bias=-1.0)

        def make_rz(t):
            nc.gpsimd.tensor_tensor(out=val["r", t][:], in0=val["r", t][:], in1=tok_of[t]["z"][:], op=ALU.add)

        def gpsimd_products_o(t):
            val["dgo"] = work2.tile([P, H], F32, name="dgo", tag="mcn")
            nc.gpsimd.tensor_tensor(out=val["dgo"][:], in0=val["u", t][:], in1=tok_of[t]["c_t"][:], op=ALU.mult)
            nc.gpsimd.tensor_tensor(out=val["dgo"][:], in0=val["dgo"][:], in1=tok_of[t]["o"][:], op=ALU.mult)

        def new_bank(slot):
            return psum.tile([P, PACK, P], F32, name="bank", tag="bank%d" % slot)

        def make_rz(t):
            nc.gpsimd.tensor_tensor(out=val["r", t][:], in0=val["r", t][:], in1=tok_of[t]["z"][:], op=ALU.add)

        def make_dc(t):
            stt(val["u", t][:], tok_of[t]["o"][:], ALU.add, 2.0, ALU.mult, val["u", t][:])

        def act_o_less_1(t):
            nc.scalar.activation(out=tok_of[t]["o"][:], in_=tok_of[t]["o"][:], func=ACT.Identity, bias=-1.0)

        def gpsimd_products_o(t):
            val["dgo"] = work2.tile([P, H], F32, name="dgo", tag="mcn")
            nc.gpsimd.tensor_tensor(out=val["dgo"][:], in0=val["u", t][:], in1=tok_of[t]["c_t"][:], op=ALU.mult)
            nc.gpsimd.tensor_tensor(out=val["dgo"][:], in0=val["dgo"][:], in1=tok_of[t]["o"][:], op=ALU.mult)

        def flip(source, c, slot):
            bank = new_bank(slot)
            for j in range(PACK):
                first = (PACK * c + j) * P
                nc.tensor.transpose(bank[:, j, :], source[:, first : first + P], identity[:])
            return bank[:].rearrange("p j k -> p k j")

        def flip_sum(first_source, second_source, c, slot):
            bank = new_bank(slot)
            for j in range(PACK):
                columns = slice((PACK * c + j) * P, (PACK * c + j + 1) * P)
                nc.tensor.matmul(
                    out=bank[:, j, :], lhsT=first_source[:, columns], rhs=identity[:], is_transpose=True, start=True, stop=False
                )
                nc.tensor.matmul(
                    out=bank[:, j, :], lhsT=second_source[:, columns], rhs=identity[:], is_transpose=True, start=False, stop=True
                )
            return bank[:].rearrange("p j k -> p k j")

        def flip_and_copy_u(t, c):
            if c == 0:
                val["uT", t] = feat.tile([P, HALVES, P, PACK], F32, name="uT")
            nc.scalar.copy(out=val["uT", t][:, c], in_=flip(val["u", t], c, U_BANKS[t][c]))

        dg_codes, dg_scales = {}, {}
        acc = {}
        passes_done = {}

        def quantise_half(t, c):
            nc.vector.quantize_mx(
                out=dg_codes[t][:, c].rearrange("p s k -> p (s k)").bitcast(E5M2X4),
                scales=dg_scales[t][:, c].rearrange("p s k -> p (s k)"),
                in_=val["dgT", t][:, c].rearrange("p s k j -> p (s k j)"),
            )

        def quantise_pass(t, c, s):
            nc.vector.quantize_mx(
                out=dg_codes[t][:, c, s].bitcast(E5M2X4),
                scales=dg_scales[t][:, c, s],
                in_=val["dgT", t][:, c, s].rearrange("p k j -> p (k j)"),
            )

        def multiply(t, s, c):
            if t not in acc:
                acc[t] = [psum.tile([P, N_MX], F32, name="acc", tag="bank%d" % slot) for slot in ACC_BANKS[t]]
                passes_done[t] = 0
            for side, n0 in enumerate(N_STARTS):
                nc.tensor.matmul_mx(
                    out=acc[t][side][:],
                    lhsT=dg_codes[t][:, c, s].bitcast(E5M2X4),
                    lhsT_scale=dg_scales[t][:, c, s],
                    rhs=w_codes[:, HALVES * s + c, n0 : n0 + N_MX].bitcast(E4M3X4),
                    rhs_scale=w_scales[:, HALVES * s + c, n0 : n0 + N_MX],
                    start=(passes_done[t] == 0),
                    stop=(passes_done[t] == PASSES - 1),
                )
            passes_done[t] += 1

        def store(t, second_copy):
            result = w_stage.tile([P, IN], F32, name="result", tag="w_raw")
            low, high = slice(0, N_MX), slice(N_MX, IN)
            nc.scalar.copy(out=result[:, low], in_=acc[t][0][:])
            second_copy(out=result[:, high], in_=acc[t][1][:, 2 * N_MX - IN : N_MX])
            for columns in (low, high):
                nc.sync.dma_start(out=out[P * t : P * (t + 1), columns], in_=result[:, columns])

        pe_jobs = []

        def push(t, places, halves):
            for s in places:
                for c in halves:
                    pe_jobs.append((t, s, c))

        def pe_fill(n):
            for count in range(n):
                if pe_jobs:
                    job = pe_jobs.pop(0)
                    if job[0] == "store":
                        store(job[1], nc.scalar.copy)
                    else:
                        multiply(*job)

        s_jobs = []

        def s_fill(n):
            for count in range(n):
                if s_jobs:
                    s, k = s_jobs.pop(0)
                    regroup_weights(nc.scalar.copy, s, W_SHARES[k])

        ORDER = (
            ("dc", 0), ("e", 0), ("mdci", 0), ("dgo", 0), ("g", 0), ("dgi", 0), ("dgf", 0), ("dc", 1),
            ("dgz", 0), ("e", 1), ("mdci", 1), ("dgo", 1), ("g", 1), ("dgi", 1), ("dgf", 1), ("dgz", 1),
        )
        FILLS = (
            ("to", 0), ("ct", 0), ("i", 0), ("tf2", 0), ("rz", 0), ("mcn", 0), ("to", 1),
            ("zsq", 0), ("ct", 1), ("i", 1), ("tf2", 1), ("rz", 1), ("mcn", 1), ("zsq", 1),
        )
        LAST_ORDER = tuple((name, c) for c in range(HALVES) for name in ("mdci", "g", "dgi", "dgf", "dgz"))
        LAST_FILLS = (("i", 0), ("tf2", 0), ("rz", 0), ("mcn", 0), ("zsq", 0), ("i", 1), ("dgo", 0), ("dgo", 1), ("tf2", 1), ("rz", 1), ("mcn", 1), ("zsq", 1))
        READER = {
            "to": "dgo", "ct": "e", "i": "mdci", "tf2": "g", "rz": "dgi", "mcn": "dgf", "zsq": "dgz",
        }

        def bank_plan(order, fills, banks):
            fill_slot, fills_after, free_at = [], {}, [(-1, slot) for slot in banks]
            for name, c in fills:
                free_at.sort()
                after, slot = free_at.pop(0)
                fills_after.setdefault(after, []).append(len(fill_slot))
                fill_slot.append(slot)
                free_at.append((after + 2 if name == "dgo" else order.index((READER[name], c)), slot))
            return order, fills, fill_slot, fills_after

        PLANS = [bank_plan(ORDER, FILLS, banks) for banks in FLIP_BANKS[:-1]]
        PLANS.append(bank_plan(LAST_ORDER, LAST_FILLS, FLIP_BANKS[-1]))
        banks_of, tiles_of = {}, {}

        def fill(t, k):
            tok = tok_of[t]
            name, c = PLANS[t][1][k]
            slot = PLANS[t][2][k]
            if name == "dgo":
                nc.scalar.activation(
                    out=val["dgT", t][:, c, PLACE_O], in_=flip(val["dgo"], c, slot), func=ACT.Copy, scale=-0.25
                )
            elif name == "rz" and t < TOK_TILES - 1:
                banks_of[t, name, c] = flip_sum(val["r", t], tok["z"], c, slot)
            else:
                source = {"to": tok["o"], "i": tok["i"], "ct": tok["c_t"], "tf2": tok["f"], "mcn": val["mcn", t],
                          "rz": val["r", t], "zsq": val["zsq", t]}[name]
                banks_of[t, name, c] = flip(source, c, slot)

        def product(t, name, c):
            dgT, uT = val["dgT", t], val["uT", t]

            def bank(which):
                return banks_of[t, which, c]

            def made(which):
                if which == "dc" and t == TOK_TILES - 1:
                    return uT[:, c]
                return tiles_of[which, c][:]

            def chain(which):
                tiles_of[name, c] = feat.tile([P, P, PACK], F32, name=which)
                return tiles_of[name, c][:]

            if name == "dc":
                stt(chain("dcT"), bank("to"), ALU.add, 1.0, ALU.mult, uT[:, c])
            elif name == "mdci":
                stt(chain("mdciT"), bank("i"), ALU.mult, -0.5, ALU.mult, made("dc"))
            elif name == "e":
                stt(chain("eT"), bank("ct"), ALU.mult, -0.25, ALU.mult, made("dc"))
            elif name == "g":
                stt(chain("gT"), bank("tf2"), ALU.subtract, 1.0, ALU.mult, made("dc"))
            elif name == "dgi":
                nc.vector.tensor_tensor(out=dgT[:, c, PLACE_I], in0=bank("rz"), in1=made("mdci"), op=ALU.mult)
            elif name == "dgo":
                stt(dgT[:, c, PLACE_O], bank("to"), ALU.subtract, 1.0, ALU.mult, made("e"))
            elif name == "dgf":
                stt(dgT[:, c, PLACE_F], bank("mcn"), ALU.mult, 0.125, ALU.mult, made("g"))
            else:
                stt(dgT[:, c, PLACE_Z], bank("zsq"), ALU.subtract, 1.0, ALU.mult, made("mdci"))

        def products(t, first, last, hooks):
            order, fills_after = PLANS[t][0], PLANS[t][3]
            for n in range(first, last):
                product(t, *order[n])
                for k in fills_after.get(n, ()):
                    fill(t, k)
                if n in hooks:
                    hooks[n]()

        def gate_activations(t):
            act_i(t)
            act_f(t)
            act_z(t)
            act_f2(t)
            act_z2(t)

        def new_gradient_tiles(t):
            val["dgT", t] = work2.tile([P, HALVES, GATES, P, PACK], BF16, name="dgT", align_bytes=64)
            dg_codes[t] = dg_keep.tile([P, HALVES, GATES, P], U32, name="dg_codes", align_bytes=64)
            dg_scales[t] = dg_keep.tile([P, HALVES, GATES, P], U8, name="dg_scales", align_bytes=64)

        load_gradients(0)
        nc.sync.dma_start(out=gamma_rows[0:1, :], in_=ln_gamma.unsqueeze(0))
        load_inputs(0, ("q",))
        load_inputs(1, ("q",))
        load_inputs(2, ("q",))
        load_inputs(3, ("q",))
        load_gradients(2)
        load_weight_pass(0)
        load_inputs(0, ("c_t", "o",))
        load_weight_pass(1)
        load_inputs(1, ("c_t",))
        load_inputs(0, ("n_prev", "c_prev",))
        load_inputs(1, ("o",))
        load_weight_pass(2)
        load_inputs(0, ("z", "i", "f",))
        load_inputs(2, ("c_t",))
        load_inputs(1, ("n_prev", "c_prev", "z", "i", "f",))
        load_weight_pass(3)

        for t in range(TOK_TILES):
            act_ln(t)
        for t in range(3):
            act_q(t)
        act_o(0)
        regroup_weights(nc.scalar.copy, 0, (896, 640))
        gamma = []
        for c in range(HALVES):
            gamma.append(psum.tile([P, N_MX], F32, name="gamma", tag="bank%d" % c))
            nc.tensor.matmul(
                out=gamma[c][:], lhsT=ones[:], rhs=gamma_rows[:, N_MX * c : N_MX * (c + 1)], start=True, stop=True
            )
        for t in range(TOK_TILES):
            make_dy(t)
        regroup_weights(nc.vector.tensor_copy, 0, (0, 512))
        regroup_weights(nc.vector.tensor_copy, 0, (512, 384))
        make_r(nc.vector, 0)
        for call in ((0, 512), (512, 256), (768, 128)):
            quantise_weights(0, call)
        make_h2(0)
        make_r(nc.vector, 1)
        make_mm(0)
        make_squares(0)
        act_o(1)
        make_rn(nc.vector, 0)
        make_cov(0)
        make_mcn(nc.vector, 0)
        variance(0)
        make_h2(1)
        make_inv_var(0)
        regroup_weights(nc.scalar.copy, 1, W_SHARES[0])
        act_i(0)
        quantise_weights(0, (896, 128))
        make_slope(0)
        make_mm(1)
        make_squares(1)
        make_x(0)
        act_z(0)
        act_f(0)
        make_qr(nc.vector, 0)
        make_offset(0)
        regroup_weights(nc.vector.tensor_copy, 0, (1536, 256))
        make_u(0)
        for c in range(HALVES):
            flip_and_copy_u(0, c)
        act_f2(0)
        act_z2(0)
        quantise_weights(0, (1024, 512))
        quantise_weights(0, (1536, 256))
        make_cov(1)
        new_gradient_tiles(0)
        for k in range(4):
            fill(0, k)
        products(0, 0, 1, {})

        for t in range(TOK_TILES - 1):
            last_but_one = t + 2 == TOK_TILES
            if not last_but_one:
                make_r(nc.gpsimd, t + 2)
            make_rn(nc.gpsimd, t + 1)
            products(t, 1, 3, {})
            variance(t + 1)
            products(t, 3, 4, {})
            make_inv_var(t + 1)
            make_qr(nc.gpsimd, t + 1)
            make_mcn(nc.gpsimd, t + 1)
            if last_but_one:
                act_z(t + 1)
                make_rz(t + 1)
                act_i(t + 1)
                act_z2(t + 1)
                act_f(t + 1)
                regroup_weights(nc.scalar.copy, t + 1, W_SHARES[2])
                act_f2(t + 1)
                act_o_less_1(t + 1)
            else:
                if t == 0:
                    regroup_weights(nc.scalar.copy, 1, W_SHARES[1])
                gate_activations(t + 1)
                regroup_weights(nc.scalar.copy, t + 1, W_SHARES[2])
            products(t, 4, 6, {})
            make_slope(t + 1)
            products(t, 6, 16, {})
            if last_but_one:
                break
            load_inputs(t + 2, ("o",))
            if t + 3 < TOK_TILES:
                load_inputs(t + 3, ("c_t",))
            load_weight_pass(HALVES * (t + 2))
            load_weight_pass(HALVES * (t + 2) + 1)
            load_inputs(t + 2, ("n_prev", "c_prev", "z", "i", "f"))
            act_o(t + 2)
            if t + 3 < TOK_TILES:
                act_q(t + 3)
            s = t + 1
            fill(s, 0)
            fill(s, 1)
            quantise_half(t, 0)
            push(t, range(s), (0,))
            pe_fill(100)
            make_x(s)
            quantise_half(t, 1)
            push(t, range(s), (1,))
            pe_fill(100)
            make_offset(s)
            quantise_weights(s, W_CALLS[0])
            for tile_ in range(s):
                push(tile_, (s,), (0,))
            pe_fill(100)
            regroup_weights(nc.scalar.copy, t + 2, W_SHARES[0])
            make_u(s)
            for c in range(HALVES):
                flip_and_copy_u(s, c)
            make_h2(t + 2)
            quantise_weights(s, W_CALLS[1])
            make_mm(t + 2)
            make_squares(t + 2)
            regroup_weights(nc.scalar.copy, t + 2, W_SHARES[1])
            quantise_weights(s, W_CALLS[2])
            for tile_ in range(s):
                push(tile_, (s,), (1,))
            pe_fill(100)
            fill(s, 2)
            fill(s, 3)
            make_cov(t + 2)
            new_gradient_tiles(s)
            products(s, 0, 1, {})

        t = TOK_TILES - 1
        s = GATES - 1
        quantise_half(t - 1, 0)
        push(t - 1, range(s), (0,))
        pe_fill(100)
        make_x(t)
        quantise_half(t - 1, 1)
        push(t - 1, range(s), (1,))
        pe_fill(100)
        make_offset(t)
        quantise_weights(s, W_CALLS[0])
        for tile_ in range(t):
            push(tile_, (s,), (0,))
        pe_fill(100)
        make_u(t)
        quantise_weights(s, W_CALLS[1])
        make_dc(t)
        gpsimd_products_o(t)
        quantise_weights(s, W_CALLS[2])
        for c in range(HALVES):
            flip_and_copy_u(t, c)
        for tile_ in (1, 0, 2):
            push(tile_, (s,), (1,))
            pe_jobs.append(("store", tile_))
        pe_fill(2)
        new_gradient_tiles(t)
        for k in range(4):
            fill(t, k)

        def after(places, c, n):
            for place in places:
                quantise_pass(t, c, place)
                push(t, (place,), (c,))
            pe_fill(n)

        hooks = {
            0: lambda: pe_fill(1),
            1: lambda: pe_fill(1),
            2: lambda: pe_fill(1),
            3: lambda: after((PLACE_I,), 0, 1),
            4: lambda: after((PLACE_F,), 0, 1),
            5: lambda: after((PLACE_Z,), 0, 1),
            6: lambda: pe_fill(1),
            7: lambda: after((PLACE_O,), 0, 1),
            8: lambda: (after((PLACE_I,), 1, 0), after((PLACE_O,), 1, 1)),
            9: lambda: after((PLACE_F,), 1, 1),
        }
        products(t, 0, len(LAST_ORDER), hooks)
        after((PLACE_Z,), 1, 100)
        store(t, nc.vector.tensor_copy)
